import numpy as np
import ml_dtypes


def mxq(x, axis, fmt="e4m3"):
    dtype, down = {"e4m3": (ml_dtypes.float8_e4m3fn, 7), "e5m2": (ml_dtypes.float8_e5m2, 14)}[fmt]
    v = np.moveaxis(np.asarray(x, np.float32).astype(ml_dtypes.bfloat16).astype(np.float64), axis, -1)
    blocks = v.reshape(v.shape[:-1] + (-1, 32))
    amax = np.abs(blocks).max(-1, keepdims=True)
    byte = np.maximum(np.where(amax > 0, np.frexp(amax)[1] - 1 + 127, 0) - down, 1)
    scale = np.exp2(byte - 127.0)
    codes = (blocks / scale).astype(np.float32).astype(dtype).astype(np.float64)
    return np.moveaxis((codes * scale).reshape(v.shape), -1, axis)


WIDE = False


def mx_kscale(k):
    if not WIDE:
        return np.ones(k)
    levels = np.array([10, -10, 5, -5, 0])
    a = np.random.permutation(np.resize(levels, k // 512 * 4)).reshape(k // 512, 4)
    idx = np.arange(k)
    return np.exp2(a[idx // 512, idx % 128 // 32])


BF16 = ml_dtypes.bfloat16


def bf(x):
    return np.asarray(x, np.float32).astype(BF16)


def f64(x):
    return np.asarray(x).astype(np.float64)


B, S, IN, OUT, Q, NS, R, ALPHA = 4, 512, 2048, 2048, 4, 8, 512, 1024
DO = OUT // Q
SCALING = ALPHA / R


def setup_inputs():
    t = mx_kscale(R)
    return {"h": bf(np.random.standard_normal((B, S, R)) * t),
            "weights": bf(np.random.uniform(0.0, 1.0, (B, Q, NS))),
            "lora_b": bf(np.random.standard_normal((Q, NS, R, DO)) / np.sqrt(NS * R) / t[None, None, :, None])}


def reference(h, weights, lora_b):
    w, lb = f64(weights), f64(lora_b)
    b_mix = sum(w[:, :, k, None, None] * lb[None, :, k] for k in range(NS))
    b_mix = b_mix.transpose(0, 2, 1, 3).reshape(B, R, OUT)
    return (mxq(f64(h), 2, "e4m3") @ mxq(b_mix, 1, "e4m3")) * SCALING

@@ -1,0 +1,204 @@
+from contextlib import ExitStack
+
+import concourse.mybir as mybir
+from concourse.masks import make_identity
+
+BF16 = mybir.dt.bfloat16
+F32 = mybir.dt.float32
+U32 = mybir.dt.uint32
+U8 = mybir.dt.uint8
+FP8X4 = mybir.dt.float8_e4m3fn_x4
+MULT = mybir.AluOpType.mult
+ADD = mybir.AluOpType.add
+COPY = mybir.ActivationFunctionType.Copy
+
+B, S, R, OUT, Q, NS = 4, 512, 512, 2048, 4, 8
+DO = OUT // Q
+SCALING = 2.0
+
+P = 128
+PACK = 4
+assert R == P * PACK
+TOKEN_TILES = S // P
+BANK = 512
+
+D_CHUNK = 256
+CHUNKS = DO // D_CHUNK
+TILES_PER_BANK = BANK // D_CHUNK
+PAIR = 2
+
+FLOPS = 2 * B * S * R * OUT + 2 * B * Q * NS * R * DO
+
+
+def tile_skilledlora_pb_kernel(tc, h, weights, lora_b, out):
+    nc = tc.nc
+    with ExitStack() as ctx:
+        consts = ctx.enter_context(tc.tile_pool(name="consts", bufs=1))
+        h_pool = ctx.enter_context(tc.tile_pool(name="h_rows", bufs=B))
+        h_grouped_pool = ctx.enter_context(tc.tile_pool(name="h_grouped", bufs=2))
+        skill_pool = ctx.enter_context(tc.tile_pool(name="skills", bufs=2 * NS))
+        sum_pool = ctx.enter_context(tc.tile_pool(name="sums", bufs=3 * PAIR))
+        mix_pool = ctx.enter_context(tc.tile_pool(name="mix", bufs=2 * PAIR))
+        store_pool = ctx.enter_context(tc.tile_pool(name="store", bufs=2 * PAIR))
+        psum_h = ctx.enter_context(tc.psum_pool(name="psum_h", bufs=2))
+        psum_out = ctx.enter_context(tc.psum_pool(name="psum_out", bufs=4))
+
+        w_bf16 = consts.tile([P, B * Q * NS], BF16)
+        nc.scalar.dma_start(
+            out=w_bf16[:], in_=weights.rearrange("b q k -> (b q k)").partition_broadcast(P)
+        )
+        w_f32 = consts.tile([P, B * Q * NS], F32)
+        nc.vector.tensor_copy(out=w_f32[:], in_=w_bf16[:])
+
+        identity = consts.tile([P, P], BF16)
+        make_identity(nc, identity[:])
+
+        h_codes = consts.tile([P, B, S], U32, align_bytes=64)
+        h_scales = consts.tile([P, B, S], U8, align_bytes=64)
+
+        def weight_of(b, q, k):
+            column = (b * Q + q) * NS + k
+            return w_f32[:, column : column + 1]
+
+        def load_skills(q):
+            tiles = []
+            for k in range(NS):
+                skill = skill_pool.tile([P, PACK, DO], BF16)
+                nc.sync.dma_start(
+                    out=skill[:], in_=lora_b[q, k].rearrange("(t p) d -> p t d", p=P)
+                )
+                tiles.append(skill)
+            return tiles
+
+        def load_h(b):
+            h_rows = h_pool.tile([P, TOKEN_TILES, R], BF16)
+            nc.sync.dma_start(out=h_rows[:], in_=h[b].rearrange("(n p) r -> p n r", p=P))
+            return h_rows
+
+        def quantise_h(b, h_rows):
+            h_grouped = h_grouped_pool.tile([P, S, PACK], BF16, align_bytes=64)
+            tiles_per_bank = 2
+            for first in range(0, TOKEN_TILES, tiles_per_bank):
+                turned = psum_h.tile([P, tiles_per_bank, PACK, P], BF16)
+                for n in range(tiles_per_bank):
+                    for t in range(PACK):
+                        nc.tensor.transpose(
+                            turned[:, n, t, :],
+                            h_rows[:, first + n, t * P : (t + 1) * P],
+                            identity[:],
+                        )
+                nc.scalar.copy(
+                    out=h_grouped[:, first * P : (first + tiles_per_bank) * P, :].rearrange(
+                        "p (n s) t -> p n s t", n=tiles_per_bank
+                    ),
+                    in_=turned[:].rearrange("p n t s -> p n s t"),
+                )
+            nc.vector.quantize_mx(
+                out=h_codes[:, b, :].bitcast(FP8X4),
+                scales=h_scales[:, b, :],
+                in_=h_grouped[:].rearrange("p s t -> p (s t)"),
+            )
+
+        def start_sums(step):
+            q, c, examples = step
+            sums = []
+            for b in examples:
+                total = sum_pool.tile([P, PACK, D_CHUNK], F32)
+                nc.scalar.activation(
+                    out=total[:],
+                    in_=skills[q][0][:, :, c * D_CHUNK : (c + 1) * D_CHUNK],
+                    func=COPY,
+                    scale=weight_of(b, q, 0),
+                )
+                sums.append(total)
+            return sums
+
+        def add_skill(step, sums, k):
+            q, c, examples = step
+            for b, total in zip(examples, sums):
+                nc.vector.scalar_tensor_tensor(
+                    out=total[:],
+                    in0=skills[q][k][:, :, c * D_CHUNK : (c + 1) * D_CHUNK],
+                    scalar=weight_of(b, q, k),
+                    in1=total[:],
+                    op0=MULT,
+                    op1=ADD,
+                )
+
+        def round_sums(sums):
+            rounded = []
+            for total in sums:
+                grouped = mix_pool.tile([P, D_CHUNK, PACK], BF16, align_bytes=64)
+                nc.scalar.copy(out=grouped[:], in_=total[:].rearrange("p t d -> p d t"))
+                rounded.append(grouped)
+            return rounded
+
+        def multiply_and_store(step, rounded):
+            q, c, examples = step
+            first_column = q * DO + c * D_CHUNK
+            for b, grouped in zip(examples, rounded):
+                codes = mix_pool.tile([P, D_CHUNK], U32, align_bytes=64)
+                scales = mix_pool.tile([P, D_CHUNK], U8, align_bytes=64)
+                nc.vector.quantize_mx(
+                    out=codes[:].bitcast(FP8X4),
+                    scales=scales[:],
+                    in_=grouped[:].rearrange("p d t -> p (d t)"),
+                )
+                result = store_pool.tile([P, TOKEN_TILES, D_CHUNK], F32)
+                for first in range(0, TOKEN_TILES, TILES_PER_BANK):
+                    product = psum_out.tile([P, TILES_PER_BANK, D_CHUNK], F32)
+                    for j in range(TILES_PER_BANK):
+                        tokens = slice((first + j) * P, (first + j + 1) * P)
+                        nc.tensor.matmul_mx(
+                            out=product[:, j, :],
+                            lhsT=h_codes[:, b, tokens].bitcast(FP8X4),
+                            lhsT_scale=h_scales[:, b, tokens],
+                            rhs=codes[:].bitcast(FP8X4),
+                            rhs_scale=scales[:],
+                            start=True,
+                            stop=True,
+                        )
+                    nc.scalar.activation(
+                        out=result[:, first : first + TILES_PER_BANK, :],
+                        in_=product[:],
+                        func=COPY,
+                        scale=SCALING,
+                    )
+                nc.scalar.dma_start(
+                    out=out[b, :, first_column : first_column + D_CHUNK].rearrange(
+                        "(n p) d -> p n d", p=P
+                    ),
+                    in_=result[:],
+                )
+
+        steps = [
+            (q, c, tuple(range(first, first + PAIR)))
+            for q in range(Q)
+            for c in range(CHUNKS)
+            for first in range(0, B, PAIR)
+        ]
+        steps_that_meet_new_examples = B // PAIR
+
+        MULTIPLY_AFTER_ROUND = 2
+        QUANTISE_H_AFTER_ROUND = 4
+
+        skills = {0: load_skills(0)}
+        h_rows_of = [load_h(b) for b in range(B)]
+        sums_of = {0: start_sums(steps[0])}
+        rounded_of = {}
+
+        for s, step in enumerate(steps):
+            q, c, examples = step
+            if c == 0 and examples[0] == 0 and q + 1 < Q:
+                skills[q + 1] = load_skills(q + 1)
+            if s + 1 < len(steps):
+                sums_of[s + 1] = start_sums(steps[s + 1])
+            for k in range(1, NS):
+                add_skill(step, sums_of[s], k)
+                if k == MULTIPLY_AFTER_ROUND and s > 0:
+                    multiply_and_store(steps[s - 1], rounded_of[s - 1])
+                if k == QUANTISE_H_AFTER_ROUND and s < steps_that_meet_new_examples:
+                    for b in examples:
+                        quantise_h(b, h_rows_of[b])
+            rounded_of[s] = round_sums(sums_of[s])
+        multiply_and_store(steps[-1], rounded_of[len(steps) - 1])

@@ -26,6 +26,15 @@ D_CHUNK = 256
 CHUNKS = DO // D_CHUNK
 TILES_PER_BANK = BANK // D_CHUNK
 PAIR = 2
+STEPS_PER_SPLIT = CHUNKS * (B // PAIR)
+
+SKILL_GROUP = 4
+SKILL_GROUPS = NS // SKILL_GROUP
+RANK_BLOCK = P // SKILL_GROUP
+RANK_BLOCKS = P // RANK_BLOCK
+FEATURE_BLOCKS = DO // P
+VECTOR_ONLY_SPLITS = 1
+assert (Q - VECTOR_ONLY_SPLITS) * RANK_BLOCKS * FEATURE_BLOCKS * SKILL_GROUPS * P * P * P * 10 < B * S * R * OUT
 
 FLOPS = 2 * B * S * R * OUT + 2 * B * Q * NS * R * DO
 
@@ -40,7 +49,10 @@ def tile_skilledlora_pb_kernel(tc, h, weights, lora_b, out):
         sum_pool = ctx.enter_context(tc.tile_pool(name="sums", bufs=3 * PAIR))
         mix_pool = ctx.enter_context(tc.tile_pool(name="mix", bufs=2 * PAIR))
         store_pool = ctx.enter_context(tc.tile_pool(name="store", bufs=2 * PAIR))
-        psum_h = ctx.enter_context(tc.psum_pool(name="psum_h", bufs=2))
+        stacked_pool = ctx.enter_context(tc.tile_pool(name="stacked", bufs=2))
+        mixed_pool = ctx.enter_context(tc.tile_pool(name="mixed", bufs=2))
+        psum_turn = ctx.enter_context(tc.psum_pool(name="psum_turn", bufs=2))
+        psum_mix = ctx.enter_context(tc.psum_pool(name="psum_mix", bufs=2))
         psum_out = ctx.enter_context(tc.psum_pool(name="psum_out", bufs=4))
 
         w_bf16 = consts.tile([P, B * Q * NS], BF16)
@@ -53,6 +65,29 @@ def tile_skilledlora_pb_kernel(tc, h, weights, lora_b, out):
         identity = consts.tile([P, P], BF16)
         make_identity(nc, identity[:])
 
+        diagonal = consts.tile([P, RANK_BLOCK], F32)
+        nc.vector.tensor_reduce(
+            out=diagonal[:],
+            in_=identity[:].rearrange("p (g r) -> p r g", g=SKILL_GROUP),
+            axis=mybir.AxisListType.X,
+            op=ADD,
+        )
+        own_weight = consts.tile([P, Q, SKILL_GROUPS, B], F32)
+        w_by_skill = w_f32[:].rearrange("p (b q i g) -> p q i b g", b=B, q=Q, i=SKILL_GROUPS)
+        for g in range(SKILL_GROUP):
+            rows = slice(g * RANK_BLOCK, (g + 1) * RANK_BLOCK)
+            nc.vector.tensor_copy(out=own_weight[rows], in_=w_by_skill[rows, :, :, :, g])
+        mixers = consts.tile([P, Q * SKILL_GROUPS * B, RANK_BLOCK], BF16)
+        nc.vector.tensor_tensor(
+            out=mixers[:],
+            in0=diagonal[:].unsqueeze(1).to_broadcast([P, Q * SKILL_GROUPS * B, RANK_BLOCK]),
+            in1=own_weight[:]
+            .rearrange("p q i b -> p (q i b)")
+            .unsqueeze(2)
+            .to_broadcast([P, Q * SKILL_GROUPS * B, RANK_BLOCK]),
+            op=MULT,
+        )
+
         h_codes = consts.tile([P, B, S], U32, align_bytes=64)
         h_scales = consts.tile([P, B, S], U8, align_bytes=64)
 
@@ -60,15 +95,52 @@ def tile_skilledlora_pb_kernel(tc, h, weights, lora_b, out):
             column = (b * Q + q) * NS + k
             return w_f32[:, column : column + 1]
 
+        def planes_on_vector(q):
+            return PACK if q < VECTOR_ONLY_SPLITS else PACK - 1
+
         def load_skills(q):
+            planes = planes_on_vector(q)
             tiles = []
             for k in range(NS):
-                skill = skill_pool.tile([P, PACK, DO], BF16)
+                skill = skill_pool.tile([P, planes, DO], BF16)
                 nc.sync.dma_start(
-                    out=skill[:], in_=lora_b[q, k].rearrange("(t p) d -> p t d", p=P)
+                    out=skill[:],
+                    in_=lora_b[q, k, 0 : planes * P, :].rearrange("(t p) d -> p t d", p=P),
                 )
                 tiles.append(skill)
             return tiles
+
+        def load_last_plane(q):
+            stacked = stacked_pool.tile([P, SKILL_GROUPS, RANK_BLOCKS, DO], BF16)
+            for k in range(NS):
+                i, g = divmod(k, SKILL_GROUP)
+                nc.sync.dma_start(
+                    out=stacked[g * RANK_BLOCK : (g + 1) * RANK_BLOCK, i, :, :],
+                    in_=lora_b[q, k, (PACK - 1) * P : R, :].rearrange(
+                        "(block r) d -> r block d", r=RANK_BLOCK
+                    ),
+                )
+            return stacked
+
+        def mix_last_plane(q, stacked):
+            mixed = mixed_pool.tile([P, FEATURE_BLOCKS, B, P], BF16)
+            for f in range(FEATURE_BLOCKS):
+                bank = psum_mix.tile([P, RANK_BLOCKS, B, RANK_BLOCK], F32)
+                for block in range(RANK_BLOCKS):
+                    for i in range(SKILL_GROUPS):
+                        first = (q * SKILL_GROUPS + i) * B
+                        nc.tensor.matmul(
+                            out=bank[:, block, :, :].rearrange("p b r -> p (b r)"),
+                            lhsT=stacked[:, i, block, f * P : (f + 1) * P],
+                            rhs=mixers[:, first : first + B, :].rearrange("p b r -> p (b r)"),
+                            start=(i == 0),
+                            stop=(i == SKILL_GROUPS - 1),
+                        )
+                nc.scalar.copy(
+                    out=mixed[:, f, :, :].rearrange("p b (block r) -> p b block r", r=RANK_BLOCK),
+                    in_=bank[:].rearrange("p block b r -> p b block r"),
+                )
+            return mixed
 
         def load_h(b):
             h_rows = h_pool.tile([P, TOKEN_TILES, R], BF16)
@@ -79,7 +151,7 @@ def tile_skilledlora_pb_kernel(tc, h, weights, lora_b, out):
             h_grouped = h_grouped_pool.tile([P, S, PACK], BF16, align_bytes=64)
             tiles_per_bank = 2
             for first in range(0, TOKEN_TILES, tiles_per_bank):
-                turned = psum_h.tile([P, tiles_per_bank, PACK, P], BF16)
+                turned = psum_turn.tile([P, tiles_per_bank, PACK, P], BF16, tag="turned")
                 for n in range(tiles_per_bank):
                     for t in range(PACK):
                         nc.tensor.transpose(
@@ -101,26 +173,40 @@ def tile_skilledlora_pb_kernel(tc, h, weights, lora_b, out):
 
         def start_sums(step):
             q, c, examples = step
+            planes = planes_on_vector(q)
             sums = []
             for b in examples:
                 total = sum_pool.tile([P, PACK, D_CHUNK], F32)
                 nc.scalar.activation(
-                    out=total[:],
+                    out=total[:, 0:planes, :],
                     in_=skills[q][0][:, :, c * D_CHUNK : (c + 1) * D_CHUNK],
                     func=COPY,
                     scale=weight_of(b, q, 0),
                 )
                 sums.append(total)
+            if planes < PACK:
+                blocks = D_CHUNK // P
+                back = psum_turn.tile([P, PAIR, D_CHUNK], BF16, tag="turned")
+                for e, b in enumerate(examples):
+                    for j in range(blocks):
+                        nc.tensor.transpose(
+                            back[:, e, j * P : (j + 1) * P],
+                            mixed_of[q][:, c * blocks + j, b, :],
+                            identity[:],
+                        )
+                for e, total in enumerate(sums):
+                    nc.scalar.copy(out=total[:, PACK - 1, :], in_=back[:, e, :])
             return sums
 
         def add_skill(step, sums, k):
             q, c, examples = step
+            planes = planes_on_vector(q)
             for b, total in zip(examples, sums):
                 nc.vector.scalar_tensor_tensor(
-                    out=total[:],
+                    out=total[:, 0:planes, :],
                     in0=skills[q][k][:, :, c * D_CHUNK : (c + 1) * D_CHUNK],
                     scalar=weight_of(b, q, k),
-                    in1=total[:],
+                    in1=total[:, 0:planes, :],
                     op0=MULT,
                     op1=ADD,
                 )
@@ -186,13 +272,19 @@ def tile_skilledlora_pb_kernel(tc, h, weights, lora_b, out):
         h_rows_of = [load_h(b) for b in range(B)]
         sums_of = {0: start_sums(steps[0])}
         rounded_of = {}
+        stacked_of = {}
+        mixed_of = {}
 
         for s, step in enumerate(steps):
             q, c, examples = step
-            if c == 0 and examples[0] == 0 and q + 1 < Q:
+            step_in_split = s % STEPS_PER_SPLIT
+            if step_in_split == 0 and q + 1 < Q:
+                stacked_of[q + 1] = load_last_plane(q + 1)
                 skills[q + 1] = load_skills(q + 1)
             if s + 1 < len(steps):
                 sums_of[s + 1] = start_sums(steps[s + 1])
+            if step_in_split == STEPS_PER_SPLIT - 2 and q + 1 < Q:
+                mixed_of[q + 1] = mix_last_plane(q + 1, stacked_of[q + 1])
             for k in range(1, NS):
                 add_skill(step, sums_of[s], k)
                 if k == MULTIPLY_AFTER_ROUND and s > 0:

@@ -11,6 +11,7 @@ FP8X4 = mybir.dt.float8_e4m3fn_x4
 MULT = mybir.AluOpType.mult
 ADD = mybir.AluOpType.add
 COPY = mybir.ActivationFunctionType.Copy
+ALONG_ROW = mybir.AxisListType.X
 
 B, S, R, OUT, Q, NS = 4, 512, 512, 2048, 4, 8
 DO = OUT // Q
@@ -28,13 +29,15 @@ TILES_PER_BANK = BANK // D_CHUNK
 PAIR = 2
 STEPS_PER_SPLIT = CHUNKS * (B // PAIR)
 
-SKILL_GROUP = 4
-SKILL_GROUPS = NS // SKILL_GROUP
-RANK_BLOCK = P // SKILL_GROUP
-RANK_BLOCKS = P // RANK_BLOCK
+RANKS_PER_MATMUL = P // NS
+RANK_STRIDE = R // RANKS_PER_MATMUL
+WORDS_PER_STRIDE = RANK_STRIDE // PACK
 FEATURE_BLOCKS = DO // P
+TENSOR_PLANES = 2
 VECTOR_ONLY_SPLITS = 1
-assert (Q - VECTOR_ONLY_SPLITS) * RANK_BLOCKS * FEATURE_BLOCKS * SKILL_GROUPS * P * P * P * 10 < B * S * R * OUT
+MIXING_MATMULS = (Q - VECTOR_ONLY_SPLITS) * TENSOR_PLANES * WORDS_PER_STRIDE * FEATURE_BLOCKS
+assert MIXING_MATMULS * P * P * B * RANKS_PER_MATMUL * 10 < B * S * R * OUT
+assert Q <= STEPS_PER_SPLIT
 
 FLOPS = 2 * B * S * R * OUT + 2 * B * Q * NS * R * DO
 
@@ -49,8 +52,7 @@ def tile_skilledlora_pb_kernel(tc, h, weights, lora_b, out):
         sum_pool = ctx.enter_context(tc.tile_pool(name="sums", bufs=3 * PAIR))
         mix_pool = ctx.enter_context(tc.tile_pool(name="mix", bufs=2 * PAIR))
         store_pool = ctx.enter_context(tc.tile_pool(name="store", bufs=2 * PAIR))
-        stacked_pool = ctx.enter_context(tc.tile_pool(name="stacked", bufs=2))
-        mixed_pool = ctx.enter_context(tc.tile_pool(name="mixed", bufs=2))
+        tensor_pool = ctx.enter_context(tc.tile_pool(name="tensor", bufs=Q - VECTOR_ONLY_SPLITS))
         psum_turn = ctx.enter_context(tc.psum_pool(name="psum_turn", bufs=2))
         psum_mix = ctx.enter_context(tc.psum_pool(name="psum_mix", bufs=2))
         psum_out = ctx.enter_context(tc.psum_pool(name="psum_out", bufs=4))
@@ -64,27 +66,40 @@ def tile_skilledlora_pb_kernel(tc, h, weights, lora_b, out):
 
         identity = consts.tile([P, P], BF16)
         make_identity(nc, identity[:])
+        identity_f32 = consts.tile([P, P], F32)
+        make_identity(nc, identity_f32[:])
 
-        diagonal = consts.tile([P, RANK_BLOCK], F32)
+        is_skill = consts.tile([P, NS], F32)
         nc.vector.tensor_reduce(
-            out=diagonal[:],
-            in_=identity[:].rearrange("p (g r) -> p r g", g=SKILL_GROUP),
-            axis=mybir.AxisListType.X,
+            out=is_skill[:],
+            in_=identity_f32[:].rearrange("p (k g) -> p k g", k=NS),
+            axis=ALONG_ROW,
             op=ADD,
         )
-        own_weight = consts.tile([P, Q, SKILL_GROUPS, B], F32)
-        w_by_skill = w_f32[:].rearrange("p (b q i g) -> p q i b g", b=B, q=Q, i=SKILL_GROUPS)
-        for g in range(SKILL_GROUP):
-            rows = slice(g * RANK_BLOCK, (g + 1) * RANK_BLOCK)
-            nc.vector.tensor_copy(out=own_weight[rows], in_=w_by_skill[rows, :, :, :, g])
-        mixers = consts.tile([P, Q * SKILL_GROUPS * B, RANK_BLOCK], BF16)
+        is_rank = consts.tile([P, RANKS_PER_MATMUL], F32)
+        nc.vector.tensor_reduce(
+            out=is_rank[:],
+            in_=identity_f32[:].rearrange("p (k g) -> p g k", k=NS),
+            axis=ALONG_ROW,
+            op=ADD,
+        )
+        masked = consts.tile([P, B * Q, NS], F32)
+        nc.vector.tensor_tensor(
+            out=masked[:],
+            in0=w_f32[:].rearrange("p (x k) -> p x k", k=NS),
+            in1=is_skill[:].unsqueeze(1).to_broadcast([P, B * Q, NS]),
+            op=MULT,
+        )
+        own_weight = consts.tile([P, B * Q], F32)
+        nc.vector.tensor_reduce(out=own_weight[:], in_=masked[:], axis=ALONG_ROW, op=ADD)
+        mixers = consts.tile([P, Q, B, RANKS_PER_MATMUL], BF16)
         nc.vector.tensor_tensor(
             out=mixers[:],
-            in0=diagonal[:].unsqueeze(1).to_broadcast([P, Q * SKILL_GROUPS * B, RANK_BLOCK]),
+            in0=is_rank[:].unsqueeze(1).unsqueeze(1).to_broadcast([P, Q, B, RANKS_PER_MATMUL]),
             in1=own_weight[:]
-            .rearrange("p q i b -> p (q i b)")
-            .unsqueeze(2)
-            .to_broadcast([P, Q * SKILL_GROUPS * B, RANK_BLOCK]),
+            .rearrange("p (b q) -> p q b", b=B)
+            .unsqueeze(3)
+            .to_broadcast([P, Q, B, RANKS_PER_MATMUL]),
             op=MULT,
         )
 
@@ -96,7 +111,7 @@ def tile_skilledlora_pb_kernel(tc, h, weights, lora_b, out):
             return w_f32[:, column : column + 1]
 
         def planes_on_vector(q):
-            return PACK if q < VECTOR_ONLY_SPLITS else PACK - 1
+            return PACK if q < VECTOR_ONLY_SPLITS else PACK - TENSOR_PLANES
 
         def load_skills(q):
             planes = planes_on_vector(q)
@@ -105,41 +120,40 @@ def tile_skilledlora_pb_kernel(tc, h, weights, lora_b, out):
                 skill = skill_pool.tile([P, planes, DO], BF16)
                 nc.sync.dma_start(
                     out=skill[:],
-                    in_=lora_b[q, k, 0 : planes * P, :].rearrange("(t p) d -> p t d", p=P),
+                    in_=lora_b[q, k].rearrange("(p t) d -> p t d", t=PACK)[:, 0:planes, :],
                 )
                 tiles.append(skill)
             return tiles
 
-        def load_last_plane(q):
-            stacked = stacked_pool.tile([P, SKILL_GROUPS, RANK_BLOCKS, DO], BF16)
-            for k in range(NS):
-                i, g = divmod(k, SKILL_GROUP)
-                nc.sync.dma_start(
-                    out=stacked[g * RANK_BLOCK : (g + 1) * RANK_BLOCK, i, :, :],
-                    in_=lora_b[q, k, (PACK - 1) * P : R, :].rearrange(
-                        "(block r) d -> r block d", r=RANK_BLOCK
-                    ),
-                )
+        def load_stacked(q):
+            stacked = tensor_pool.tile([P, WORDS_PER_STRIDE, TENSOR_PLANES, DO], BF16)
+            nc.sync.dma_start(
+                out=stacked[:],
+                in_=lora_b[q].rearrange(
+                    "k (g a t) d -> (k g) a t d", a=WORDS_PER_STRIDE, t=PACK
+                )[:, :, PACK - TENSOR_PLANES : PACK, :],
+            )
             return stacked
 
-        def mix_last_plane(q, stacked):
-            mixed = mixed_pool.tile([P, FEATURE_BLOCKS, B, P], BF16)
+        def mix_on_tensor(q, stacked):
+            mixed = tensor_pool.tile([P, FEATURE_BLOCKS, TENSOR_PLANES, B, P], BF16)
             for f in range(FEATURE_BLOCKS):
-                bank = psum_mix.tile([P, RANK_BLOCKS, B, RANK_BLOCK], F32)
-                for block in range(RANK_BLOCKS):
-                    for i in range(SKILL_GROUPS):
-                        first = (q * SKILL_GROUPS + i) * B
+                for t in range(TENSOR_PLANES):
+                    bank = psum_mix.tile([P, WORDS_PER_STRIDE, B, RANKS_PER_MATMUL], F32)
+                    for a in range(WORDS_PER_STRIDE):
                         nc.tensor.matmul(
-                            out=bank[:, block, :, :].rearrange("p b r -> p (b r)"),
-                            lhsT=stacked[:, i, block, f * P : (f + 1) * P],
-                            rhs=mixers[:, first : first + B, :].rearrange("p b r -> p (b r)"),
-                            start=(i == 0),
-                            stop=(i == SKILL_GROUPS - 1),
+                            out=bank[:, a, :, :].rearrange("p b g -> p (b g)"),
+                            lhsT=stacked[:, a, t, f * P : (f + 1) * P],
+                            rhs=mixers[:, q, :, :].rearrange("p b g -> p (b g)"),
+                            start=True,
+                            stop=True,
                         )
-                nc.scalar.copy(
-                    out=mixed[:, f, :, :].rearrange("p b (block r) -> p b block r", r=RANK_BLOCK),
-                    in_=bank[:].rearrange("p block b r -> p b block r"),
-                )
+                    nc.scalar.copy(
+                        out=mixed[:, f, t, :, :].rearrange(
+                            "p b (g a) -> p b g a", a=WORDS_PER_STRIDE
+                        ),
+                        in_=bank[:].rearrange("p a b g -> p b g a"),
+                    )
             return mixed
 
         def load_h(b):
@@ -148,27 +162,26 @@ def tile_skilledlora_pb_kernel(tc, h, weights, lora_b, out):
             return h_rows
 
         def quantise_h(b, h_rows):
-            h_grouped = h_grouped_pool.tile([P, S, PACK], BF16, align_bytes=64)
-            tiles_per_bank = 2
+            halves = PACK // 2
+            h_grouped = h_grouped_pool.tile([P, S * PACK], BF16, align_bytes=64)
+            grouped_words = h_grouped[:].bitcast(F32).rearrange("p (s u) -> p s u", u=halves)
+            tiles_per_bank = BANK // (halves * P)
             for first in range(0, TOKEN_TILES, tiles_per_bank):
-                turned = psum_turn.tile([P, tiles_per_bank, PACK, P], BF16, tag="turned")
+                turned = psum_turn.tile([P, tiles_per_bank, halves, P], F32, tag="turned")
                 for n in range(tiles_per_bank):
-                    for t in range(PACK):
-                        nc.tensor.transpose(
-                            turned[:, n, t, :],
-                            h_rows[:, first + n, t * P : (t + 1) * P],
-                            identity[:],
-                        )
+                    words = h_rows[:, first + n, :].bitcast(F32).rearrange(
+                        "p (w u) -> p u w", u=halves
+                    )
+                    for u in range(halves):
+                        nc.tensor.transpose(turned[:, n, u, :], words[:, u, :], identity_f32[:])
                 nc.scalar.copy(
-                    out=h_grouped[:, first * P : (first + tiles_per_bank) * P, :].rearrange(
-                        "p (n s) t -> p n s t", n=tiles_per_bank
+                    out=grouped_words[:, first * P : (first + tiles_per_bank) * P, :].rearrange(
+                        "p (n s) u -> p n s u", n=tiles_per_bank
                     ),
-                    in_=turned[:].rearrange("p n t s -> p n s t"),
+                    in_=turned[:].rearrange("p n u s -> p n s u"),
                 )
             nc.vector.quantize_mx(
-                out=h_codes[:, b, :].bitcast(FP8X4),
-                scales=h_scales[:, b, :],
-                in_=h_grouped[:].rearrange("p s t -> p (s t)"),
+                out=h_codes[:, b, :].bitcast(FP8X4), scales=h_scales[:, b, :], in_=h_grouped[:]
             )
 
         def start_sums(step):
@@ -186,16 +199,16 @@ def tile_skilledlora_pb_kernel(tc, h, weights, lora_b, out):
                 sums.append(total)
             if planes < PACK:
                 blocks = D_CHUNK // P
-                back = psum_turn.tile([P, PAIR, D_CHUNK], BF16, tag="turned")
-                for e, b in enumerate(examples):
-                    for j in range(blocks):
-                        nc.tensor.transpose(
-                            back[:, e, j * P : (j + 1) * P],
-                            mixed_of[q][:, c * blocks + j, b, :],
-                            identity[:],
-                        )
-                for e, total in enumerate(sums):
-                    nc.scalar.copy(out=total[:, PACK - 1, :], in_=back[:, e, :])
+                for b, total in zip(examples, sums):
+                    back = psum_turn.tile([P, TENSOR_PLANES, D_CHUNK], BF16, tag="turned")
+                    for t in range(TENSOR_PLANES):
+                        for j in range(blocks):
+                            nc.tensor.transpose(
+                                back[:, t, j * P : (j + 1) * P],
+                                mixed_of[q][:, c * blocks + j, t, b, :],
+                                identity[:],
+                            )
+                    nc.scalar.copy(out=total[:, planes:PACK, :], in_=back[:])
             return sums
 
         def add_skill(step, sums, k):
@@ -250,7 +263,7 @@ def tile_skilledlora_pb_kernel(tc, h, weights, lora_b, out):
                         func=COPY,
                         scale=SCALING,
                     )
-                nc.scalar.dma_start(
+                nc.sync.dma_start(
                     out=out[b, :, first_column : first_column + D_CHUNK].rearrange(
                         "(n p) d -> p n d", p=P
                     ),
@@ -265,26 +278,26 @@ def tile_skilledlora_pb_kernel(tc, h, weights, lora_b, out):
         ]
         steps_that_meet_new_examples = B // PAIR
 
-        MULTIPLY_AFTER_ROUND = 2
+        MULTIPLY_AFTER_ROUND = 3
         QUANTISE_H_AFTER_ROUND = 4
 
         skills = {0: load_skills(0)}
         h_rows_of = [load_h(b) for b in range(B)]
+        stacked_of = {}
+        for q in range(VECTOR_ONLY_SPLITS, Q):
+            stacked_of[q] = load_stacked(q)
+        mixed_of = {}
         sums_of = {0: start_sums(steps[0])}
         rounded_of = {}
-        stacked_of = {}
-        mixed_of = {}
 
         for s, step in enumerate(steps):
             q, c, examples = step
-            step_in_split = s % STEPS_PER_SPLIT
-            if step_in_split == 0 and q + 1 < Q:
-                stacked_of[q + 1] = load_last_plane(q + 1)
+            if s % STEPS_PER_SPLIT == 0 and q + 1 < Q:
                 skills[q + 1] = load_skills(q + 1)
             if s + 1 < len(steps):
                 sums_of[s + 1] = start_sums(steps[s + 1])
-            if step_in_split == STEPS_PER_SPLIT - 2 and q + 1 < Q:
-                mixed_of[q + 1] = mix_last_plane(q + 1, stacked_of[q + 1])
+            if VECTOR_ONLY_SPLITS <= s < Q:
+                mixed_of[s] = mix_on_tensor(s, stacked_of[s])
             for k in range(1, NS):
                 add_skill(step, sums_of[s], k)
                 if k == MULTIPLY_AFTER_ROUND and s > 0:

@@ -35,7 +35,8 @@ WORDS_PER_STRIDE = RANK_STRIDE // PACK
 FEATURE_BLOCKS = DO // P
 TENSOR_PLANES = 2
 VECTOR_ONLY_SPLITS = 1
-MIXING_MATMULS = (Q - VECTOR_ONLY_SPLITS) * TENSOR_PLANES * WORDS_PER_STRIDE * FEATURE_BLOCKS
+TENSOR_SPLITS = Q - VECTOR_ONLY_SPLITS
+MIXING_MATMULS = TENSOR_SPLITS * TENSOR_PLANES * WORDS_PER_STRIDE * FEATURE_BLOCKS
 assert MIXING_MATMULS * P * P * B * RANKS_PER_MATMUL * 10 < B * S * R * OUT
 assert Q <= STEPS_PER_SPLIT
 
@@ -49,13 +50,15 @@ def tile_skilledlora_pb_kernel(tc, h, weights, lora_b, out):
         h_pool = ctx.enter_context(tc.tile_pool(name="h_rows", bufs=B))
         h_grouped_pool = ctx.enter_context(tc.tile_pool(name="h_grouped", bufs=2))
         skill_pool = ctx.enter_context(tc.tile_pool(name="skills", bufs=2 * NS))
-        sum_pool = ctx.enter_context(tc.tile_pool(name="sums", bufs=3 * PAIR))
+        sum_pool = ctx.enter_context(tc.tile_pool(name="sums", bufs=2 * PAIR))
+        rounded_pool = ctx.enter_context(tc.tile_pool(name="rounded", bufs=3 * PAIR))
         mix_pool = ctx.enter_context(tc.tile_pool(name="mix", bufs=2 * PAIR))
         store_pool = ctx.enter_context(tc.tile_pool(name="store", bufs=2 * PAIR))
-        tensor_pool = ctx.enter_context(tc.tile_pool(name="tensor", bufs=Q - VECTOR_ONLY_SPLITS))
+        tensor_pool = ctx.enter_context(tc.tile_pool(name="tensor", bufs=TENSOR_SPLITS))
         psum_turn = ctx.enter_context(tc.psum_pool(name="psum_turn", bufs=2))
         psum_mix = ctx.enter_context(tc.psum_pool(name="psum_mix", bufs=2))
         psum_out = ctx.enter_context(tc.psum_pool(name="psum_out", bufs=4))
+        ctx.enter_context(tc.manual_schedule())
 
         w_bf16 = consts.tile([P, B * Q * NS], BF16)
         nc.scalar.dma_start(
@@ -83,23 +86,26 @@ def tile_skilledlora_pb_kernel(tc, h, weights, lora_b, out):
             axis=ALONG_ROW,
             op=ADD,
         )
-        masked = consts.tile([P, B * Q, NS], F32)
+        masked = consts.tile([P, B, TENSOR_SPLITS, NS], F32)
         nc.vector.tensor_tensor(
             out=masked[:],
-            in0=w_f32[:].rearrange("p (x k) -> p x k", k=NS),
-            in1=is_skill[:].unsqueeze(1).to_broadcast([P, B * Q, NS]),
+            in0=w_f32[:].rearrange("p (b q k) -> p b q k", b=B, q=Q)[:, :, VECTOR_ONLY_SPLITS:Q, :],
+            in1=is_skill[:].unsqueeze(1).unsqueeze(1).to_broadcast([P, B, TENSOR_SPLITS, NS]),
             op=MULT,
         )
-        own_weight = consts.tile([P, B * Q], F32)
+        own_weight = consts.tile([P, B, TENSOR_SPLITS], F32)
         nc.vector.tensor_reduce(out=own_weight[:], in_=masked[:], axis=ALONG_ROW, op=ADD)
-        mixers = consts.tile([P, Q, B, RANKS_PER_MATMUL], BF16)
+        mixers = consts.tile([P, TENSOR_SPLITS, B, RANKS_PER_MATMUL], BF16)
         nc.vector.tensor_tensor(
             out=mixers[:],
-            in0=is_rank[:].unsqueeze(1).unsqueeze(1).to_broadcast([P, Q, B, RANKS_PER_MATMUL]),
+            in0=is_rank[:]
+            .unsqueeze(1)
+            .unsqueeze(1)
+            .to_broadcast([P, TENSOR_SPLITS, B, RANKS_PER_MATMUL]),
             in1=own_weight[:]
-            .rearrange("p (b q) -> p q b", b=B)
+            .rearrange("p b q -> p q b")
             .unsqueeze(3)
-            .to_broadcast([P, Q, B, RANKS_PER_MATMUL]),
+            .to_broadcast([P, TENSOR_SPLITS, B, RANKS_PER_MATMUL]),
             op=MULT,
         )
 
@@ -144,7 +150,7 @@ def tile_skilledlora_pb_kernel(tc, h, weights, lora_b, out):
                         nc.tensor.matmul(
                             out=bank[:, a, :, :].rearrange("p b g -> p (b g)"),
                             lhsT=stacked[:, a, t, f * P : (f + 1) * P],
-                            rhs=mixers[:, q, :, :].rearrange("p b g -> p (b g)"),
+                            rhs=mixers[:, q - VECTOR_ONLY_SPLITS, :, :].rearrange("p b g -> p (b g)"),
                             start=True,
                             stop=True,
                         )
@@ -189,17 +195,18 @@ def tile_skilledlora_pb_kernel(tc, h, weights, lora_b, out):
             planes = planes_on_vector(q)
             sums = []
             for b in examples:
-                total = sum_pool.tile([P, PACK, D_CHUNK], F32)
+                total = sum_pool.tile([P, planes, D_CHUNK], F32)
+                rounded = rounded_pool.tile([P, PACK, D_CHUNK], BF16)
                 nc.scalar.activation(
-                    out=total[:, 0:planes, :],
+                    out=total[:],
                     in_=skills[q][0][:, :, c * D_CHUNK : (c + 1) * D_CHUNK],
                     func=COPY,
                     scale=weight_of(b, q, 0),
                 )
-                sums.append(total)
+                sums.append((total, rounded))
             if planes < PACK:
                 blocks = D_CHUNK // P
-                for b, total in zip(examples, sums):
+                for b, (total, rounded) in zip(examples, sums):
                     back = psum_turn.tile([P, TENSOR_PLANES, D_CHUNK], BF16, tag="turned")
                     for t in range(TENSOR_PLANES):
                         for j in range(blocks):
@@ -208,34 +215,34 @@ def tile_skilledlora_pb_kernel(tc, h, weights, lora_b, out):
                                 mixed_of[q][:, c * blocks + j, t, b, :],
                                 identity[:],
                             )
-                    nc.scalar.copy(out=total[:, planes:PACK, :], in_=back[:])
+                    nc.scalar.copy(out=rounded[:, planes:PACK, :], in_=back[:])
             return sums
 
         def add_skill(step, sums, k):
             q, c, examples = step
             planes = planes_on_vector(q)
-            for b, total in zip(examples, sums):
+            for b, (total, rounded) in zip(examples, sums):
                 nc.vector.scalar_tensor_tensor(
-                    out=total[:, 0:planes, :],
+                    out=rounded[:, 0:planes, :] if k == NS - 1 else total[:],
                     in0=skills[q][k][:, :, c * D_CHUNK : (c + 1) * D_CHUNK],
                     scalar=weight_of(b, q, k),
-                    in1=total[:, 0:planes, :],
+                    in1=total[:],
                     op0=MULT,
                     op1=ADD,
                 )
 
-        def round_sums(sums):
-            rounded = []
-            for total in sums:
+        def group_words(sums):
+            grouped_tiles = []
+            for total, rounded in sums:
                 grouped = mix_pool.tile([P, D_CHUNK, PACK], BF16, align_bytes=64)
-                nc.scalar.copy(out=grouped[:], in_=total[:].rearrange("p t d -> p d t"))
-                rounded.append(grouped)
-            return rounded
+                nc.scalar.copy(out=grouped[:], in_=rounded[:].rearrange("p t d -> p d t"))
+                grouped_tiles.append(grouped)
+            return grouped_tiles
 
-        def multiply_and_store(step, rounded):
+        def multiply_and_store(step, grouped_tiles):
             q, c, examples = step
             first_column = q * DO + c * D_CHUNK
-            for b, grouped in zip(examples, rounded):
+            for b, grouped in zip(examples, grouped_tiles):
                 codes = mix_pool.tile([P, D_CHUNK], U32, align_bytes=64)
                 scales = mix_pool.tile([P, D_CHUNK], U8, align_bytes=64)
                 nc.vector.quantize_mx(
@@ -288,7 +295,7 @@ def tile_skilledlora_pb_kernel(tc, h, weights, lora_b, out):
             stacked_of[q] = load_stacked(q)
         mixed_of = {}
         sums_of = {0: start_sums(steps[0])}
-        rounded_of = {}
+        grouped_of = {}
 
         for s, step in enumerate(steps):
             q, c, examples = step
@@ -301,9 +308,9 @@ def tile_skilledlora_pb_kernel(tc, h, weights, lora_b, out):
             for k in range(1, NS):
                 add_skill(step, sums_of[s], k)
                 if k == MULTIPLY_AFTER_ROUND and s > 0:
-                    multiply_and_store(steps[s - 1], rounded_of[s - 1])
+                    multiply_and_store(steps[s - 1], grouped_of[s - 1])
                 if k == QUANTISE_H_AFTER_ROUND and s < steps_that_meet_new_examples:
                     for b in examples:
                         quantise_h(b, h_rows_of[b])
-            rounded_of[s] = round_sums(sums_of[s])
-        multiply_and_store(steps[-1], rounded_of[len(steps) - 1])
+            grouped_of[s] = group_words(sums_of[s])
+        multiply_and_store(steps[-1], grouped_of[len(steps) - 1])

@@ -286,7 +286,7 @@ def tile_skilledlora_pb_kernel(tc, h, weights, lora_b, out):
         steps_that_meet_new_examples = B // PAIR
 
         MULTIPLY_AFTER_ROUND = 3
-        QUANTISE_H_AFTER_ROUND = 4
+        QUANTISE_H_AFTER_ROUND = NS - 1
 
         skills = {0: load_skills(0)}
         h_rows_of = [load_h(b) for b in range(B)]

@@ -19,26 +19,36 @@ SCALING = 2.0
 
 P = 128
 PACK = 4
+HALVES = PACK // 2
 assert R == P * PACK
 TOKEN_TILES = S // P
 BANK = 512
 
-D_CHUNK = 256
-CHUNKS = DO // D_CHUNK
-TILES_PER_BANK = BANK // D_CHUNK
-PAIR = 2
-STEPS_PER_SPLIT = CHUNKS * (B // PAIR)
+GROUP = 256
+BLOCKS = GROUP // P
+GROUPS_PER_SPLIT = DO // GROUP
+TILES_PER_BANK = BANK // GROUP
 
 RANKS_PER_MATMUL = P // NS
-RANK_STRIDE = R // RANKS_PER_MATMUL
-WORDS_PER_STRIDE = RANK_STRIDE // PACK
-FEATURE_BLOCKS = DO // P
-TENSOR_PLANES = 2
-VECTOR_ONLY_SPLITS = 1
-TENSOR_SPLITS = Q - VECTOR_ONLY_SPLITS
-MIXING_MATMULS = TENSOR_SPLITS * TENSOR_PLANES * WORDS_PER_STRIDE * FEATURE_BLOCKS
+WORDS_PER_STRIDE = R // RANKS_PER_MATMUL // PACK
+MATMULS_PER_BANK = BANK // (B * RANKS_PER_MATMUL)
+
+MATMUL_GROUPS = ((2, 1), (3, 0), (3, 1))
+FIRST_MATMUL_SPLIT = 2
+MATMUL_SPLITS = Q - FIRST_MATMUL_SPLIT
+MIXING_MATMULS = len(MATMUL_GROUPS) * BLOCKS * PACK * WORDS_PER_STRIDE
 assert MIXING_MATMULS * P * P * B * RANKS_PER_MATMUL * 10 < B * S * R * OUT
-assert Q <= STEPS_PER_SPLIT
+
+ROLES = "SVVVVAAA"
+SCALAR_TERM_BUFS = 4
+VECTOR_TERM_BUFS = 10
+PINNED = True
+DRAIN = 4
+FIRST_LOAD_ROUND = 2
+LOADS_PER_ROUND = 2
+FIRST_PIECE_ROUND = 3
+PIECES_PER_ROUND = 2
+FIRST_MATMUL_UNIT_ROUND = 8
 
 FLOPS = 2 * B * S * R * OUT + 2 * B * Q * NS * R * DO
 
@@ -47,18 +57,22 @@ def tile_skilledlora_pb_kernel(tc, h, weights, lora_b, out):
     nc = tc.nc
     with ExitStack() as ctx:
         consts = ctx.enter_context(tc.tile_pool(name="consts", bufs=1))
-        h_pool = ctx.enter_context(tc.tile_pool(name="h_rows", bufs=B))
-        h_grouped_pool = ctx.enter_context(tc.tile_pool(name="h_grouped", bufs=2))
-        skill_pool = ctx.enter_context(tc.tile_pool(name="skills", bufs=2 * NS))
-        sum_pool = ctx.enter_context(tc.tile_pool(name="sums", bufs=2 * PAIR))
-        rounded_pool = ctx.enter_context(tc.tile_pool(name="rounded", bufs=3 * PAIR))
-        mix_pool = ctx.enter_context(tc.tile_pool(name="mix", bufs=2 * PAIR))
-        store_pool = ctx.enter_context(tc.tile_pool(name="store", bufs=2 * PAIR))
-        tensor_pool = ctx.enter_context(tc.tile_pool(name="tensor", bufs=TENSOR_SPLITS))
-        psum_turn = ctx.enter_context(tc.psum_pool(name="psum_turn", bufs=2))
-        psum_mix = ctx.enter_context(tc.psum_pool(name="psum_mix", bufs=2))
-        psum_out = ctx.enter_context(tc.psum_pool(name="psum_out", bufs=4))
-        ctx.enter_context(tc.manual_schedule())
+        h_pool = ctx.enter_context(tc.tile_pool(name="h_rows", bufs=2))
+        h_grouped_pool = ctx.enter_context(tc.tile_pool(name="h_grouped", bufs=1))
+        half_pool = ctx.enter_context(tc.tile_pool(name="half_skills", bufs=2 * NS))
+        whole_pool = ctx.enter_context(tc.tile_pool(name="whole_skills", bufs=NS))
+        stacked_pool = ctx.enter_context(tc.tile_pool(name="stacked", bufs=2))
+        scalar_term_pool = ctx.enter_context(tc.tile_pool(name="scalar_terms", bufs=SCALAR_TERM_BUFS))
+        vector_term_pool = ctx.enter_context(tc.tile_pool(name="vector_terms", bufs=VECTOR_TERM_BUFS))
+        turned_pool = ctx.enter_context(tc.tile_pool(name="turned", bufs=2))
+        mixed_pool = ctx.enter_context(tc.tile_pool(name="mixed", bufs=3))
+        mx_pool = ctx.enter_context(tc.tile_pool(name="mx", bufs=5))
+        store_pool = ctx.enter_context(tc.tile_pool(name="store", bufs=3))
+        psum_acc = ctx.enter_context(tc.psum_pool(name="psum_acc", bufs=3))
+        psum_back = ctx.enter_context(tc.psum_pool(name="psum_back", bufs=2))
+        psum_out = ctx.enter_context(tc.psum_pool(name="psum_out", bufs=3))
+        if PINNED:
+            ctx.enter_context(tc.manual_schedule())
 
         w_bf16 = consts.tile([P, B * Q * NS], BF16)
         nc.scalar.dma_start(
@@ -67,8 +81,6 @@ def tile_skilledlora_pb_kernel(tc, h, weights, lora_b, out):
         w_f32 = consts.tile([P, B * Q * NS], F32)
         nc.vector.tensor_copy(out=w_f32[:], in_=w_bf16[:])
 
-        identity = consts.tile([P, P], BF16)
-        make_identity(nc, identity[:])
         identity_f32 = consts.tile([P, P], F32)
         make_identity(nc, identity_f32[:])
 
@@ -86,26 +98,26 @@ def tile_skilledlora_pb_kernel(tc, h, weights, lora_b, out):
             axis=ALONG_ROW,
             op=ADD,
         )
-        masked = consts.tile([P, B, TENSOR_SPLITS, NS], F32)
+        masked = consts.tile([P, B, MATMUL_SPLITS, NS], F32)
         nc.vector.tensor_tensor(
             out=masked[:],
-            in0=w_f32[:].rearrange("p (b q k) -> p b q k", b=B, q=Q)[:, :, VECTOR_ONLY_SPLITS:Q, :],
-            in1=is_skill[:].unsqueeze(1).unsqueeze(1).to_broadcast([P, B, TENSOR_SPLITS, NS]),
+            in0=w_f32[:].rearrange("p (b q k) -> p b q k", b=B, q=Q)[:, :, FIRST_MATMUL_SPLIT:Q, :],
+            in1=is_skill[:].unsqueeze(1).unsqueeze(1).to_broadcast([P, B, MATMUL_SPLITS, NS]),
             op=MULT,
         )
-        own_weight = consts.tile([P, B, TENSOR_SPLITS], F32)
+        own_weight = consts.tile([P, B, MATMUL_SPLITS], F32)
         nc.vector.tensor_reduce(out=own_weight[:], in_=masked[:], axis=ALONG_ROW, op=ADD)
-        mixers = consts.tile([P, TENSOR_SPLITS, B, RANKS_PER_MATMUL], BF16)
+        mixers = consts.tile([P, MATMUL_SPLITS, B, RANKS_PER_MATMUL], BF16)
         nc.vector.tensor_tensor(
             out=mixers[:],
             in0=is_rank[:]
             .unsqueeze(1)
             .unsqueeze(1)
-            .to_broadcast([P, TENSOR_SPLITS, B, RANKS_PER_MATMUL]),
+            .to_broadcast([P, MATMUL_SPLITS, B, RANKS_PER_MATMUL]),
             in1=own_weight[:]
             .rearrange("p b q -> p q b")
             .unsqueeze(3)
-            .to_broadcast([P, TENSOR_SPLITS, B, RANKS_PER_MATMUL]),
+            .to_broadcast([P, MATMUL_SPLITS, B, RANKS_PER_MATMUL]),
             op=MULT,
         )
 
@@ -116,201 +128,279 @@ def tile_skilledlora_pb_kernel(tc, h, weights, lora_b, out):
             column = (b * Q + q) * NS + k
             return w_f32[:, column : column + 1]
 
-        def planes_on_vector(q):
-            return PACK if q < VECTOR_ONLY_SPLITS else PACK - TENSOR_PLANES
+        skills = {}
 
-        def load_skills(q):
-            planes = planes_on_vector(q)
-            tiles = []
-            for k in range(NS):
-                skill = skill_pool.tile([P, planes, DO], BF16)
-                nc.sync.dma_start(
-                    out=skill[:],
-                    in_=lora_b[q, k].rearrange("(p t) d -> p t d", t=PACK)[:, 0:planes, :],
-                )
-                tiles.append(skill)
-            return tiles
+        def load_half_skill(q, c, k):
+            half = half_pool.tile([P, PACK, GROUP], BF16)
+            nc.sync.dma_start(
+                out=half[:],
+                in_=lora_b[q, k].rearrange("(p t) d -> p t d", t=PACK)[
+                    :, :, c * GROUP : (c + 1) * GROUP
+                ],
+            )
+            skills.setdefault((q, c), []).append(half[:])
 
-        def load_stacked(q):
-            stacked = tensor_pool.tile([P, WORDS_PER_STRIDE, TENSOR_PLANES, DO], BF16)
+        def load_whole_skill(q, k):
+            whole = whole_pool.tile([P, PACK, DO], BF16)
+            nc.sync.dma_start(out=whole[:], in_=lora_b[q, k].rearrange("(p t) d -> p t d", t=PACK))
+            for c in range(GROUPS_PER_SPLIT):
+                skills.setdefault((q, c), []).append(whole[:, :, c * GROUP : (c + 1) * GROUP])
+
+        stacked_of = {}
+
+        def load_stacked(g):
+            q, c = MATMUL_GROUPS[g]
+            stacked = stacked_pool.tile([P, WORDS_PER_STRIDE, PACK, GROUP], BF16)
             nc.sync.dma_start(
                 out=stacked[:],
                 in_=lora_b[q].rearrange(
                     "k (g a t) d -> (k g) a t d", a=WORDS_PER_STRIDE, t=PACK
-                )[:, :, PACK - TENSOR_PLANES : PACK, :],
+                )[:, :, :, c * GROUP : (c + 1) * GROUP],
             )
-            return stacked
+            stacked_of[g] = stacked
 
-        def mix_on_tensor(q, stacked):
-            mixed = tensor_pool.tile([P, FEATURE_BLOCKS, TENSOR_PLANES, B, P], BF16)
-            for f in range(FEATURE_BLOCKS):
-                for t in range(TENSOR_PLANES):
-                    bank = psum_mix.tile([P, WORDS_PER_STRIDE, B, RANKS_PER_MATMUL], F32)
-                    for a in range(WORDS_PER_STRIDE):
-                        nc.tensor.matmul(
-                            out=bank[:, a, :, :].rearrange("p b g -> p (b g)"),
-                            lhsT=stacked[:, a, t, f * P : (f + 1) * P],
-                            rhs=mixers[:, q - VECTOR_ONLY_SPLITS, :, :].rearrange("p b g -> p (b g)"),
-                            start=True,
-                            stop=True,
-                        )
-                    nc.scalar.copy(
-                        out=mixed[:, f, t, :, :].rearrange(
-                            "p b (g a) -> p b g a", a=WORDS_PER_STRIDE
-                        ),
-                        in_=bank[:].rearrange("p a b g -> p b g a"),
-                    )
-            return mixed
+        h_rows_of = {}
 
         def load_h(b):
             h_rows = h_pool.tile([P, TOKEN_TILES, R], BF16)
             nc.sync.dma_start(out=h_rows[:], in_=h[b].rearrange("(n p) r -> p n r", p=P))
-            return h_rows
+            h_rows_of[b] = h_rows
 
         def quantise_h(b, h_rows):
-            halves = PACK // 2
             h_grouped = h_grouped_pool.tile([P, S * PACK], BF16, align_bytes=64)
-            grouped_words = h_grouped[:].bitcast(F32).rearrange("p (s u) -> p s u", u=halves)
-            tiles_per_bank = BANK // (halves * P)
+            grouped_words = h_grouped[:].bitcast(F32).rearrange("p (s u) -> p s u", u=HALVES)
+            tiles_per_bank = BANK // (HALVES * P)
             for first in range(0, TOKEN_TILES, tiles_per_bank):
-                turned = psum_turn.tile([P, tiles_per_bank, halves, P], F32, tag="turned")
+                turned_h = psum_back.tile([P, tiles_per_bank, HALVES, P], F32, tag="back")
                 for n in range(tiles_per_bank):
                     words = h_rows[:, first + n, :].bitcast(F32).rearrange(
-                        "p (w u) -> p u w", u=halves
+                        "p (w u) -> p u w", u=HALVES
                     )
-                    for u in range(halves):
-                        nc.tensor.transpose(turned[:, n, u, :], words[:, u, :], identity_f32[:])
+                    for u in range(HALVES):
+                        nc.tensor.transpose(turned_h[:, n, u, :], words[:, u, :], identity_f32[:])
                 nc.scalar.copy(
                     out=grouped_words[:, first * P : (first + tiles_per_bank) * P, :].rearrange(
                         "p (n s) u -> p n s u", n=tiles_per_bank
                     ),
-                    in_=turned[:].rearrange("p n u s -> p n s u"),
+                    in_=turned_h[:].rearrange("p n u s -> p n s u"),
                 )
             nc.vector.quantize_mx(
                 out=h_codes[:, b, :].bitcast(FP8X4), scales=h_scales[:, b, :], in_=h_grouped[:]
             )
 
-        def start_sums(step):
-            q, c, examples = step
-            planes = planes_on_vector(q)
-            sums = []
-            for b in examples:
-                total = sum_pool.tile([P, planes, D_CHUNK], F32)
-                rounded = rounded_pool.tile([P, PACK, D_CHUNK], BF16)
-                nc.scalar.activation(
-                    out=total[:],
-                    in_=skills[q][0][:, :, c * D_CHUNK : (c + 1) * D_CHUNK],
-                    func=COPY,
-                    scale=weight_of(b, q, 0),
+        def mix_piece(q, stacked, mixed, j, u, hi):
+            bank = psum_acc.tile([P, MATMULS_PER_BANK, B, RANKS_PER_MATMUL], F32, tag="acc")
+            for m in range(MATMULS_PER_BANK):
+                lo, e = divmod(m, HALVES)
+                nc.tensor.matmul(
+                    out=bank[:, m, :, :].rearrange("p b g -> p (b g)"),
+                    lhsT=stacked[:, 4 * hi + lo, HALVES * u + e, j * P : (j + 1) * P],
+                    rhs=mixers[:, q - FIRST_MATMUL_SPLIT, :, :].rearrange("p b g -> p (b g)"),
+                    start=True,
+                    stop=True,
                 )
-                sums.append((total, rounded))
-            if planes < PACK:
-                blocks = D_CHUNK // P
-                for b, (total, rounded) in zip(examples, sums):
-                    back = psum_turn.tile([P, TENSOR_PLANES, D_CHUNK], BF16, tag="turned")
-                    for t in range(TENSOR_PLANES):
-                        for j in range(blocks):
-                            nc.tensor.transpose(
-                                back[:, t, j * P : (j + 1) * P],
-                                mixed_of[q][:, c * blocks + j, t, b, :],
-                                identity[:],
-                            )
-                    nc.scalar.copy(out=rounded[:, planes:PACK, :], in_=back[:])
-            return sums
+            nc.scalar.copy(
+                out=mixed[:, j, :, :].rearrange(
+                    "p b (u g hi m) -> p b u g hi m", u=HALVES, hi=2, m=MATMULS_PER_BANK
+                )[:, :, u, :, hi, :],
+                in_=bank[:].rearrange("p m b g -> p b g m"),
+            )
 
-        def add_skill(step, sums, k):
-            q, c, examples = step
-            planes = planes_on_vector(q)
-            for b, (total, rounded) in zip(examples, sums):
-                nc.vector.scalar_tensor_tensor(
-                    out=rounded[:, 0:planes, :] if k == NS - 1 else total[:],
-                    in0=skills[q][k][:, :, c * D_CHUNK : (c + 1) * D_CHUNK],
-                    scalar=weight_of(b, q, k),
-                    in1=total[:],
-                    op0=MULT,
-                    op1=ADD,
-                )
-
-        def group_words(sums):
-            grouped_tiles = []
-            for total, rounded in sums:
-                grouped = mix_pool.tile([P, D_CHUNK, PACK], BF16, align_bytes=64)
-                nc.scalar.copy(out=grouped[:], in_=rounded[:].rearrange("p t d -> p d t"))
-                grouped_tiles.append(grouped)
-            return grouped_tiles
-
-        def multiply_and_store(step, grouped_tiles):
-            q, c, examples = step
-            first_column = q * DO + c * D_CHUNK
-            for b, grouped in zip(examples, grouped_tiles):
-                codes = mix_pool.tile([P, D_CHUNK], U32, align_bytes=64)
-                scales = mix_pool.tile([P, D_CHUNK], U8, align_bytes=64)
-                nc.vector.quantize_mx(
-                    out=codes[:].bitcast(FP8X4),
-                    scales=scales[:],
-                    in_=grouped[:].rearrange("p d t -> p (d t)"),
-                )
-                result = store_pool.tile([P, TOKEN_TILES, D_CHUNK], F32)
-                for first in range(0, TOKEN_TILES, TILES_PER_BANK):
-                    product = psum_out.tile([P, TILES_PER_BANK, D_CHUNK], F32)
-                    for j in range(TILES_PER_BANK):
-                        tokens = slice((first + j) * P, (first + j + 1) * P)
-                        nc.tensor.matmul_mx(
-                            out=product[:, j, :],
-                            lhsT=h_codes[:, b, tokens].bitcast(FP8X4),
-                            lhsT_scale=h_scales[:, b, tokens],
-                            rhs=codes[:].bitcast(FP8X4),
-                            rhs_scale=scales[:],
-                            start=True,
-                            stop=True,
-                        )
+        def scalar_terms(unit):
+            q, c, b = unit
+            terms = []
+            for k in range(NS):
+                if ROLES[k] == "S":
+                    term = scalar_term_pool.tile([P, PACK, GROUP], F32)
                     nc.scalar.activation(
-                        out=result[:, first : first + TILES_PER_BANK, :],
-                        in_=product[:],
-                        func=COPY,
-                        scale=SCALING,
+                        out=term[:], in_=skills[(q, c)][k], func=COPY,
+                        scale=weight_of(b, q, k),
                     )
-                nc.sync.dma_start(
-                    out=out[b, :, first_column : first_column + D_CHUNK].rearrange(
-                        "(n p) d -> p n d", p=P
-                    ),
-                    in_=result[:],
+                    terms.append(term)
+            return terms
+
+        def vector_products(unit, terms):
+            q, c, b = unit
+            for k in range(NS):
+                if ROLES[k] == "V":
+                    term = vector_term_pool.tile([P, PACK, GROUP], F32)
+                    nc.vector.tensor_scalar(
+                        out=term[:], in0=skills[(q, c)][k],
+                        scalar1=weight_of(b, q, k), scalar2=None, op0=MULT,
+                    )
+                    terms.append(term)
+
+        def vector_adds(unit, terms):
+            q, c, b = unit
+            onto = 0
+            for k in range(NS):
+                if ROLES[k] == "A":
+                    nc.vector.scalar_tensor_tensor(
+                        out=terms[onto][:], in0=skills[(q, c)][k],
+                        scalar=weight_of(b, q, k), in1=terms[onto][:], op0=MULT, op1=ADD,
+                    )
+                    onto += 1
+
+        def add_terms(terms):
+            turned = turned_pool.tile([P, BLOCKS, R], BF16)
+            for j in range(BLOCKS):
+                acc = psum_acc.tile([P, PACK, P], F32, tag="acc")
+                for t in range(PACK):
+                    for i, term in enumerate(terms):
+                        nc.tensor.matmul(
+                            out=acc[:, t, :],
+                            lhsT=term[:, t, j * P : (j + 1) * P],
+                            rhs=identity_f32[:],
+                            is_transpose=True,
+                            start=(i == 0),
+                            stop=(i == len(terms) - 1),
+                        )
+                nc.scalar.copy(
+                    out=turned[:, j, :].rearrange("d (u p e) -> d u p e", u=HALVES, e=HALVES),
+                    in_=acc[:].rearrange("d (u e) p -> d u p e", u=HALVES),
                 )
+            return [turned[:, j, :] for j in range(BLOCKS)]
 
-        steps = [
-            (q, c, tuple(range(first, first + PAIR)))
+        def turn_back(blocks):
+            back = psum_back.tile([P, HALVES, GROUP], F32, tag="back")
+            for j, block in enumerate(blocks):
+                words = block.bitcast(F32)
+                for u in range(HALVES):
+                    nc.tensor.transpose(
+                        back[:, u, j * P : (j + 1) * P], words[:, u * P : (u + 1) * P],
+                        identity_f32[:],
+                    )
+            grouped = mx_pool.tile([P, GROUP * PACK], BF16, align_bytes=64)
+            nc.scalar.copy(
+                out=grouped[:].bitcast(F32).rearrange("p (d u) -> p d u", u=HALVES),
+                in_=back[:].rearrange("p u d -> p d u"),
+            )
+            return grouped
+
+        def quantise(grouped):
+            codes = mx_pool.tile([P, GROUP], U32, align_bytes=64)
+            scales = mx_pool.tile([P, GROUP], U8, align_bytes=64)
+            nc.vector.quantize_mx(out=codes[:].bitcast(FP8X4), scales=scales[:], in_=grouped[:])
+            return codes, scales
+
+        def multiply_and_store(unit, operand):
+            q, c, b = unit
+            codes, scales = operand
+            first_column = q * DO + c * GROUP
+            result = store_pool.tile([P, TOKEN_TILES, GROUP], F32)
+            for first in range(0, TOKEN_TILES, TILES_PER_BANK):
+                product = psum_out.tile([P, TILES_PER_BANK, GROUP], F32)
+                for n in range(TILES_PER_BANK):
+                    tokens = slice((first + n) * P, (first + n + 1) * P)
+                    nc.tensor.matmul_mx(
+                        out=product[:, n, :],
+                        lhsT=h_codes[:, b, tokens].bitcast(FP8X4),
+                        lhsT_scale=h_scales[:, b, tokens],
+                        rhs=codes[:].bitcast(FP8X4),
+                        rhs_scale=scales[:],
+                        start=True,
+                        stop=True,
+                    )
+                nc.scalar.activation(
+                    out=result[:, first : first + TILES_PER_BANK, :], in_=product[:], func=COPY,
+                    scale=SCALING,
+                )
+            nc.sync.dma_start(
+                out=out[b, :, first_column : first_column + GROUP].rearrange(
+                    "(n p) d -> p n d", p=P
+                ),
+                in_=result[:],
+            )
+
+        summed_units = [
+            (q, c, b)
             for q in range(Q)
-            for c in range(CHUNKS)
-            for first in range(0, B, PAIR)
+            for c in range(GROUPS_PER_SPLIT)
+            if (q, c) not in MATMUL_GROUPS
+            for b in range(B)
         ]
-        steps_that_meet_new_examples = B // PAIR
+        matmul_units = [(q, c, b) for (q, c) in MATMUL_GROUPS for b in range(B)]
+        pieces = [
+            (g, j, u, hi)
+            for g in range(len(MATMUL_GROUPS))
+            for j in range(BLOCKS)
+            for u in range(HALVES)
+            for hi in range(2)
+        ]
 
-        MULTIPLY_AFTER_ROUND = 3
-        QUANTISE_H_AFTER_ROUND = NS - 1
-
-        skills = {0: load_skills(0)}
-        h_rows_of = [load_h(b) for b in range(B)]
-        stacked_of = {}
-        for q in range(VECTOR_ONLY_SPLITS, Q):
-            stacked_of[q] = load_stacked(q)
+        for k in range(NS):
+            load_half_skill(0, 0, k)
+        load_h(0)
+        load_h(1)
+        for k in range(NS):
+            load_half_skill(0, 1, k)
+        load_stacked(0)
+        later_loads = (
+            [("whole", 1, k) for k in range(NS // 2)]
+            + [("stacked", 1, 0)]
+            + [("whole", 1, k) for k in range(NS // 2, NS)]
+            + [("stacked", 2, 0)]
+            + [("half", 2, k) for k in range(NS)]
+        )
+        loads_done = 0
         mixed_of = {}
-        sums_of = {0: start_sums(steps[0])}
-        grouped_of = {}
+        PIECES_PER_GROUP = len(pieces) // len(MATMUL_GROUPS)
 
-        for s, step in enumerate(steps):
-            q, c, examples = step
-            if s % STEPS_PER_SPLIT == 0 and q + 1 < Q:
-                skills[q + 1] = load_skills(q + 1)
-            if s + 1 < len(steps):
-                sums_of[s + 1] = start_sums(steps[s + 1])
-            if VECTOR_ONLY_SPLITS <= s < Q:
-                mixed_of[s] = mix_on_tensor(s, stacked_of[s])
-            for k in range(1, NS):
-                add_skill(step, sums_of[s], k)
-                if k == MULTIPLY_AFTER_ROUND and s > 0:
-                    multiply_and_store(steps[s - 1], grouped_of[s - 1])
-                if k == QUANTISE_H_AFTER_ROUND and s < steps_that_meet_new_examples:
-                    for b in examples:
-                        quantise_h(b, h_rows_of[b])
-            grouped_of[s] = group_words(sums_of[s])
-        multiply_and_store(steps[-1], grouped_of[len(steps) - 1])
+        rounds = len(summed_units)
+        terms_of = {0: scalar_terms(summed_units[0])}
+        to_turn = []
+        to_quantise = []
+        to_multiply = []
+        pieces_done = 0
+        matmul_units_done = 0
+
+        for i in range(rounds + DRAIN):
+            if i + 1 < rounds:
+                terms_of[i + 1] = scalar_terms(summed_units[i + 1])
+            if i < rounds:
+                vector_products(summed_units[i], terms_of[i])
+            quantised = [(unit, quantise(grouped)) for unit, grouped in to_quantise]
+            to_quantise = []
+            if i < rounds:
+                vector_adds(summed_units[i], terms_of[i])
+            if 1 <= i <= rounds:
+                to_turn.append((summed_units[i - 1], add_terms(terms_of[i - 1])))
+            if 1 <= i <= B:
+                quantise_h(i - 1, h_rows_of[i - 1])
+                if i + 1 < B:
+                    load_h(i + 1)
+            for unit, operand in to_multiply:
+                multiply_and_store(unit, operand)
+            to_multiply = quantised
+            if i >= FIRST_MATMUL_UNIT_ROUND and matmul_units_done < len(matmul_units):
+                unit = matmul_units[matmul_units_done]
+                g = MATMUL_GROUPS.index((unit[0], unit[1]))
+                assert pieces_done >= (g + 1) * PIECES_PER_GROUP
+                to_turn.append((unit, [mixed_of[g][:, j, unit[2], :] for j in range(BLOCKS)]))
+                matmul_units_done += 1
+            for unit, blocks in to_turn:
+                to_quantise.append((unit, turn_back(blocks)))
+            to_turn = []
+            if i >= FIRST_PIECE_ROUND:
+                for n in range(PIECES_PER_ROUND):
+                    if pieces_done < len(pieces):
+                        g, j, u, hi = pieces[pieces_done]
+                        if g not in mixed_of:
+                            mixed = mixed_pool.tile([P, BLOCKS, B, R], BF16)
+                            mixed_of[g] = mixed
+                        mix_piece(MATMUL_GROUPS[g][0], stacked_of[g], mixed_of[g], j, u, hi)
+                        pieces_done += 1
+            if i >= FIRST_LOAD_ROUND:
+                for n in range(LOADS_PER_ROUND):
+                    if loads_done < len(later_loads):
+                        kind, which, k = later_loads[loads_done]
+                        if kind == "whole":
+                            load_whole_skill(which, k)
+                        elif kind == "half":
+                            assert i >= B - 1
+                            load_half_skill(which, 0, k)
+                        else:
+                            assert pieces_done >= (which - 1) * PIECES_PER_GROUP
+                            load_stacked(which)
+                        loads_done += 1
+        assert matmul_units_done == len(matmul_units) and not to_quantise and not to_multiply

@@ -39,7 +39,7 @@ MATMUL_SPLITS = Q - FIRST_MATMUL_SPLIT
 MIXING_MATMULS = len(MATMUL_GROUPS) * BLOCKS * PACK * WORDS_PER_STRIDE
 assert MIXING_MATMULS * P * P * B * RANKS_PER_MATMUL * 10 < B * S * R * OUT
 
-ROLES = "SVVVVAAA"
+ROLES = "SVVVAAAA"
 SCALAR_TERM_BUFS = 4
 VECTOR_TERM_BUFS = 10
 PINNED = True

@@ -31,7 +31,7 @@ TILES_PER_BANK = BANK // GROUP
 
 RANKS_PER_MATMUL = P // NS
 WORDS_PER_STRIDE = R // RANKS_PER_MATMUL // PACK
-MATMULS_PER_BANK = BANK // (B * RANKS_PER_MATMUL)
+MATMULS_PER_BANK = 2 * BANK // (B * RANKS_PER_MATMUL)
 
 MATMUL_GROUPS = ((2, 1), (3, 0), (3, 1))
 FIRST_MATMUL_SPLIT = 2
@@ -39,16 +39,17 @@ MATMUL_SPLITS = Q - FIRST_MATMUL_SPLIT
 MIXING_MATMULS = len(MATMUL_GROUPS) * BLOCKS * PACK * WORDS_PER_STRIDE
 assert MIXING_MATMULS * P * P * B * RANKS_PER_MATMUL * 10 < B * S * R * OUT
 
-ROLES = "SVVVAAAA"
-SCALAR_TERM_BUFS = 4
-VECTOR_TERM_BUFS = 10
+ROLES_IN_TURN = ("SSVVAAAA", "SVVVAAAA")
+HALVED_UNITS = 1
+SCALAR_TERM_BUFS = 6
+VECTOR_TERM_BUFS = 8
 PINNED = True
 DRAIN = 4
 FIRST_LOAD_ROUND = 2
 LOADS_PER_ROUND = 2
 FIRST_PIECE_ROUND = 3
-PIECES_PER_ROUND = 2
-FIRST_MATMUL_UNIT_ROUND = 8
+PIECES_PER_ROUND = 1
+FIRST_MATMUL_UNIT_ROUND = 7
 
 FLOPS = 2 * B * S * R * OUT + 2 * B * Q * NS * R * DO
 
@@ -188,81 +189,79 @@ def tile_skilledlora_pb_kernel(tc, h, weights, lora_b, out):
                 out=h_codes[:, b, :].bitcast(FP8X4), scales=h_scales[:, b, :], in_=h_grouped[:]
             )
 
-        def mix_piece(q, stacked, mixed, j, u, hi):
-            bank = psum_acc.tile([P, MATMULS_PER_BANK, B, RANKS_PER_MATMUL], F32, tag="acc")
+        def mix_piece(q, stacked, mixed, j, u):
+            bank = psum_acc.tile([P, MATMULS_PER_BANK, B, RANKS_PER_MATMUL], BF16, tag="acc")
             for m in range(MATMULS_PER_BANK):
-                lo, e = divmod(m, HALVES)
+                a, e = divmod(m, HALVES)
                 nc.tensor.matmul(
                     out=bank[:, m, :, :].rearrange("p b g -> p (b g)"),
-                    lhsT=stacked[:, 4 * hi + lo, HALVES * u + e, j * P : (j + 1) * P],
+                    lhsT=stacked[:, a, HALVES * u + e, j * P : (j + 1) * P],
                     rhs=mixers[:, q - FIRST_MATMUL_SPLIT, :, :].rearrange("p b g -> p (b g)"),
                     start=True,
                     stop=True,
                 )
             nc.scalar.copy(
                 out=mixed[:, j, :, :].rearrange(
-                    "p b (u g hi m) -> p b u g hi m", u=HALVES, hi=2, m=MATMULS_PER_BANK
-                )[:, :, u, :, hi, :],
+                    "p b (u g m) -> p b u g m", u=HALVES, m=MATMULS_PER_BANK
+                )[:, :, u, :, :],
                 in_=bank[:].rearrange("p m b g -> p b g m"),
             )
 
-        def scalar_terms(unit):
-            q, c, b = unit
-            terms = []
-            for k in range(NS):
-                if ROLES[k] == "S":
-                    term = scalar_term_pool.tile([P, PACK, GROUP], F32)
-                    nc.scalar.activation(
-                        out=term[:], in_=skills[(q, c)][k], func=COPY,
-                        scale=weight_of(b, q, k),
-                    )
-                    terms.append(term)
-            return terms
+        def columns_of(unit):
+            q, c, b, first_block, blocks = unit
+            return slice(first_block * P, (first_block + blocks) * P)
 
-        def vector_products(unit, terms):
-            q, c, b = unit
+        def scalar_term(unit, k):
+            q, c, b, first_block, blocks = unit
+            term = scalar_term_pool.tile([P, PACK, blocks * P], F32)
+            nc.scalar.activation(
+                out=term[:], in_=skills[(q, c)][k][:, :, columns_of(unit)], func=COPY,
+                scale=weight_of(b, q, k),
+            )
+            return term
+
+        def vector_products(unit, roles, terms):
+            q, c, b, first_block, blocks = unit
             for k in range(NS):
-                if ROLES[k] == "V":
-                    term = vector_term_pool.tile([P, PACK, GROUP], F32)
+                if roles[k] == "V":
+                    term = vector_term_pool.tile([P, PACK, blocks * P], F32)
                     nc.vector.tensor_scalar(
-                        out=term[:], in0=skills[(q, c)][k],
+                        out=term[:], in0=skills[(q, c)][k][:, :, columns_of(unit)],
                         scalar1=weight_of(b, q, k), scalar2=None, op0=MULT,
                     )
                     terms.append(term)
 
-        def vector_adds(unit, terms):
-            q, c, b = unit
+        def vector_adds(unit, roles, terms):
+            q, c, b, first_block, blocks = unit
             onto = 0
             for k in range(NS):
-                if ROLES[k] == "A":
+                if roles[k] == "A":
                     nc.vector.scalar_tensor_tensor(
-                        out=terms[onto][:], in0=skills[(q, c)][k],
+                        out=terms[onto][:], in0=skills[(q, c)][k][:, :, columns_of(unit)],
                         scalar=weight_of(b, q, k), in1=terms[onto][:], op0=MULT, op1=ADD,
                     )
                     onto += 1
 
-        def add_terms(terms):
-            turned = turned_pool.tile([P, BLOCKS, R], BF16)
-            for j in range(BLOCKS):
-                acc = psum_acc.tile([P, PACK, P], F32, tag="acc")
-                for t in range(PACK):
-                    for i, term in enumerate(terms):
-                        nc.tensor.matmul(
-                            out=acc[:, t, :],
-                            lhsT=term[:, t, j * P : (j + 1) * P],
-                            rhs=identity_f32[:],
-                            is_transpose=True,
-                            start=(i == 0),
-                            stop=(i == len(terms) - 1),
-                        )
-                nc.scalar.copy(
-                    out=turned[:, j, :].rearrange("d (u p e) -> d u p e", u=HALVES, e=HALVES),
-                    in_=acc[:].rearrange("d (u e) p -> d u p e", u=HALVES),
-                )
-            return [turned[:, j, :] for j in range(BLOCKS)]
+        def add_block(terms, j, turned):
+            acc = psum_acc.tile([P, PACK, P], F32, tag="acc")
+            for t in range(PACK):
+                for i, term in enumerate(terms):
+                    nc.tensor.matmul(
+                        out=acc[:, t, :],
+                        lhsT=term[:, t, j * P : (j + 1) * P],
+                        rhs=identity_f32[:],
+                        is_transpose=True,
+                        start=(i == 0),
+                        stop=(i == len(terms) - 1),
+                    )
+            nc.scalar.copy(
+                out=turned[:, j, :].rearrange("d (u p e) -> d u p e", u=HALVES, e=HALVES),
+                in_=acc[:].rearrange("d (u e) p -> d u p e", u=HALVES),
+            )
 
         def turn_back(blocks):
-            back = psum_back.tile([P, HALVES, GROUP], F32, tag="back")
+            width = len(blocks) * P
+            back = psum_back.tile([P, HALVES, width], F32, tag="back")
             for j, block in enumerate(blocks):
                 words = block.bitcast(F32)
                 for u in range(HALVES):
@@ -270,27 +269,30 @@ def tile_skilledlora_pb_kernel(tc, h, weights, lora_b, out):
                         back[:, u, j * P : (j + 1) * P], words[:, u * P : (u + 1) * P],
                         identity_f32[:],
                     )
-            grouped = mx_pool.tile([P, GROUP * PACK], BF16, align_bytes=64)
+            grouped = mx_pool.tile([P, width * PACK], BF16, align_bytes=64)
             nc.scalar.copy(
                 out=grouped[:].bitcast(F32).rearrange("p (d u) -> p d u", u=HALVES),
                 in_=back[:].rearrange("p u d -> p d u"),
             )
             return grouped
 
-        def quantise(grouped):
-            codes = mx_pool.tile([P, GROUP], U32, align_bytes=64)
-            scales = mx_pool.tile([P, GROUP], U8, align_bytes=64)
+        def quantise(unit, grouped):
+            width = unit[4] * P
+            codes = mx_pool.tile([P, width], U32, align_bytes=64)
+            scales = mx_pool.tile([P, width], U8, align_bytes=64)
             nc.vector.quantize_mx(out=codes[:].bitcast(FP8X4), scales=scales[:], in_=grouped[:])
             return codes, scales
 
         def multiply_and_store(unit, operand):
-            q, c, b = unit
+            q, c, b, first_block, blocks = unit
             codes, scales = operand
-            first_column = q * DO + c * GROUP
-            result = store_pool.tile([P, TOKEN_TILES, GROUP], F32)
-            for first in range(0, TOKEN_TILES, TILES_PER_BANK):
-                product = psum_out.tile([P, TILES_PER_BANK, GROUP], F32)
-                for n in range(TILES_PER_BANK):
+            width = blocks * P
+            first_column = q * DO + c * GROUP + first_block * P
+            tiles_per_bank = BANK // width
+            result = store_pool.tile([P, TOKEN_TILES, width], F32)
+            for first in range(0, TOKEN_TILES, tiles_per_bank):
+                product = psum_out.tile([P, tiles_per_bank, width], F32)
+                for n in range(tiles_per_bank):
                     tokens = slice((first + n) * P, (first + n + 1) * P)
                     nc.tensor.matmul_mx(
                         out=product[:, n, :],
@@ -302,30 +304,34 @@ def tile_skilledlora_pb_kernel(tc, h, weights, lora_b, out):
                         stop=True,
                     )
                 nc.scalar.activation(
-                    out=result[:, first : first + TILES_PER_BANK, :], in_=product[:], func=COPY,
+                    out=result[:, first : first + tiles_per_bank, :], in_=product[:], func=COPY,
                     scale=SCALING,
                 )
             nc.sync.dma_start(
-                out=out[b, :, first_column : first_column + GROUP].rearrange(
+                out=out[b, :, first_column : first_column + width].rearrange(
                     "(n p) d -> p n d", p=P
                 ),
                 in_=result[:],
             )
 
-        summed_units = [
-            (q, c, b)
+        whole_units = [
+            (q, c, b, 0, BLOCKS)
             for q in range(Q)
             for c in range(GROUPS_PER_SPLIT)
             if (q, c) not in MATMUL_GROUPS
             for b in range(B)
         ]
-        matmul_units = [(q, c, b) for (q, c) in MATMUL_GROUPS for b in range(B)]
+        summed_units = whole_units[: len(whole_units) - HALVED_UNITS] + [
+            (q, c, b, j, 1)
+            for (q, c, b, first_block, blocks) in whole_units[len(whole_units) - HALVED_UNITS :]
+            for j in range(BLOCKS)
+        ]
+        matmul_units = [(q, c, b, 0, BLOCKS) for (q, c) in MATMUL_GROUPS for b in range(B)]
         pieces = [
-            (g, j, u, hi)
+            (g, j, u)
             for g in range(len(MATMUL_GROUPS))
             for j in range(BLOCKS)
             for u in range(HALVES)
-            for hi in range(2)
         ]
 
         for k in range(NS):
@@ -347,7 +353,14 @@ def tile_skilledlora_pb_kernel(tc, h, weights, lora_b, out):
         PIECES_PER_GROUP = len(pieces) // len(MATMUL_GROUPS)
 
         rounds = len(summed_units)
-        terms_of = {0: scalar_terms(summed_units[0])}
+
+        def roles_of(i):
+            return ROLES_IN_TURN[i % len(ROLES_IN_TURN)]
+
+        def scalar_skills(i):
+            return [k for k in range(NS) if roles_of(i)[k] == "S"]
+
+        terms_of = {0: [scalar_term(summed_units[0], k) for k in scalar_skills(0)]}
         to_turn = []
         to_quantise = []
         to_multiply = []
@@ -355,16 +368,27 @@ def tile_skilledlora_pb_kernel(tc, h, weights, lora_b, out):
         matmul_units_done = 0
 
         for i in range(rounds + DRAIN):
-            if i + 1 < rounds:
-                terms_of[i + 1] = scalar_terms(summed_units[i + 1])
             if i < rounds:
-                vector_products(summed_units[i], terms_of[i])
-            quantised = [(unit, quantise(grouped)) for unit, grouped in to_quantise]
+                vector_products(summed_units[i], roles_of(i), terms_of[i])
+            if i < rounds:
+                vector_adds(summed_units[i], roles_of(i), terms_of[i])
+            quantised = [(unit, quantise(unit, grouped)) for unit, grouped in to_quantise]
             to_quantise = []
-            if i < rounds:
-                vector_adds(summed_units[i], terms_of[i])
+            fillers = scalar_skills(i + 1) if i + 1 < rounds else []
+            filled = 0
+            if i + 1 < rounds:
+                terms_of[i + 1] = []
             if 1 <= i <= rounds:
-                to_turn.append((summed_units[i - 1], add_terms(terms_of[i - 1])))
+                unit = summed_units[i - 1]
+                turned = turned_pool.tile([P, unit[4], R], BF16)
+                for j in range(unit[4]):
+                    if filled < len(fillers):
+                        terms_of[i + 1].append(scalar_term(summed_units[i + 1], fillers[filled]))
+                        filled += 1
+                    add_block(terms_of[i - 1], j, turned)
+                to_turn.append((unit, [turned[:, j, :] for j in range(unit[4])]))
+            for k in fillers[filled:]:
+                terms_of[i + 1].append(scalar_term(summed_units[i + 1], k))
             if 1 <= i <= B:
                 quantise_h(i - 1, h_rows_of[i - 1])
                 if i + 1 < B:
@@ -384,11 +408,11 @@ def tile_skilledlora_pb_kernel(tc, h, weights, lora_b, out):
             if i >= FIRST_PIECE_ROUND:
                 for n in range(PIECES_PER_ROUND):
                     if pieces_done < len(pieces):
-                        g, j, u, hi = pieces[pieces_done]
+                        g, j, u = pieces[pieces_done]
                         if g not in mixed_of:
                             mixed = mixed_pool.tile([P, BLOCKS, B, R], BF16)
                             mixed_of[g] = mixed
-                        mix_piece(MATMUL_GROUPS[g][0], stacked_of[g], mixed_of[g], j, u, hi)
+                        mix_piece(MATMUL_GROUPS[g][0], stacked_of[g], mixed_of[g], j, u)
                         pieces_done += 1
             if i >= FIRST_LOAD_ROUND:
                 for n in range(LOADS_PER_ROUND):

@@ -69,9 +69,7 @@ def tile_skilledlora_pb_kernel(tc, h, weights, lora_b, out):
         mixed_pool = ctx.enter_context(tc.tile_pool(name="mixed", bufs=3))
         mx_pool = ctx.enter_context(tc.tile_pool(name="mx", bufs=5))
         store_pool = ctx.enter_context(tc.tile_pool(name="store", bufs=3))
-        psum_acc = ctx.enter_context(tc.psum_pool(name="psum_acc", bufs=3))
-        psum_back = ctx.enter_context(tc.psum_pool(name="psum_back", bufs=2))
-        psum_out = ctx.enter_context(tc.psum_pool(name="psum_out", bufs=3))
+        psum = ctx.enter_context(tc.psum_pool(name="psum", bufs=8))
         if PINNED:
             ctx.enter_context(tc.manual_schedule())
 
@@ -172,7 +170,7 @@ def tile_skilledlora_pb_kernel(tc, h, weights, lora_b, out):
             grouped_words = h_grouped[:].bitcast(F32).rearrange("p (s u) -> p s u", u=HALVES)
             tiles_per_bank = BANK // (HALVES * P)
             for first in range(0, TOKEN_TILES, tiles_per_bank):
-                turned_h = psum_back.tile([P, tiles_per_bank, HALVES, P], F32, tag="back")
+                turned_h = psum.tile([P, tiles_per_bank, HALVES, P], F32, tag="bank")
                 for n in range(tiles_per_bank):
                     words = h_rows[:, first + n, :].bitcast(F32).rearrange(
                         "p (w u) -> p u w", u=HALVES
@@ -190,7 +188,7 @@ def tile_skilledlora_pb_kernel(tc, h, weights, lora_b, out):
             )
 
         def mix_piece(q, stacked, mixed, j, u):
-            bank = psum_acc.tile([P, MATMULS_PER_BANK, B, RANKS_PER_MATMUL], BF16, tag="acc")
+            bank = psum.tile([P, MATMULS_PER_BANK, B, RANKS_PER_MATMUL], BF16, tag="bank")
             for m in range(MATMULS_PER_BANK):
                 a, e = divmod(m, HALVES)
                 nc.tensor.matmul(
@@ -243,7 +241,7 @@ def tile_skilledlora_pb_kernel(tc, h, weights, lora_b, out):
                     onto += 1
 
         def add_block(terms, j, turned):
-            acc = psum_acc.tile([P, PACK, P], F32, tag="acc")
+            acc = psum.tile([P, PACK, P], F32, tag="bank")
             for t in range(PACK):
                 for i, term in enumerate(terms):
                     nc.tensor.matmul(
@@ -261,7 +259,7 @@ def tile_skilledlora_pb_kernel(tc, h, weights, lora_b, out):
 
         def turn_back(blocks):
             width = len(blocks) * P
-            back = psum_back.tile([P, HALVES, width], F32, tag="back")
+            back = psum.tile([P, HALVES, width], F32, tag="bank")
             for j, block in enumerate(blocks):
                 words = block.bitcast(F32)
                 for u in range(HALVES):
@@ -291,7 +289,7 @@ def tile_skilledlora_pb_kernel(tc, h, weights, lora_b, out):
             tiles_per_bank = BANK // width
             result = store_pool.tile([P, TOKEN_TILES, width], F32)
             for first in range(0, TOKEN_TILES, tiles_per_bank):
-                product = psum_out.tile([P, tiles_per_bank, width], F32)
+                product = psum.tile([P, tiles_per_bank, width], F32, tag="bank")
                 for n in range(tiles_per_bank):
                     tokens = slice((first + n) * P, (first + n + 1) * P)
                     nc.tensor.matmul_mx(

@@ -11,7 +11,8 @@ FP8X4 = mybir.dt.float8_e4m3fn_x4
 MULT = mybir.AluOpType.mult
 ADD = mybir.AluOpType.add
 COPY = mybir.ActivationFunctionType.Copy
-ALONG_ROW = mybir.AxisListType.X
+X = mybir.AxisListType.X
+XY = mybir.AxisListType.XY
 
 B, S, R, OUT, Q, NS = 4, 512, 512, 2048, 4, 8
 DO = OUT // Q
@@ -27,29 +28,38 @@ BANK = 512
 GROUP = 256
 BLOCKS = GROUP // P
 GROUPS_PER_SPLIT = DO // GROUP
-TILES_PER_BANK = BANK // GROUP
 
-RANKS_PER_MATMUL = P // NS
-WORDS_PER_STRIDE = R // RANKS_PER_MATMUL // PACK
-MATMULS_PER_BANK = 2 * BANK // (B * RANKS_PER_MATMUL)
+RUNS = 8
+PAIRS = R // RUNS // 2
+FULL = B * RUNS * 2
+MATMULS_PER_BANK = 2 * BANK // FULL
 
 MATMUL_GROUPS = ((2, 1), (3, 0), (3, 1))
 FIRST_MATMUL_SPLIT = 2
 MATMUL_SPLITS = Q - FIRST_MATMUL_SPLIT
-MIXING_MATMULS = len(MATMUL_GROUPS) * BLOCKS * PACK * WORDS_PER_STRIDE
-assert MIXING_MATMULS * P * P * B * RANKS_PER_MATMUL * 10 < B * S * R * OUT
+MIXING_MATMULS = len(MATMUL_GROUPS) * BLOCKS * PAIRS
+assert MIXING_MATMULS * P * P * FULL * 10 < B * S * R * OUT
 
-ROLES_IN_TURN = ("SSVVAAAA", "SVVVAAAA")
-HALVED_UNITS = 1
-SCALAR_TERM_BUFS = 6
-VECTOR_TERM_BUFS = 8
-PINNED = True
-DRAIN = 4
-FIRST_LOAD_ROUND = 2
-LOADS_PER_ROUND = 2
-FIRST_PIECE_ROUND = 3
-PIECES_PER_ROUND = 1
-FIRST_MATMUL_UNIT_ROUND = 7
+LATE = NS - 1
+TERM_BUFS = 14
+EXIT = 3
+COPY_OUT = 2
+QUANT = 3
+MERGE = 2
+TURN = 1
+ADD_GAP = 3
+ADD_DELAY = 2
+ADDS_FIRST = True
+BACKLOG = 3
+EXITS_FIRST = True
+SPLIT_V = (2, 5)
+H_STEPS = (3, 8, 12, 16)
+M_START = 20
+M_EVERY = 5
+P_START = 10
+MX_BUFS = 4
+STORE_BUFS = 4
+TURNED_BUFS = 2
 
 FLOPS = 2 * B * S * R * OUT + 2 * B * Q * NS * R * DO
 
@@ -63,15 +73,15 @@ def tile_skilledlora_pb_kernel(tc, h, weights, lora_b, out):
         half_pool = ctx.enter_context(tc.tile_pool(name="half_skills", bufs=2 * NS))
         whole_pool = ctx.enter_context(tc.tile_pool(name="whole_skills", bufs=NS))
         stacked_pool = ctx.enter_context(tc.tile_pool(name="stacked", bufs=2))
-        scalar_term_pool = ctx.enter_context(tc.tile_pool(name="scalar_terms", bufs=SCALAR_TERM_BUFS))
-        vector_term_pool = ctx.enter_context(tc.tile_pool(name="vector_terms", bufs=VECTOR_TERM_BUFS))
-        turned_pool = ctx.enter_context(tc.tile_pool(name="turned", bufs=2))
-        mixed_pool = ctx.enter_context(tc.tile_pool(name="mixed", bufs=3))
-        mx_pool = ctx.enter_context(tc.tile_pool(name="mx", bufs=5))
-        store_pool = ctx.enter_context(tc.tile_pool(name="store", bufs=3))
+        term_pool = ctx.enter_context(tc.tile_pool(name="terms", bufs=TERM_BUFS))
+        sum_pool = ctx.enter_context(tc.tile_pool(name="sums", bufs=2))
+        late_pool = ctx.enter_context(tc.tile_pool(name="late", bufs=2))
+        turned_pool = ctx.enter_context(tc.tile_pool(name="turned", bufs=TURNED_BUFS))
+        mixed_pool = ctx.enter_context(tc.tile_pool(name="mixed", bufs=2))
+        mx_pool = ctx.enter_context(tc.tile_pool(name="mx", bufs=MX_BUFS))
+        store_pool = ctx.enter_context(tc.tile_pool(name="store", bufs=STORE_BUFS))
         psum = ctx.enter_context(tc.psum_pool(name="psum", bufs=8))
-        if PINNED:
-            ctx.enter_context(tc.manual_schedule())
+        ctx.enter_context(tc.manual_schedule())
 
         w_bf16 = consts.tile([P, B * Q * NS], BF16)
         nc.scalar.dma_start(
@@ -82,43 +92,38 @@ def tile_skilledlora_pb_kernel(tc, h, weights, lora_b, out):
 
         identity_f32 = consts.tile([P, P], F32)
         make_identity(nc, identity_f32[:])
+        identity_bf16 = consts.tile([P, P], BF16)
+        make_identity(nc, identity_bf16[:])
 
-        is_skill = consts.tile([P, NS], F32)
-        nc.vector.tensor_reduce(
-            out=is_skill[:],
-            in_=identity_f32[:].rearrange("p (k g) -> p k g", k=NS),
-            axis=ALONG_ROW,
-            op=ADD,
-        )
-        is_rank = consts.tile([P, RANKS_PER_MATMUL], F32)
-        nc.vector.tensor_reduce(
-            out=is_rank[:],
-            in_=identity_f32[:].rearrange("p (k g) -> p g k", k=NS),
-            axis=ALONG_ROW,
-            op=ADD,
-        )
-        masked = consts.tile([P, B, MATMUL_SPLITS, NS], F32)
-        nc.vector.tensor_tensor(
-            out=masked[:],
-            in0=w_f32[:].rearrange("p (b q k) -> p b q k", b=B, q=Q)[:, :, FIRST_MATMUL_SPLIT:Q, :],
-            in1=is_skill[:].unsqueeze(1).unsqueeze(1).to_broadcast([P, B, MATMUL_SPLITS, NS]),
-            op=MULT,
-        )
-        own_weight = consts.tile([P, B, MATMUL_SPLITS], F32)
-        nc.vector.tensor_reduce(out=own_weight[:], in_=masked[:], axis=ALONG_ROW, op=ADD)
-        mixers = consts.tile([P, MATMUL_SPLITS, B, RANKS_PER_MATMUL], BF16)
-        nc.vector.tensor_tensor(
-            out=mixers[:],
-            in0=is_rank[:]
-            .unsqueeze(1)
-            .unsqueeze(1)
-            .to_broadcast([P, MATMUL_SPLITS, B, RANKS_PER_MATMUL]),
-            in1=own_weight[:]
-            .rearrange("p b q -> p q b")
-            .unsqueeze(3)
-            .to_broadcast([P, MATMUL_SPLITS, B, RANKS_PER_MATMUL]),
-            op=MULT,
-        )
+        mixers = consts.tile([P, MATMUL_SPLITS, B, RUNS * 2], BF16)
+
+        def make_mixers():
+            by_part = identity_f32[:].rearrange("p (e k g) -> p k e g", e=2, k=NS)
+            is_skill = consts.tile([P, NS], F32)
+            nc.vector.tensor_reduce(out=is_skill[:], in_=by_part, axis=XY, op=ADD)
+            is_rank = consts.tile([P, RUNS, 2], F32)
+            nc.vector.tensor_reduce(
+                out=is_rank[:],
+                in_=identity_f32[:].rearrange("p (e k g) -> p g e k", e=2, k=NS),
+                axis=X,
+                op=ADD,
+            )
+            masked = consts.tile([P, B, MATMUL_SPLITS, NS], F32)
+            nc.vector.tensor_tensor(
+                out=masked[:],
+                in0=w_f32[:].rearrange("p (b q k) -> p b q k", b=B, q=Q)[:, :, FIRST_MATMUL_SPLIT:Q, :],
+                in1=is_skill[:].unsqueeze(1).unsqueeze(1).to_broadcast([P, B, MATMUL_SPLITS, NS]),
+                op=MULT,
+            )
+            own_weight = consts.tile([P, B, MATMUL_SPLITS], F32)
+            nc.vector.tensor_reduce(out=own_weight[:], in_=masked[:], axis=X, op=ADD)
+            shape = [P, MATMUL_SPLITS, B, RUNS * 2]
+            nc.vector.tensor_tensor(
+                out=mixers[:],
+                in0=is_rank[:].rearrange("p g e -> p (g e)").unsqueeze(1).unsqueeze(1).to_broadcast(shape),
+                in1=own_weight[:].rearrange("p b q -> p q b").unsqueeze(3).to_broadcast(shape),
+                op=MULT,
+            )
 
         h_codes = consts.tile([P, B, S], U32, align_bytes=64)
         h_scales = consts.tile([P, B, S], U8, align_bytes=64)
@@ -149,13 +154,14 @@ def tile_skilledlora_pb_kernel(tc, h, weights, lora_b, out):
 
         def load_stacked(g):
             q, c = MATMUL_GROUPS[g]
-            stacked = stacked_pool.tile([P, WORDS_PER_STRIDE, PACK, GROUP], BF16)
-            nc.sync.dma_start(
-                out=stacked[:],
-                in_=lora_b[q].rearrange(
-                    "k (g a t) d -> (k g) a t d", a=WORDS_PER_STRIDE, t=PACK
-                )[:, :, :, c * GROUP : (c + 1) * GROUP],
-            )
+            stacked = stacked_pool.tile([P, PAIRS, GROUP], BF16)
+            for e in range(2):
+                nc.sync.dma_start(
+                    out=stacked[e * (P // 2) : (e + 1) * (P // 2), :, :],
+                    in_=lora_b[q].rearrange("k (g s e) d -> e (k g) s d", g=RUNS, e=2)[
+                        e, :, :, c * GROUP : (c + 1) * GROUP
+                    ],
+                )
             stacked_of[g] = stacked
 
         h_rows_of = {}
@@ -165,101 +171,140 @@ def tile_skilledlora_pb_kernel(tc, h, weights, lora_b, out):
             nc.sync.dma_start(out=h_rows[:], in_=h[b].rearrange("(n p) r -> p n r", p=P))
             h_rows_of[b] = h_rows
 
-        def quantise_h(b, h_rows):
+        agenda = {"tensor": {}, "scalar": {}}
+        vector_queue = []
+
+        def due(engine, step, job):
+            agenda[engine].setdefault(step, []).append(job)
+
+        def for_vector(step, job):
+            vector_queue.append([step, job])
+
+        def turn_h(b, n):
+            h_rows = h_rows_of[b]
             h_grouped = h_grouped_pool.tile([P, S * PACK], BF16, align_bytes=64)
             grouped_words = h_grouped[:].bitcast(F32).rearrange("p (s u) -> p s u", u=HALVES)
             tiles_per_bank = BANK // (HALVES * P)
-            for first in range(0, TOKEN_TILES, tiles_per_bank):
-                turned_h = psum.tile([P, tiles_per_bank, HALVES, P], F32, tag="bank")
-                for n in range(tiles_per_bank):
-                    words = h_rows[:, first + n, :].bitcast(F32).rearrange(
-                        "p (w u) -> p u w", u=HALVES
-                    )
-                    for u in range(HALVES):
-                        nc.tensor.transpose(turned_h[:, n, u, :], words[:, u, :], identity_f32[:])
+
+            def copy_out(turned_h, first):
                 nc.scalar.copy(
                     out=grouped_words[:, first * P : (first + tiles_per_bank) * P, :].rearrange(
                         "p (n s) u -> p n s u", n=tiles_per_bank
                     ),
                     in_=turned_h[:].rearrange("p n u s -> p n s u"),
                 )
-            nc.vector.quantize_mx(
-                out=h_codes[:, b, :].bitcast(FP8X4), scales=h_scales[:, b, :], in_=h_grouped[:]
-            )
 
-        def mix_piece(q, stacked, mixed, j, u):
-            bank = psum.tile([P, MATMULS_PER_BANK, B, RANKS_PER_MATMUL], BF16, tag="bank")
-            for m in range(MATMULS_PER_BANK):
-                a, e = divmod(m, HALVES)
+            for first in range(0, TOKEN_TILES, tiles_per_bank):
+                turned_h = psum.tile([P, tiles_per_bank, HALVES, P], F32, tag="bank")
+                for m in range(tiles_per_bank):
+                    words = h_rows[:, first + m, :].bitcast(F32).rearrange(
+                        "p (w u) -> p u w", u=HALVES
+                    )
+                    for u in range(HALVES):
+                        nc.tensor.transpose(turned_h[:, m, u, :], words[:, u, :], identity_f32[:])
+                due("scalar", n + COPY_OUT, lambda turned_h=turned_h, first=first: copy_out(turned_h, first))
+
+            def quantise_h(step):
+                nc.vector.quantize_mx(
+                    out=h_codes[:, b, :].bitcast(FP8X4), scales=h_scales[:, b, :], in_=h_grouped[:]
+                )
+
+            for_vector(n + COPY_OUT + 1, quantise_h)
+            if b + 2 < B:
+                load_h(b + 2)
+
+        def mix_piece(g, j, u, n):
+            q, c = MATMUL_GROUPS[g]
+            if g not in mixed_of:
+                mixed = mixed_pool.tile([P, BLOCKS, B, R], BF16)
+                mixed_of[g] = mixed
+            mixed = mixed_of[g]
+            bank = psum.tile([P, MATMULS_PER_BANK, FULL], BF16, tag="bank")
+            for a in range(MATMULS_PER_BANK):
                 nc.tensor.matmul(
-                    out=bank[:, m, :, :].rearrange("p b g -> p (b g)"),
-                    lhsT=stacked[:, a, HALVES * u + e, j * P : (j + 1) * P],
+                    out=bank[:, a, :],
+                    lhsT=stacked_of[g][:, HALVES * a + u, j * P : (j + 1) * P],
                     rhs=mixers[:, q - FIRST_MATMUL_SPLIT, :, :].rearrange("p b g -> p (b g)"),
                     start=True,
                     stop=True,
                 )
-            nc.scalar.copy(
-                out=mixed[:, j, :, :].rearrange(
-                    "p b (u g m) -> p b u g m", u=HALVES, m=MATMULS_PER_BANK
-                )[:, :, u, :, :],
-                in_=bank[:].rearrange("p m b g -> p b g m"),
-            )
 
-        def columns_of(unit):
-            q, c, b, first_block, blocks = unit
-            return slice(first_block * P, (first_block + blocks) * P)
+            def copy_out():
+                nc.scalar.copy(
+                    out=mixed[:, j, :, :].bitcast(F32).rearrange(
+                        "p b (u g a) -> p b u g a", u=HALVES, g=RUNS
+                    )[:, :, u, :, :],
+                    in_=bank[:].bitcast(F32).rearrange("p a (b g) -> p b g a", b=B),
+                )
 
-        def scalar_term(unit, k):
-            q, c, b, first_block, blocks = unit
-            term = scalar_term_pool.tile([P, PACK, blocks * P], F32)
-            nc.scalar.activation(
-                out=term[:], in_=skills[(q, c)][k][:, :, columns_of(unit)], func=COPY,
-                scale=weight_of(b, q, k),
-            )
+            due("scalar", n + COPY_OUT, copy_out)
+
+        mixed_of = {}
+
+        def product(engine, unit, k):
+            q, c, b = unit
+            term = term_pool.tile([P, PACK, GROUP], F32)
+            if engine == "scalar":
+                nc.scalar.activation(
+                    out=term[:], in_=skills[(q, c)][k], func=COPY, scale=weight_of(b, q, k)
+                )
+            else:
+                nc.vector.tensor_scalar(
+                    out=term[:], in0=skills[(q, c)][k], scalar1=weight_of(b, q, k), scalar2=None,
+                    op0=MULT,
+                )
             return term
 
-        def vector_products(unit, roles, terms):
-            q, c, b, first_block, blocks = unit
-            for k in range(NS):
-                if roles[k] == "V":
-                    term = vector_term_pool.tile([P, PACK, blocks * P], F32)
-                    nc.vector.tensor_scalar(
-                        out=term[:], in0=skills[(q, c)][k][:, :, columns_of(unit)],
-                        scalar1=weight_of(b, q, k), scalar2=None, op0=MULT,
-                    )
-                    terms.append(term)
+        late_of = {}
 
-        def vector_adds(unit, roles, terms):
-            q, c, b, first_block, blocks = unit
-            onto = 0
-            for k in range(NS):
-                if roles[k] == "A":
-                    nc.vector.scalar_tensor_tensor(
-                        out=terms[onto][:], in0=skills[(q, c)][k][:, :, columns_of(unit)],
-                        scalar=weight_of(b, q, k), in1=terms[onto][:], op0=MULT, op1=ADD,
+        def turn_late(q, c, n):
+            bank = psum.tile([P, BLOCKS, 2, HALVES, P], BF16, tag="bank")
+            for j in range(BLOCKS):
+                for t in range(PACK):
+                    nc.tensor.transpose(
+                        bank[:, j, t % 2, t // 2, :],
+                        skills[(q, c)][LATE][:, t, j * P : (j + 1) * P],
+                        identity_bf16[:],
                     )
-                    onto += 1
+            late = late_pool.tile([P, BLOCKS, HALVES * P, 2], BF16)
+            late_of[(q, c)] = late
 
-        def add_block(terms, j, turned):
-            acc = psum.tile([P, PACK, P], F32, tag="bank")
+            def copy_out():
+                nc.scalar.copy(out=late[:], in_=bank[:].rearrange("d j e u p -> d j (u p) e"))
+
+            due("scalar", n + COPY_OUT, copy_out)
+
+        def add_block(unit, terms, j, turned, n):
+            q, c, b = unit
+            acc = psum.tile([P, 2, HALVES, P], F32, tag="bank")
             for t in range(PACK):
                 for i, term in enumerate(terms):
                     nc.tensor.matmul(
-                        out=acc[:, t, :],
+                        out=acc[:, t % 2, t // 2, :],
                         lhsT=term[:, t, j * P : (j + 1) * P],
                         rhs=identity_f32[:],
                         is_transpose=True,
                         start=(i == 0),
                         stop=(i == len(terms) - 1),
                     )
-            nc.scalar.copy(
-                out=turned[:, j, :].rearrange("d (u p e) -> d u p e", u=HALVES, e=HALVES),
-                in_=acc[:].rearrange("d (u e) p -> d u p e", u=HALVES),
-            )
 
-        def turn_back(blocks):
-            width = len(blocks) * P
-            back = psum.tile([P, HALVES, width], F32, tag="bank")
+            def merge(step):
+                nc.vector.scalar_tensor_tensor(
+                    out=turned[:, j, :].rearrange("d (x e) -> d x e", e=2),
+                    in0=late_of[(q, c)][:, j, :, :],
+                    scalar=weight_of(b, q, LATE),
+                    in1=acc[:].rearrange("d e u p -> d (u p) e"),
+                    op0=MULT,
+                    op1=ADD,
+                )
+                if j == BLOCKS - 1:
+                    due("tensor", step + TURN, lambda m: turn_back(
+                        unit, [turned[:, i, :] for i in range(BLOCKS)], m))
+
+            for_vector(n + MERGE, merge)
+
+        def turn_back(unit, blocks, n):
+            back = psum.tile([P, HALVES, GROUP], F32, tag="bank")
             for j, block in enumerate(blocks):
                 words = block.bitcast(F32)
                 for u in range(HALVES):
@@ -267,33 +312,46 @@ def tile_skilledlora_pb_kernel(tc, h, weights, lora_b, out):
                         back[:, u, j * P : (j + 1) * P], words[:, u * P : (u + 1) * P],
                         identity_f32[:],
                     )
-            grouped = mx_pool.tile([P, width * PACK], BF16, align_bytes=64)
-            nc.scalar.copy(
-                out=grouped[:].bitcast(F32).rearrange("p (d u) -> p d u", u=HALVES),
-                in_=back[:].rearrange("p u d -> p d u"),
-            )
-            return grouped
 
-        def quantise(unit, grouped):
-            width = unit[4] * P
+            def copy_out():
+                grouped = mx_pool.tile([P, GROUP * PACK], BF16, align_bytes=64)
+                nc.scalar.copy(
+                    out=grouped[:].bitcast(F32).rearrange("p (d u) -> p d u", u=HALVES),
+                    in_=back[:].rearrange("p u d -> p d u"),
+                )
+                for_vector(n + QUANT, lambda step: quantise_and_multiply(unit, 0, BLOCKS, grouped, step))
+
+            due("scalar", n + COPY_OUT, copy_out)
+
+        def quantise_and_multiply(unit, first_block, blocks, grouped, n):
+            q, c, b = unit
+            width = blocks * P
             codes = mx_pool.tile([P, width], U32, align_bytes=64)
             scales = mx_pool.tile([P, width], U8, align_bytes=64)
             nc.vector.quantize_mx(out=codes[:].bitcast(FP8X4), scales=scales[:], in_=grouped[:])
-            return codes, scales
-
-        def multiply_and_store(unit, operand):
-            q, c, b, first_block, blocks = unit
-            codes, scales = operand
-            width = blocks * P
             first_column = q * DO + c * GROUP + first_block * P
             tiles_per_bank = BANK // width
             result = store_pool.tile([P, TOKEN_TILES, width], F32)
+
+            def leave(product_bank, first):
+                nc.scalar.activation(
+                    out=result[:, first : first + tiles_per_bank, :], in_=product_bank[:],
+                    func=COPY, scale=SCALING,
+                )
+                if first + tiles_per_bank == TOKEN_TILES:
+                    nc.sync.dma_start(
+                        out=out[b, :, first_column : first_column + width].rearrange(
+                            "(n p) d -> p n d", p=P
+                        ),
+                        in_=result[:],
+                    )
+
             for first in range(0, TOKEN_TILES, tiles_per_bank):
-                product = psum.tile([P, tiles_per_bank, width], F32, tag="bank")
-                for n in range(tiles_per_bank):
-                    tokens = slice((first + n) * P, (first + n + 1) * P)
+                product_bank = psum.tile([P, tiles_per_bank, width], F32, tag="bank")
+                for m in range(tiles_per_bank):
+                    tokens = slice((first + m) * P, (first + m + 1) * P)
                     nc.tensor.matmul_mx(
-                        out=product[:, n, :],
+                        out=product_bank[:, m, :],
                         lhsT=h_codes[:, b, tokens].bitcast(FP8X4),
                         lhsT_scale=h_scales[:, b, tokens],
                         rhs=codes[:].bitcast(FP8X4),
@@ -301,128 +359,132 @@ def tile_skilledlora_pb_kernel(tc, h, weights, lora_b, out):
                         start=True,
                         stop=True,
                     )
-                nc.scalar.activation(
-                    out=result[:, first : first + tiles_per_bank, :], in_=product[:], func=COPY,
-                    scale=SCALING,
-                )
-            nc.sync.dma_start(
-                out=out[b, :, first_column : first_column + width].rearrange(
-                    "(n p) d -> p n d", p=P
-                ),
-                in_=result[:],
-            )
+                due("scalar", n + EXIT, lambda bank=product_bank, first=first: leave(bank, first))
 
-        whole_units = [
-            (q, c, b, 0, BLOCKS)
-            for q in range(Q)
-            for c in range(GROUPS_PER_SPLIT)
-            if (q, c) not in MATMUL_GROUPS
-            for b in range(B)
-        ]
-        summed_units = whole_units[: len(whole_units) - HALVED_UNITS] + [
-            (q, c, b, j, 1)
-            for (q, c, b, first_block, blocks) in whole_units[len(whole_units) - HALVED_UNITS :]
-            for j in range(BLOCKS)
-        ]
-        matmul_units = [(q, c, b, 0, BLOCKS) for (q, c) in MATMUL_GROUPS for b in range(B)]
+        turned_units = (
+            [(0, 0, b) for b in range(B)] + [(1, 0, b) for b in range(B)] + [(2, 0, 0), (2, 0, 1)]
+        )
+        straight_units = (
+            [(0, 1, b) for b in range(B)] + [(1, 1, b) for b in range(B)] + [(2, 0, 2), (2, 0, 3)]
+        )
+        matmul_units = [(q, c, b) for (q, c) in MATMUL_GROUPS for b in range(B)]
         pieces = [
             (g, j, u)
             for g in range(len(MATMUL_GROUPS))
             for j in range(BLOCKS)
             for u in range(HALVES)
         ]
+        steps = len(straight_units) * NS
 
         for k in range(NS):
             load_half_skill(0, 0, k)
-        load_h(0)
-        load_h(1)
-        for k in range(NS):
+        for k in range(NS // 2):
             load_half_skill(0, 1, k)
+        load_h(0)
+        for k in range(NS // 2, NS):
+            load_half_skill(0, 1, k)
+        load_h(1)
         load_stacked(0)
         later_loads = (
-            [("whole", 1, k) for k in range(NS // 2)]
-            + [("stacked", 1, 0)]
-            + [("whole", 1, k) for k in range(NS // 2, NS)]
-            + [("stacked", 2, 0)]
-            + [("half", 2, k) for k in range(NS)]
+            [lambda k=k: load_whole_skill(1, k) for k in range(NS)]
+            + [lambda: load_stacked(1)]
+            + [lambda: load_stacked(2)]
+            + [lambda k=k: load_half_skill(2, 0, k) for k in range(NS)]
         )
-        loads_done = 0
-        mixed_of = {}
-        PIECES_PER_GROUP = len(pieces) // len(MATMUL_GROUPS)
+        load_steps = (
+            [6 + k for k in range(NS)] + [16, 30] + [36 + k for k in range(NS)]
+        )
 
-        rounds = len(summed_units)
+        for b in range(B):
+            due("tensor", H_STEPS[b], lambda n, b=b: turn_h(b, n))
+        for i, (g, j, u) in enumerate(pieces):
+            step = P_START + 2 * i if i < PACK else M_START + 1 + M_EVERY * (i - PACK)
+            due("tensor", step, lambda n, g=g, j=j, u=u: mix_piece(g, j, u, n))
+        for i, unit in enumerate(matmul_units):
+            g = i // B
+            due("tensor", M_START + M_EVERY * i, lambda n, g=g, unit=unit: turn_back(
+                unit, [mixed_of[g][:, j, unit[2], :] for j in range(BLOCKS)], n))
 
-        def roles_of(i):
-            return ROLES_IN_TURN[i % len(ROLES_IN_TURN)]
+        def vector_makes(i, k):
+            if i == 0:
+                return k % 2 == 1
+            return i > 2 and k in SPLIT_V
 
-        def scalar_skills(i):
-            return [k for k in range(NS) if roles_of(i)[k] == "S"]
+        terms = []
+        for k in range(NS - 1):
+            terms.append(product("vector" if vector_makes(0, k) else "scalar", turned_units[0], k))
+        make_mixers()
 
-        terms_of = {0: [scalar_term(summed_units[0], k) for k in scalar_skills(0)]}
-        to_turn = []
-        to_quantise = []
-        to_multiply = []
-        pieces_done = 0
-        matmul_units_done = 0
+        def due_adds(i, terms, n):
+            unit = turned_units[i]
+            turned = turned_pool.tile([P, BLOCKS, R], BF16)
+            for j in range(BLOCKS):
+                due("tensor", n + ADD_GAP * j, lambda m, j=j: add_block(unit, terms, j, turned, m))
 
-        for i in range(rounds + DRAIN):
-            if i < rounds:
-                vector_products(summed_units[i], roles_of(i), terms_of[i])
-            if i < rounds:
-                vector_adds(summed_units[i], roles_of(i), terms_of[i])
-            quantised = [(unit, quantise(unit, grouped)) for unit, grouped in to_quantise]
-            to_quantise = []
-            fillers = scalar_skills(i + 1) if i + 1 < rounds else []
-            filled = 0
-            if i + 1 < rounds:
-                terms_of[i + 1] = []
-            if 1 <= i <= rounds:
-                unit = summed_units[i - 1]
-                turned = turned_pool.tile([P, unit[4], R], BF16)
-                for j in range(unit[4]):
-                    if filled < len(fillers):
-                        terms_of[i + 1].append(scalar_term(summed_units[i + 1], fillers[filled]))
-                        filled += 1
-                    add_block(terms_of[i - 1], j, turned)
-                to_turn.append((unit, [turned[:, j, :] for j in range(unit[4])]))
-            for k in fillers[filled:]:
-                terms_of[i + 1].append(scalar_term(summed_units[i + 1], k))
-            if 1 <= i <= B:
-                quantise_h(i - 1, h_rows_of[i - 1])
-                if i + 1 < B:
-                    load_h(i + 1)
-            for unit, operand in to_multiply:
-                multiply_and_store(unit, operand)
-            to_multiply = quantised
-            if i >= FIRST_MATMUL_UNIT_ROUND and matmul_units_done < len(matmul_units):
-                unit = matmul_units[matmul_units_done]
-                g = MATMUL_GROUPS.index((unit[0], unit[1]))
-                assert pieces_done >= (g + 1) * PIECES_PER_GROUP
-                to_turn.append((unit, [mixed_of[g][:, j, unit[2], :] for j in range(BLOCKS)]))
-                matmul_units_done += 1
-            for unit, blocks in to_turn:
-                to_quantise.append((unit, turn_back(blocks)))
-            to_turn = []
-            if i >= FIRST_PIECE_ROUND:
-                for n in range(PIECES_PER_ROUND):
-                    if pieces_done < len(pieces):
-                        g, j, u = pieces[pieces_done]
-                        if g not in mixed_of:
-                            mixed = mixed_pool.tile([P, BLOCKS, B, R], BF16)
-                            mixed_of[g] = mixed
-                        mix_piece(MATMUL_GROUPS[g][0], stacked_of[g], mixed_of[g], j, u)
-                        pieces_done += 1
-            if i >= FIRST_LOAD_ROUND:
-                for n in range(LOADS_PER_ROUND):
-                    if loads_done < len(later_loads):
-                        kind, which, k = later_loads[loads_done]
-                        if kind == "whole":
-                            load_whole_skill(which, k)
-                        elif kind == "half":
-                            assert i >= B - 1
-                            load_half_skill(which, 0, k)
-                        else:
-                            assert pieces_done >= (which - 1) * PIECES_PER_GROUP
-                            load_stacked(which)
-                        loads_done += 1
-        assert matmul_units_done == len(matmul_units) and not to_quantise and not to_multiply
+        due("tensor", 0, lambda n: turn_late(0, 0, n))
+        due_adds(0, terms, 0)
+
+        state = {}
+        n = 0
+        while n < steps or vector_queue or any(
+            step >= n for jobs in agenda.values() for step in jobs
+        ):
+            i, k = divmod(n, NS)
+            if n < steps:
+                unit = straight_units[i]
+                q, c, b = unit
+                skill = skills[(q, c)][k]
+                if k == 0:
+                    total = sum_pool.tile([P, PACK, GROUP], F32)
+                    state["sum"] = total
+                    nc.vector.tensor_scalar(
+                        out=total[:], in0=skill, scalar1=weight_of(b, q, k), scalar2=None, op0=MULT
+                    )
+                elif k < NS - 1:
+                    total = state["sum"]
+                    nc.vector.scalar_tensor_tensor(
+                        out=total[:], in0=skill, scalar=weight_of(b, q, k), in1=total[:],
+                        op0=MULT, op1=ADD,
+                    )
+                else:
+                    total = state["sum"]
+                    grouped = mx_pool.tile([P, GROUP * PACK], BF16, align_bytes=64)
+                    nc.vector.scalar_tensor_tensor(
+                        out=grouped[:].rearrange("p (d t) -> p d t", t=PACK),
+                        in0=skill.rearrange("p t d -> p d t"),
+                        scalar=weight_of(b, q, k),
+                        in1=total[:].rearrange("p t d -> p d t"),
+                        op0=MULT, op1=ADD,
+                    )
+                    for_vector(n + 1, lambda step, unit=unit, grouped=grouped:
+                               quantise_and_multiply(unit, 0, BLOCKS, grouped, step))
+            if EXITS_FIRST:
+                for job in agenda["scalar"].get(n, []):
+                    job()
+            if n < steps and i + 1 < len(turned_units) and k < NS - 1:
+                if k == 0:
+                    state["terms"] = []
+                unit = turned_units[i + 1]
+                engine = "vector" if vector_makes(i + 1, k) else "scalar"
+                state["terms"].append(product(engine, unit, k))
+                if k == NS - 2:
+                    if unit[:2] not in late_of:
+                        due("tensor", n + 1, lambda m, unit=unit: turn_late(unit[0], unit[1], m))
+                    due_adds(i + 1, state["terms"], n + ADD_DELAY)
+            if not EXITS_FIRST:
+                for job in agenda["scalar"].get(n, []):
+                    job()
+            if ADDS_FIRST:
+                for job in agenda["tensor"].get(n, []):
+                    job(n)
+            ready = [entry for entry in vector_queue if entry[0] <= n]
+            for entry in ready[: 1 if len(ready) < BACKLOG else 2]:
+                vector_queue.remove(entry)
+                entry[1](n)
+            if not ADDS_FIRST:
+                for job in agenda["tensor"].get(n, []):
+                    job(n)
+            for load_step, load in zip(load_steps, later_loads):
+                if load_step == n:
+                    load()
+            n += 1

@@ -41,10 +41,10 @@ MIXING_MATMULS = len(MATMUL_GROUPS) * BLOCKS * PAIRS
 assert MIXING_MATMULS * P * P * FULL * 10 < B * S * R * OUT
 
 LATE = NS - 1
-TERM_BUFS = 14
+TERM_BUFS = 13
 EXIT = 3
 COPY_OUT = 2
-QUANT = 3
+QUANT = 2
 MERGE = 2
 TURN = 1
 ADD_GAP = 3
@@ -52,14 +52,22 @@ ADD_DELAY = 2
 ADDS_FIRST = True
 BACKLOG = 3
 EXITS_FIRST = True
-SPLIT_V = (2, 5)
-H_STEPS = (3, 8, 12, 16)
+H_STEPS = (6, 10, 14, 18)
 M_START = 20
 M_EVERY = 5
 P_START = 10
 MX_BUFS = 4
 STORE_BUFS = 4
 TURNED_BUFS = 2
+NT = 10
+EARLY = 12
+S_STEPS = (0, 1, 3, 4, 6)
+V_STEPS = (2, 5, 7)
+REGROUP = 1
+QUANT_S = 2
+HALF_STEPS = 36
+WHOLE_STEP = 6
+STACK_STEPS = (16, 30)
 
 FLOPS = 2 * B * S * R * OUT + 2 * B * Q * NS * R * DO
 
@@ -75,6 +83,7 @@ def tile_skilledlora_pb_kernel(tc, h, weights, lora_b, out):
         stacked_pool = ctx.enter_context(tc.tile_pool(name="stacked", bufs=2))
         term_pool = ctx.enter_context(tc.tile_pool(name="terms", bufs=TERM_BUFS))
         sum_pool = ctx.enter_context(tc.tile_pool(name="sums", bufs=2))
+        rounded_pool = ctx.enter_context(tc.tile_pool(name="rounded", bufs=2))
         late_pool = ctx.enter_context(tc.tile_pool(name="late", bufs=2))
         turned_pool = ctx.enter_context(tc.tile_pool(name="turned", bufs=TURNED_BUFS))
         mixed_pool = ctx.enter_context(tc.tile_pool(name="mixed", bufs=2))
@@ -323,6 +332,14 @@ def tile_skilledlora_pb_kernel(tc, h, weights, lora_b, out):
 
             due("scalar", n + COPY_OUT, copy_out)
 
+        def regroup(unit, rounded, n):
+            grouped = mx_pool.tile([P, GROUP * PACK], BF16, align_bytes=64)
+            nc.vector.tensor_copy(
+                out=grouped[:].rearrange("p (d t) -> p d t", t=PACK),
+                in_=rounded[:].rearrange("p t d -> p d t"),
+            )
+            for_vector(n + QUANT_S, lambda step: quantise_and_multiply(unit, 0, BLOCKS, grouped, step))
+
         def quantise_and_multiply(unit, first_block, blocks, grouped, n):
             q, c, b = unit
             width = blocks * P
@@ -361,11 +378,12 @@ def tile_skilledlora_pb_kernel(tc, h, weights, lora_b, out):
                     )
                 due("scalar", n + EXIT, lambda bank=product_bank, first=first: leave(bank, first))
 
+        last_group = [(2, 0, b) for b in range(B)]
         turned_units = (
-            [(0, 0, b) for b in range(B)] + [(1, 0, b) for b in range(B)] + [(2, 0, 0), (2, 0, 1)]
+            [(0, 0, b) for b in range(B)] + [(1, 0, b) for b in range(B)] + last_group[: NT - 2 * B]
         )
         straight_units = (
-            [(0, 1, b) for b in range(B)] + [(1, 1, b) for b in range(B)] + [(2, 0, 2), (2, 0, 3)]
+            [(0, 1, b) for b in range(B)] + [(1, 1, b) for b in range(B)] + last_group[NT - 2 * B :]
         )
         matmul_units = [(q, c, b) for (q, c) in MATMUL_GROUPS for b in range(B)]
         pieces = [
@@ -377,12 +395,9 @@ def tile_skilledlora_pb_kernel(tc, h, weights, lora_b, out):
         steps = len(straight_units) * NS
 
         for k in range(NS):
+            load_half_skill(0, 1, k)
             load_half_skill(0, 0, k)
-        for k in range(NS // 2):
-            load_half_skill(0, 1, k)
         load_h(0)
-        for k in range(NS // 2, NS):
-            load_half_skill(0, 1, k)
         load_h(1)
         load_stacked(0)
         later_loads = (
@@ -392,7 +407,7 @@ def tile_skilledlora_pb_kernel(tc, h, weights, lora_b, out):
             + [lambda k=k: load_half_skill(2, 0, k) for k in range(NS)]
         )
         load_steps = (
-            [6 + k for k in range(NS)] + [16, 30] + [36 + k for k in range(NS)]
+            [WHOLE_STEP + k for k in range(NS)] + list(STACK_STEPS) + [HALF_STEPS + k for k in range(NS)]
         )
 
         for b in range(B):
@@ -405,15 +420,8 @@ def tile_skilledlora_pb_kernel(tc, h, weights, lora_b, out):
             due("tensor", M_START + M_EVERY * i, lambda n, g=g, unit=unit: turn_back(
                 unit, [mixed_of[g][:, j, unit[2], :] for j in range(BLOCKS)], n))
 
-        def vector_makes(i, k):
-            if i == 0:
-                return k % 2 == 1
-            return i > 2 and k in SPLIT_V
+        stream = [(i, k) for i in range(len(turned_units)) for k in range(NS - 1)]
 
-        terms = []
-        for k in range(NS - 1):
-            terms.append(product("vector" if vector_makes(0, k) else "scalar", turned_units[0], k))
-        make_mixers()
 
         def due_adds(i, terms, n):
             unit = turned_units[i]
@@ -421,10 +429,22 @@ def tile_skilledlora_pb_kernel(tc, h, weights, lora_b, out):
             for j in range(BLOCKS):
                 due("tensor", n + ADD_GAP * j, lambda m, j=j: add_block(unit, terms, j, turned, m))
 
-        due("tensor", 0, lambda n: turn_late(0, 0, n))
-        due_adds(0, terms, 0)
+        state = {"made": 0}
 
-        state = {}
+        def next_product(engine, n):
+            if state["made"] == len(stream):
+                return
+            i, k = stream[state["made"]]
+            state["made"] += 1
+            unit = turned_units[i]
+            if k == 0:
+                state["terms"] = []
+            state["terms"].append(product(engine, unit, k))
+            if k == NS - 2:
+                if unit[:2] not in late_of:
+                    due("tensor", n + 1, lambda m: turn_late(unit[0], unit[1], m))
+                due_adds(i, state["terms"], n + ADD_DELAY)
+
         n = 0
         while n < steps or vector_queue or any(
             step >= n for jobs in agenda.values() for step in jobs
@@ -448,29 +468,22 @@ def tile_skilledlora_pb_kernel(tc, h, weights, lora_b, out):
                     )
                 else:
                     total = state["sum"]
-                    grouped = mx_pool.tile([P, GROUP * PACK], BF16, align_bytes=64)
+                    rounded = rounded_pool.tile([P, PACK, GROUP], BF16)
                     nc.vector.scalar_tensor_tensor(
-                        out=grouped[:].rearrange("p (d t) -> p d t", t=PACK),
-                        in0=skill.rearrange("p t d -> p d t"),
-                        scalar=weight_of(b, q, k),
-                        in1=total[:].rearrange("p t d -> p d t"),
+                        out=rounded[:], in0=skill, scalar=weight_of(b, q, k), in1=total[:],
                         op0=MULT, op1=ADD,
                     )
-                    for_vector(n + 1, lambda step, unit=unit, grouped=grouped:
-                               quantise_and_multiply(unit, 0, BLOCKS, grouped, step))
+                    for_vector(n + REGROUP, lambda step, unit=unit, rounded=rounded:
+                               regroup(unit, rounded, step))
             if EXITS_FIRST:
                 for job in agenda["scalar"].get(n, []):
                     job()
-            if n < steps and i + 1 < len(turned_units) and k < NS - 1:
-                if k == 0:
-                    state["terms"] = []
-                unit = turned_units[i + 1]
-                engine = "vector" if vector_makes(i + 1, k) else "scalar"
-                state["terms"].append(product(engine, unit, k))
-                if k == NS - 2:
-                    if unit[:2] not in late_of:
-                        due("tensor", n + 1, lambda m, unit=unit: turn_late(unit[0], unit[1], m))
-                    due_adds(i + 1, state["terms"], n + ADD_DELAY)
+            if n < EARLY or k in S_STEPS:
+                next_product("scalar", n)
+            if n >= EARLY and k in V_STEPS:
+                next_product("vector", n)
+            if n == 1:
+                make_mixers()
             if not EXITS_FIRST:
                 for job in agenda["scalar"].get(n, []):
                     job()

@@ -41,31 +41,34 @@ MIXING_MATMULS = len(MATMUL_GROUPS) * BLOCKS * PAIRS
 assert MIXING_MATMULS * P * P * FULL * 10 < B * S * R * OUT
 
 LATE = NS - 1
-TERM_BUFS = 13
+TERM_BUFS = 11
 EXIT = 3
-COPY_OUT = 2
-QUANT = 2
-MERGE = 2
+COPY_OUT = 1
+QUANT = 6
+MERGE = 4
 TURN = 1
-ADD_GAP = 3
+ADD_GAP = 2
 ADD_DELAY = 2
 ADDS_FIRST = True
 BACKLOG = 3
 EXITS_FIRST = True
 H_STEPS = (6, 10, 14, 18)
-M_START = 20
-M_EVERY = 5
+M_START = 24
+M_EVERY = 5.5
 P_START = 10
 MX_BUFS = 4
 STORE_BUFS = 4
 TURNED_BUFS = 2
 NT = 10
-EARLY = 12
+EARLY = 6
 S_STEPS = (0, 1, 3, 4, 6)
-V_STEPS = (2, 5, 7)
+V_STEPS = ()
 REGROUP = 1
-QUANT_S = 2
-HALF_STEPS = 36
+STRIDED = True
+NTURN = 8
+SCALAR_REGROUPS = 0
+QUANT_S = 3
+HALF_STEPS = 44
 WHOLE_STEP = 6
 STACK_STEPS = (16, 30)
 
@@ -82,7 +85,7 @@ def tile_skilledlora_pb_kernel(tc, h, weights, lora_b, out):
         whole_pool = ctx.enter_context(tc.tile_pool(name="whole_skills", bufs=NS))
         stacked_pool = ctx.enter_context(tc.tile_pool(name="stacked", bufs=2))
         term_pool = ctx.enter_context(tc.tile_pool(name="terms", bufs=TERM_BUFS))
-        sum_pool = ctx.enter_context(tc.tile_pool(name="sums", bufs=2))
+        sum_pool = ctx.enter_context(tc.tile_pool(name="sums", bufs=4))
         rounded_pool = ctx.enter_context(tc.tile_pool(name="rounded", bufs=2))
         late_pool = ctx.enter_context(tc.tile_pool(name="late", bufs=2))
         turned_pool = ctx.enter_context(tc.tile_pool(name="turned", bufs=TURNED_BUFS))
@@ -283,10 +286,15 @@ def tile_skilledlora_pb_kernel(tc, h, weights, lora_b, out):
 
             due("scalar", n + COPY_OUT, copy_out)
 
-        def add_block(unit, terms, j, turned, n):
+        accs = {}
+
+        def add_block(unit, terms, j, u, turned, n):
             q, c, b = unit
-            acc = psum.tile([P, 2, HALVES, P], F32, tag="bank")
-            for t in range(PACK):
+            if u == 0:
+                acc = psum.tile([P, 2, HALVES, P], F32, tag="bank")
+                accs[j] = acc
+            acc = accs[j]
+            for t in range(2 * u, 2 * u + 2):
                 for i, term in enumerate(terms):
                     nc.tensor.matmul(
                         out=acc[:, t % 2, t // 2, :],
@@ -310,7 +318,8 @@ def tile_skilledlora_pb_kernel(tc, h, weights, lora_b, out):
                     due("tensor", step + TURN, lambda m: turn_back(
                         unit, [turned[:, i, :] for i in range(BLOCKS)], m))
 
-            for_vector(n + MERGE, merge)
+            if u == HALVES - 1:
+                for_vector(n + MERGE, merge)
 
         def turn_back(unit, blocks, n):
             back = psum.tile([P, HALVES, GROUP], F32, tag="bank")
@@ -332,9 +341,9 @@ def tile_skilledlora_pb_kernel(tc, h, weights, lora_b, out):
 
             due("scalar", n + COPY_OUT, copy_out)
 
-        def regroup(unit, rounded, n):
+        def regroup(copy, unit, rounded, n):
             grouped = mx_pool.tile([P, GROUP * PACK], BF16, align_bytes=64)
-            nc.vector.tensor_copy(
+            copy(
                 out=grouped[:].rearrange("p (d t) -> p d t", t=PACK),
                 in_=rounded[:].rearrange("p t d -> p d t"),
             )
@@ -378,13 +387,13 @@ def tile_skilledlora_pb_kernel(tc, h, weights, lora_b, out):
                     )
                 due("scalar", n + EXIT, lambda bank=product_bank, first=first: leave(bank, first))
 
-        last_group = [(2, 0, b) for b in range(B)]
-        turned_units = (
-            [(0, 0, b) for b in range(B)] + [(1, 0, b) for b in range(B)] + last_group[: NT - 2 * B]
-        )
-        straight_units = (
-            [(0, 1, b) for b in range(B)] + [(1, 1, b) for b in range(B)] + last_group[NT - 2 * B :]
-        )
+        groups = [(q, c, b) for q, c in ((0, 0), (1, 0), (0, 1), (1, 1), (2, 0)) for b in range(B)]
+        if NTURN >= 8:
+            turned_units = groups[:8]
+            straight_units = groups[8:]
+        else:
+            turned_units = groups[:NTURN]
+            straight_units = groups[8:12] + groups[NTURN:8] + groups[12:]
         matmul_units = [(q, c, b) for (q, c) in MATMUL_GROUPS for b in range(B)]
         pieces = [
             (g, j, u)
@@ -413,11 +422,11 @@ def tile_skilledlora_pb_kernel(tc, h, weights, lora_b, out):
         for b in range(B):
             due("tensor", H_STEPS[b], lambda n, b=b: turn_h(b, n))
         for i, (g, j, u) in enumerate(pieces):
-            step = P_START + 2 * i if i < PACK else M_START + 1 + M_EVERY * (i - PACK)
+            step = P_START + 2 * i if i < PACK else int(M_START + 1 + M_EVERY * (i - PACK))
             due("tensor", step, lambda n, g=g, j=j, u=u: mix_piece(g, j, u, n))
         for i, unit in enumerate(matmul_units):
             g = i // B
-            due("tensor", M_START + M_EVERY * i, lambda n, g=g, unit=unit: turn_back(
+            due("tensor", int(M_START + M_EVERY * i), lambda n, g=g, unit=unit: turn_back(
                 unit, [mixed_of[g][:, j, unit[2], :] for j in range(BLOCKS)], n))
 
         stream = [(i, k) for i in range(len(turned_units)) for k in range(NS - 1)]
@@ -427,9 +436,12 @@ def tile_skilledlora_pb_kernel(tc, h, weights, lora_b, out):
             unit = turned_units[i]
             turned = turned_pool.tile([P, BLOCKS, R], BF16)
             for j in range(BLOCKS):
-                due("tensor", n + ADD_GAP * j, lambda m, j=j: add_block(unit, terms, j, turned, m))
+                for u in range(HALVES):
+                    due("tensor", n + ADD_GAP * (HALVES * j + u), lambda m, j=j, u=u:
+                        add_block(unit, terms, j, u, turned, m))
 
         state = {"made": 0}
+        sums = {}
 
         def next_product(engine, n):
             if state["made"] == len(stream):
@@ -449,38 +461,54 @@ def tile_skilledlora_pb_kernel(tc, h, weights, lora_b, out):
         while n < steps or vector_queue or any(
             step >= n for jobs in agenda.values() for step in jobs
         ):
-            i, k = divmod(n, NS)
+            pair, k, member = n // (2 * NS), n // 2 % NS, n % 2
             if n < steps:
-                unit = straight_units[i]
+                unit = straight_units[2 * pair + member]
                 q, c, b = unit
                 skill = skills[(q, c)][k]
                 if k == 0:
                     total = sum_pool.tile([P, PACK, GROUP], F32)
-                    state["sum"] = total
+                    sums[member] = total
                     nc.vector.tensor_scalar(
                         out=total[:], in0=skill, scalar1=weight_of(b, q, k), scalar2=None, op0=MULT
                     )
                 elif k < NS - 1:
-                    total = state["sum"]
+                    total = sums[member]
                     nc.vector.scalar_tensor_tensor(
                         out=total[:], in0=skill, scalar=weight_of(b, q, k), in1=total[:],
                         op0=MULT, op1=ADD,
                     )
+                elif STRIDED:
+                    total = sums[member]
+                    grouped = mx_pool.tile([P, GROUP * PACK], BF16, align_bytes=64)
+                    nc.vector.scalar_tensor_tensor(
+                        out=grouped[:].rearrange("p (d t) -> p d t", t=PACK),
+                        in0=skill.rearrange("p t d -> p d t"),
+                        scalar=weight_of(b, q, k),
+                        in1=total[:].rearrange("p t d -> p d t"),
+                        op0=MULT, op1=ADD,
+                    )
+                    for_vector(n + QUANT_S, lambda step, unit=unit, grouped=grouped:
+                               quantise_and_multiply(unit, 0, BLOCKS, grouped, step))
                 else:
-                    total = state["sum"]
+                    total = sums[member]
                     rounded = rounded_pool.tile([P, PACK, GROUP], BF16)
                     nc.vector.scalar_tensor_tensor(
                         out=rounded[:], in0=skill, scalar=weight_of(b, q, k), in1=total[:],
                         op0=MULT, op1=ADD,
                     )
-                    for_vector(n + REGROUP, lambda step, unit=unit, rounded=rounded:
-                               regroup(unit, rounded, step))
+                    if member < SCALAR_REGROUPS:
+                        due("scalar", n + REGROUP, lambda unit=unit, rounded=rounded, n=n:
+                            regroup(nc.scalar.copy, unit, rounded, n + REGROUP))
+                    else:
+                        for_vector(n + REGROUP, lambda step, unit=unit, rounded=rounded:
+                                   regroup(nc.vector.tensor_copy, unit, rounded, step))
             if EXITS_FIRST:
                 for job in agenda["scalar"].get(n, []):
                     job()
-            if n < EARLY or k in S_STEPS:
+            if n < EARLY or n % 8 in S_STEPS:
                 next_product("scalar", n)
-            if n >= EARLY and k in V_STEPS:
+            if n >= EARLY and n % 8 in V_STEPS:
                 next_product("vector", n)
             if n == 1:
                 make_mixers()

@@ -12,7 +12,6 @@ MULT = mybir.AluOpType.mult
 ADD = mybir.AluOpType.add
 COPY = mybir.ActivationFunctionType.Copy
 X = mybir.AxisListType.X
-XY = mybir.AxisListType.XY
 
 B, S, R, OUT, Q, NS = 4, 512, 512, 2048, 4, 8
 DO = OUT // Q
@@ -43,19 +42,19 @@ assert MIXING_MATMULS * P * P * FULL * 10 < B * S * R * OUT
 LATE = NS - 1
 TERM_BUFS = 11
 EXIT = 3
-COPY_OUT = 1
+COPY_OUT = 2
 QUANT = 6
-MERGE = 4
-TURN = 1
+MERGE = 5
+TURN = 2
 ADD_GAP = 2
 ADD_DELAY = 2
 ADDS_FIRST = True
 BACKLOG = 3
 EXITS_FIRST = True
 H_STEPS = (6, 10, 14, 18)
-M_START = 24
+M_START = 28
 M_EVERY = 5.5
-P_START = 10
+P_START = 14
 MX_BUFS = 4
 STORE_BUFS = 4
 TURNED_BUFS = 2
@@ -69,8 +68,8 @@ NTURN = 8
 SCALAR_REGROUPS = 0
 QUANT_S = 3
 HALF_STEPS = 44
-WHOLE_STEP = 6
-STACK_STEPS = (16, 30)
+WHOLE_STEP = 8
+STACK_STEPS = (12, 30)
 
 FLOPS = 2 * B * S * R * OUT + 2 * B * Q * NS * R * DO
 
@@ -81,8 +80,7 @@ def tile_skilledlora_pb_kernel(tc, h, weights, lora_b, out):
         consts = ctx.enter_context(tc.tile_pool(name="consts", bufs=1))
         h_pool = ctx.enter_context(tc.tile_pool(name="h_rows", bufs=2))
         h_grouped_pool = ctx.enter_context(tc.tile_pool(name="h_grouped", bufs=1))
-        half_pool = ctx.enter_context(tc.tile_pool(name="half_skills", bufs=2 * NS))
-        whole_pool = ctx.enter_context(tc.tile_pool(name="whole_skills", bufs=NS))
+        whole_pool = ctx.enter_context(tc.tile_pool(name="whole_skills", bufs=2 * NS))
         stacked_pool = ctx.enter_context(tc.tile_pool(name="stacked", bufs=2))
         term_pool = ctx.enter_context(tc.tile_pool(name="terms", bufs=TERM_BUFS))
         sum_pool = ctx.enter_context(tc.tile_pool(name="sums", bufs=4))
@@ -110,13 +108,13 @@ def tile_skilledlora_pb_kernel(tc, h, weights, lora_b, out):
         mixers = consts.tile([P, MATMUL_SPLITS, B, RUNS * 2], BF16)
 
         def make_mixers():
-            by_part = identity_f32[:].rearrange("p (e k g) -> p k e g", e=2, k=NS)
+            by_part = identity_f32[:].rearrange("p (k g) -> p k g", k=NS)
             is_skill = consts.tile([P, NS], F32)
-            nc.vector.tensor_reduce(out=is_skill[:], in_=by_part, axis=XY, op=ADD)
-            is_rank = consts.tile([P, RUNS, 2], F32)
+            nc.vector.tensor_reduce(out=is_skill[:], in_=by_part, axis=X, op=ADD)
+            is_rank = consts.tile([P, RUNS * 2], F32)
             nc.vector.tensor_reduce(
                 out=is_rank[:],
-                in_=identity_f32[:].rearrange("p (e k g) -> p g e k", e=2, k=NS),
+                in_=identity_f32[:].rearrange("p (k g) -> p g k", k=NS),
                 axis=X,
                 op=ADD,
             )
@@ -132,7 +130,7 @@ def tile_skilledlora_pb_kernel(tc, h, weights, lora_b, out):
             shape = [P, MATMUL_SPLITS, B, RUNS * 2]
             nc.vector.tensor_tensor(
                 out=mixers[:],
-                in0=is_rank[:].rearrange("p g e -> p (g e)").unsqueeze(1).unsqueeze(1).to_broadcast(shape),
+                in0=is_rank[:].unsqueeze(1).unsqueeze(1).to_broadcast(shape),
                 in1=own_weight[:].rearrange("p b q -> p q b").unsqueeze(3).to_broadcast(shape),
                 op=MULT,
             )
@@ -147,7 +145,7 @@ def tile_skilledlora_pb_kernel(tc, h, weights, lora_b, out):
         skills = {}
 
         def load_half_skill(q, c, k):
-            half = half_pool.tile([P, PACK, GROUP], BF16)
+            half = whole_pool.tile([P, PACK, GROUP], BF16, tag="whole")
             nc.sync.dma_start(
                 out=half[:],
                 in_=lora_b[q, k].rearrange("(p t) d -> p t d", t=PACK)[
@@ -157,7 +155,7 @@ def tile_skilledlora_pb_kernel(tc, h, weights, lora_b, out):
             skills.setdefault((q, c), []).append(half[:])
 
         def load_whole_skill(q, k):
-            whole = whole_pool.tile([P, PACK, DO], BF16)
+            whole = whole_pool.tile([P, PACK, DO], BF16, tag="whole")
             nc.sync.dma_start(out=whole[:], in_=lora_b[q, k].rearrange("(p t) d -> p t d", t=PACK))
             for c in range(GROUPS_PER_SPLIT):
                 skills.setdefault((q, c), []).append(whole[:, :, c * GROUP : (c + 1) * GROUP])
@@ -169,7 +167,7 @@ def tile_skilledlora_pb_kernel(tc, h, weights, lora_b, out):
             stacked = stacked_pool.tile([P, PAIRS, GROUP], BF16)
             for e in range(2):
                 nc.sync.dma_start(
-                    out=stacked[e * (P // 2) : (e + 1) * (P // 2), :, :],
+                    out=stacked[e:P:2, :, :],
                     in_=lora_b[q].rearrange("k (g s e) d -> e (k g) s d", g=RUNS, e=2)[
                         e, :, :, c * GROUP : (c + 1) * GROUP
                     ],
@@ -388,12 +386,8 @@ def tile_skilledlora_pb_kernel(tc, h, weights, lora_b, out):
                 due("scalar", n + EXIT, lambda bank=product_bank, first=first: leave(bank, first))
 
         groups = [(q, c, b) for q, c in ((0, 0), (1, 0), (0, 1), (1, 1), (2, 0)) for b in range(B)]
-        if NTURN >= 8:
-            turned_units = groups[:8]
-            straight_units = groups[8:]
-        else:
-            turned_units = groups[:NTURN]
-            straight_units = groups[8:12] + groups[NTURN:8] + groups[12:]
+        turned_units = groups[:8] + groups[16 : 8 + NTURN]
+        straight_units = groups[8:16] + groups[8 + NTURN :]
         matmul_units = [(q, c, b) for (q, c) in MATMUL_GROUPS for b in range(B)]
         pieces = [
             (g, j, u)
@@ -404,8 +398,7 @@ def tile_skilledlora_pb_kernel(tc, h, weights, lora_b, out):
         steps = len(straight_units) * NS
 
         for k in range(NS):
-            load_half_skill(0, 1, k)
-            load_half_skill(0, 0, k)
+            load_whole_skill(0, k)
         load_h(0)
         load_h(1)
         load_stacked(0)

@@ -45,31 +45,35 @@ EXIT = 3
 COPY_OUT = 2
 QUANT = 6
 MERGE = 5
-TURN = 2
+TURN = 1
 ADD_GAP = 2
 ADD_DELAY = 2
 ADDS_FIRST = True
 BACKLOG = 3
 EXITS_FIRST = True
-H_STEPS = (6, 10, 14, 18)
-M_START = 28
-M_EVERY = 5.5
-P_START = 14
+H_STEPS = (5, 8, 11, 14)
+M_START = 30
+M_EVERY = 5
+P_START = 18
 MX_BUFS = 4
 STORE_BUFS = 4
 TURNED_BUFS = 2
 NT = 10
-EARLY = 6
+EARLY = 24
 S_STEPS = (0, 1, 3, 4, 6)
 V_STEPS = ()
 REGROUP = 1
-STRIDED = True
+FINAL = "pairs"
+TAIL_V = True
+H_AFTER = (3, 7, 7, 7)
+SPLIT_LAST = True
+LAST_STEPS = (40, 62, 64, 66)
 NTURN = 8
 SCALAR_REGROUPS = 0
-QUANT_S = 3
+QUANT_S = 4
 HALF_STEPS = 44
 WHOLE_STEP = 8
-STACK_STEPS = (12, 30)
+STACK_STEPS = (22, 36)
 
 FLOPS = 2 * B * S * R * OUT + 2 * B * Q * NS * R * DO
 
@@ -78,7 +82,6 @@ def tile_skilledlora_pb_kernel(tc, h, weights, lora_b, out):
     nc = tc.nc
     with ExitStack() as ctx:
         consts = ctx.enter_context(tc.tile_pool(name="consts", bufs=1))
-        h_pool = ctx.enter_context(tc.tile_pool(name="h_rows", bufs=2))
         h_grouped_pool = ctx.enter_context(tc.tile_pool(name="h_grouped", bufs=1))
         whole_pool = ctx.enter_context(tc.tile_pool(name="whole_skills", bufs=2 * NS))
         stacked_pool = ctx.enter_context(tc.tile_pool(name="stacked", bufs=2))
@@ -174,12 +177,10 @@ def tile_skilledlora_pb_kernel(tc, h, weights, lora_b, out):
                 )
             stacked_of[g] = stacked
 
-        h_rows_of = {}
+        h_rows = stacked_pool.tile([P, B, TOKEN_TILES, R], BF16, tag="stacked")
 
         def load_h(b):
-            h_rows = h_pool.tile([P, TOKEN_TILES, R], BF16)
-            nc.sync.dma_start(out=h_rows[:], in_=h[b].rearrange("(n p) r -> p n r", p=P))
-            h_rows_of[b] = h_rows
+            nc.sync.dma_start(out=h_rows[:, b, :, :], in_=h[b].rearrange("(n p) r -> p n r", p=P))
 
         agenda = {"tensor": {}, "scalar": {}}
         vector_queue = []
@@ -191,7 +192,6 @@ def tile_skilledlora_pb_kernel(tc, h, weights, lora_b, out):
             vector_queue.append([step, job])
 
         def turn_h(b, n):
-            h_rows = h_rows_of[b]
             h_grouped = h_grouped_pool.tile([P, S * PACK], BF16, align_bytes=64)
             grouped_words = h_grouped[:].bitcast(F32).rearrange("p (s u) -> p s u", u=HALVES)
             tiles_per_bank = BANK // (HALVES * P)
@@ -207,7 +207,7 @@ def tile_skilledlora_pb_kernel(tc, h, weights, lora_b, out):
             for first in range(0, TOKEN_TILES, tiles_per_bank):
                 turned_h = psum.tile([P, tiles_per_bank, HALVES, P], F32, tag="bank")
                 for m in range(tiles_per_bank):
-                    words = h_rows[:, first + m, :].bitcast(F32).rearrange(
+                    words = h_rows[:, b, first + m, :].bitcast(F32).rearrange(
                         "p (w u) -> p u w", u=HALVES
                     )
                     for u in range(HALVES):
@@ -220,8 +220,6 @@ def tile_skilledlora_pb_kernel(tc, h, weights, lora_b, out):
                 )
 
             for_vector(n + COPY_OUT + 1, quantise_h)
-            if b + 2 < B:
-                load_h(b + 2)
 
         def mix_piece(g, j, u, n):
             q, c = MATMUL_GROUPS[g]
@@ -252,7 +250,7 @@ def tile_skilledlora_pb_kernel(tc, h, weights, lora_b, out):
         mixed_of = {}
 
         def product(engine, unit, k):
-            q, c, b = unit
+            q, c, b = unit[:3]
             term = term_pool.tile([P, PACK, GROUP], F32)
             if engine == "scalar":
                 nc.scalar.activation(
@@ -287,7 +285,7 @@ def tile_skilledlora_pb_kernel(tc, h, weights, lora_b, out):
         accs = {}
 
         def add_block(unit, terms, j, u, turned, n):
-            q, c, b = unit
+            q, c, b = unit[:3]
             if u == 0:
                 acc = psum.tile([P, 2, HALVES, P], F32, tag="bank")
                 accs[j] = acc
@@ -320,7 +318,8 @@ def tile_skilledlora_pb_kernel(tc, h, weights, lora_b, out):
                 for_vector(n + MERGE, merge)
 
         def turn_back(unit, blocks, n):
-            back = psum.tile([P, HALVES, GROUP], F32, tag="bank")
+            width = len(blocks) * P
+            back = psum.tile([P, HALVES, width], F32, tag="bank")
             for j, block in enumerate(blocks):
                 words = block.bitcast(F32)
                 for u in range(HALVES):
@@ -330,12 +329,12 @@ def tile_skilledlora_pb_kernel(tc, h, weights, lora_b, out):
                     )
 
             def copy_out():
-                grouped = mx_pool.tile([P, GROUP * PACK], BF16, align_bytes=64)
+                grouped = mx_pool.tile([P, width * PACK], BF16, align_bytes=64)
                 nc.scalar.copy(
                     out=grouped[:].bitcast(F32).rearrange("p (d u) -> p d u", u=HALVES),
                     in_=back[:].rearrange("p u d -> p d u"),
                 )
-                for_vector(n + QUANT, lambda step: quantise_and_multiply(unit, 0, BLOCKS, grouped, step))
+                for_vector(n + QUANT, lambda step: quantise_and_multiply(unit, unit[3], unit[4], grouped, step))
 
             due("scalar", n + COPY_OUT, copy_out)
 
@@ -347,8 +346,17 @@ def tile_skilledlora_pb_kernel(tc, h, weights, lora_b, out):
             )
             for_vector(n + QUANT_S, lambda step: quantise_and_multiply(unit, 0, BLOCKS, grouped, step))
 
+        def regroup_pairs(copy, unit, paired, n):
+            first, blocks = unit[3:]
+            grouped = mx_pool.tile([P, blocks * P * PACK], BF16, align_bytes=64)
+            copy(
+                out=grouped[:].bitcast(F32).rearrange("p (d u) -> p d u", u=HALVES),
+                in_=paired[:].rearrange("p u d e -> p u (d e)").bitcast(F32).rearrange("p u d -> p d u"),
+            )
+            for_vector(n + QUANT_S, lambda step: quantise_and_multiply(unit, first, blocks, grouped, step))
+
         def quantise_and_multiply(unit, first_block, blocks, grouped, n):
-            q, c, b = unit
+            q, c, b = unit[:3]
             width = blocks * P
             codes = mx_pool.tile([P, width], U32, align_bytes=64)
             scales = mx_pool.tile([P, width], U8, align_bytes=64)
@@ -358,10 +366,17 @@ def tile_skilledlora_pb_kernel(tc, h, weights, lora_b, out):
             result = store_pool.tile([P, TOKEN_TILES, width], F32)
 
             def leave(product_bank, first):
-                nc.scalar.activation(
-                    out=result[:, first : first + tiles_per_bank, :], in_=product_bank[:],
-                    func=COPY, scale=SCALING,
-                )
+                if TAIL_V and state["over"] and state["turn"]:
+                    nc.vector.tensor_scalar(
+                        out=result[:, first : first + tiles_per_bank, :], in0=product_bank[:],
+                        scalar1=SCALING, scalar2=None, op0=MULT,
+                    )
+                else:
+                    nc.scalar.activation(
+                        out=result[:, first : first + tiles_per_bank, :], in_=product_bank[:],
+                        func=COPY, scale=SCALING,
+                    )
+                state["turn"] = not state["turn"]
                 if first + tiles_per_bank == TOKEN_TILES:
                     nc.sync.dma_start(
                         out=out[b, :, first_column : first_column + width].rearrange(
@@ -385,10 +400,12 @@ def tile_skilledlora_pb_kernel(tc, h, weights, lora_b, out):
                     )
                 due("scalar", n + EXIT, lambda bank=product_bank, first=first: leave(bank, first))
 
-        groups = [(q, c, b) for q, c in ((0, 0), (1, 0), (0, 1), (1, 1), (2, 0)) for b in range(B)]
+        groups = [(q, c, b, 0, BLOCKS) for q, c in ((0, 0), (1, 0), (0, 1), (1, 1), (2, 0)) for b in range(B)]
         turned_units = groups[:8] + groups[16 : 8 + NTURN]
         straight_units = groups[8:16] + groups[8 + NTURN :]
-        matmul_units = [(q, c, b) for (q, c) in MATMUL_GROUPS for b in range(B)]
+        if SPLIT_LAST:
+            straight_units[-1] = straight_units[-1][:3] + (1, 1)
+        matmul_units = [(q, c, b, 0, BLOCKS) for (q, c) in MATMUL_GROUPS for b in range(B)]
         pieces = [
             (g, j, u)
             for g in range(len(MATMUL_GROUPS))
@@ -399,8 +416,9 @@ def tile_skilledlora_pb_kernel(tc, h, weights, lora_b, out):
 
         for k in range(NS):
             load_whole_skill(0, k)
-        load_h(0)
-        load_h(1)
+            for b in range(B):
+                if H_AFTER[b] == k:
+                    load_h(b)
         load_stacked(0)
         later_loads = (
             [lambda k=k: load_whole_skill(1, k) for k in range(NS)]
@@ -421,6 +439,43 @@ def tile_skilledlora_pb_kernel(tc, h, weights, lora_b, out):
             g = i // B
             due("tensor", int(M_START + M_EVERY * i), lambda n, g=g, unit=unit: turn_back(
                 unit, [mixed_of[g][:, j, unit[2], :] for j in range(BLOCKS)], n))
+        if SPLIT_LAST:
+            last_q, last_c, last_b = straight_units[-1][:3]
+
+            def load_last():
+                stacked = stacked_pool.tile([P, PAIRS, P], BF16)
+                for e in range(2):
+                    nc.sync.dma_start(
+                        out=stacked[e:P:2, :, :],
+                        in_=lora_b[last_q].rearrange("k (g s e) d -> e (k g) s d", g=RUNS, e=2)[
+                            e, :, :, last_c * GROUP : last_c * GROUP + P
+                        ],
+                    )
+                state["stacked"] = stacked
+
+            def mix_last(u, n):
+                if u == 0:
+                    last = turned_pool.tile([P, R], BF16)
+                    state["last"] = last
+                last = state["last"]
+                bank = psum.tile([P, MATMULS_PER_BANK, 2 * RUNS], BF16, tag="bank")
+                for a in range(MATMULS_PER_BANK):
+                    nc.tensor.matmul(
+                        out=bank[:, a, :], lhsT=state["stacked"][:, HALVES * a + u, :],
+                        rhs=mixers[:, last_q - FIRST_MATMUL_SPLIT, last_b, :], start=True, stop=True,
+                    )
+
+                def copy_out():
+                    nc.scalar.copy(
+                        out=last[:].bitcast(F32).rearrange("p (u g a) -> p u g a", u=HALVES, g=RUNS)[:, u, :, :],
+                        in_=bank[:].bitcast(F32).rearrange("p a g -> p g a"),
+                    )
+
+                due("scalar", n + COPY_OUT, copy_out)
+
+            for u in range(HALVES):
+                due("tensor", LAST_STEPS[1 + u], lambda n, u=u: mix_last(u, n))
+            due("tensor", LAST_STEPS[3] + COPY_OUT, lambda n: turn_back((last_q, last_c, last_b, 0, 1), [state["last"][:]], n))
 
         stream = [(i, k) for i in range(len(turned_units)) for k in range(NS - 1)]
 
@@ -433,7 +488,7 @@ def tile_skilledlora_pb_kernel(tc, h, weights, lora_b, out):
                     due("tensor", n + ADD_GAP * (HALVES * j + u), lambda m, j=j, u=u:
                         add_block(unit, terms, j, u, turned, m))
 
-        state = {"made": 0}
+        state = {"made": 0, "over": False, "turn": False}
         sums = {}
 
         def next_product(engine, n):
@@ -454,13 +509,14 @@ def tile_skilledlora_pb_kernel(tc, h, weights, lora_b, out):
         while n < steps or vector_queue or any(
             step >= n for jobs in agenda.values() for step in jobs
         ):
+            state["over"] = n >= steps + 2
             pair, k, member = n // (2 * NS), n // 2 % NS, n % 2
             if n < steps:
                 unit = straight_units[2 * pair + member]
-                q, c, b = unit
-                skill = skills[(q, c)][k]
+                q, c, b, first, blocks = unit
+                skill = skills[(q, c)][k][:, :, first * P : (first + blocks) * P]
                 if k == 0:
-                    total = sum_pool.tile([P, PACK, GROUP], F32)
+                    total = sum_pool.tile([P, PACK, blocks * P], F32)
                     sums[member] = total
                     nc.vector.tensor_scalar(
                         out=total[:], in0=skill, scalar1=weight_of(b, q, k), scalar2=None, op0=MULT
@@ -471,7 +527,25 @@ def tile_skilledlora_pb_kernel(tc, h, weights, lora_b, out):
                         out=total[:], in0=skill, scalar=weight_of(b, q, k), in1=total[:],
                         op0=MULT, op1=ADD,
                     )
-                elif STRIDED:
+                elif FINAL == "pairs":
+                    total = sums[member]
+                    paired = rounded_pool.tile([P, HALVES, blocks * P, 2], BF16)
+                    for u in range(HALVES):
+                        planes = slice(2 * u, 2 * u + 2)
+                        nc.vector.scalar_tensor_tensor(
+                            out=paired[:, u, :, :],
+                            in0=skill[:, planes, :].rearrange("p e d -> p d e"),
+                            scalar=weight_of(b, q, k),
+                            in1=total[:, planes, :].rearrange("p e d -> p d e"),
+                            op0=MULT, op1=ADD,
+                        )
+                    if member < SCALAR_REGROUPS:
+                        due("scalar", n + REGROUP, lambda unit=unit, paired=paired, n=n:
+                            regroup_pairs(nc.scalar.copy, unit, paired, n + REGROUP))
+                    else:
+                        for_vector(n + REGROUP, lambda step, unit=unit, paired=paired:
+                                   regroup_pairs(nc.vector.tensor_copy, unit, paired, step))
+                elif FINAL == "strided":
                     total = sums[member]
                     grouped = mx_pool.tile([P, GROUP * PACK], BF16, align_bytes=64)
                     nc.vector.scalar_tensor_tensor(
@@ -518,6 +592,8 @@ def tile_skilledlora_pb_kernel(tc, h, weights, lora_b, out):
             if not ADDS_FIRST:
                 for job in agenda["tensor"].get(n, []):
                     job(n)
+            if SPLIT_LAST and n == LAST_STEPS[0]:
+                load_last()
             for load_step, load in zip(load_steps, later_loads):
                 if load_step == n:
                     load()

@@ -26,54 +26,51 @@ BANK = 512
 
 GROUP = 256
 BLOCKS = GROUP // P
-GROUPS_PER_SPLIT = DO // GROUP
 
 RUNS = 8
 PAIRS = R // RUNS // 2
 FULL = B * RUNS * 2
 MATMULS_PER_BANK = 2 * BANK // FULL
 
-MATMUL_GROUPS = ((2, 1), (3, 0), (3, 1))
+MATMUL_GROUPS = ((2, GROUP), (3, 0), (3, GROUP))
 FIRST_MATMUL_SPLIT = 2
 MATMUL_SPLITS = Q - FIRST_MATMUL_SPLIT
-MIXING_MATMULS = len(MATMUL_GROUPS) * BLOCKS * PAIRS
-assert MIXING_MATMULS * P * P * FULL * 10 < B * S * R * OUT
+LAST_MATMULS = 2 * MATMULS_PER_BANK
+assert (
+    len(MATMUL_GROUPS) * BLOCKS * PAIRS * FULL + LAST_MATMULS * 2 * RUNS
+) * P * P * 10 < B * S * R * OUT
 
 LATE = NS - 1
-TERM_BUFS = 11
-EXIT = 3
-COPY_OUT = 2
-QUANT = 6
-MERGE = 5
-TURN = 1
-ADD_GAP = 2
-ADD_DELAY = 2
-ADDS_FIRST = True
-BACKLOG = 3
-EXITS_FIRST = True
-H_STEPS = (5, 8, 11, 14)
-M_START = 30
-M_EVERY = 5
-P_START = 18
-MX_BUFS = 4
+TERM_BUFS = 13
 STORE_BUFS = 4
+MX_BUFS = 3
 TURNED_BUFS = 2
-NT = 10
-EARLY = 24
+EXIT = 3
+COPY_OUT = 1
+QUANT = 5
+MERGE = 6
+TURN = 1
+ADD_GAP = 1
+ADD_DELAY = 2
+BACKLOG = 3
+EARLY = 16
 S_STEPS = (0, 1, 3, 4, 6)
-V_STEPS = ()
-REGROUP = 1
-FINAL = "pairs"
+V_STEPS = (7,)
+QUANT_S = 2
+H_STEPS = (10, 14, 18, 22)
+P_START = 22
+P_EVERY = 2
+M_START = 32
+M_EVERY = 10
+LAST_STEPS = (60, 80, 82, 84)
+STACK_STEPS = (26, 42)
+SECOND_STEP = 22
+THIRD_STEP = 38
 TAIL_V = True
-H_AFTER = (3, 7, 7, 7)
-SPLIT_LAST = True
-LAST_STEPS = (40, 62, 64, 66)
-NTURN = 8
-SCALAR_REGROUPS = 0
-QUANT_S = 4
-HALF_STEPS = 44
-WHOLE_STEP = 8
-STACK_STEPS = (22, 36)
+HALF_BUFS = 11
+SECOND_EVERY = 2
+THIRD_EVERY = 4
+HEAD = "WhhhhWhhhhWHWHWHWHWW"
 
 FLOPS = 2 * B * S * R * OUT + 2 * B * Q * NS * R * DO
 
@@ -83,11 +80,11 @@ def tile_skilledlora_pb_kernel(tc, h, weights, lora_b, out):
     with ExitStack() as ctx:
         consts = ctx.enter_context(tc.tile_pool(name="consts", bufs=1))
         h_grouped_pool = ctx.enter_context(tc.tile_pool(name="h_grouped", bufs=1))
-        whole_pool = ctx.enter_context(tc.tile_pool(name="whole_skills", bufs=2 * NS))
+        half_pool = ctx.enter_context(tc.tile_pool(name="half_skills", bufs=HALF_BUFS))
+        whole_pool = ctx.enter_context(tc.tile_pool(name="whole_skills", bufs=NS))
         stacked_pool = ctx.enter_context(tc.tile_pool(name="stacked", bufs=2))
         term_pool = ctx.enter_context(tc.tile_pool(name="terms", bufs=TERM_BUFS))
-        sum_pool = ctx.enter_context(tc.tile_pool(name="sums", bufs=4))
-        rounded_pool = ctx.enter_context(tc.tile_pool(name="rounded", bufs=2))
+        sum_pool = ctx.enter_context(tc.tile_pool(name="sums", bufs=2))
         late_pool = ctx.enter_context(tc.tile_pool(name="late", bufs=2))
         turned_pool = ctx.enter_context(tc.tile_pool(name="turned", bufs=TURNED_BUFS))
         mixed_pool = ctx.enter_context(tc.tile_pool(name="mixed", bufs=2))
@@ -111,15 +108,13 @@ def tile_skilledlora_pb_kernel(tc, h, weights, lora_b, out):
         mixers = consts.tile([P, MATMUL_SPLITS, B, RUNS * 2], BF16)
 
         def make_mixers():
-            by_part = identity_f32[:].rearrange("p (k g) -> p k g", k=NS)
             is_skill = consts.tile([P, NS], F32)
-            nc.vector.tensor_reduce(out=is_skill[:], in_=by_part, axis=X, op=ADD)
+            nc.vector.tensor_reduce(
+                out=is_skill[:], in_=identity_f32[:].rearrange("p (k g) -> p k g", k=NS), axis=X, op=ADD
+            )
             is_rank = consts.tile([P, RUNS * 2], F32)
             nc.vector.tensor_reduce(
-                out=is_rank[:],
-                in_=identity_f32[:].rearrange("p (k g) -> p g k", k=NS),
-                axis=X,
-                op=ADD,
+                out=is_rank[:], in_=identity_f32[:].rearrange("p (k g) -> p g k", k=NS), axis=X, op=ADD
             )
             masked = consts.tile([P, B, MATMUL_SPLITS, NS], F32)
             nc.vector.tensor_tensor(
@@ -145,34 +140,32 @@ def tile_skilledlora_pb_kernel(tc, h, weights, lora_b, out):
             column = (b * Q + q) * NS + k
             return w_f32[:, column : column + 1]
 
-        skills = {}
+        parts = {}
 
-        def load_half_skill(q, c, k):
-            half = whole_pool.tile([P, PACK, GROUP], BF16, tag="whole")
+        def skill_of(unit, k):
+            q, b, column, width = unit
+            view = parts[(q, column // GROUP)][k]
+            inside = column % GROUP
+            return view[:, :, inside : inside + width]
+
+        def load_skill(pool, q, column, width, k):
+            skill = pool.tile([P, PACK, width], BF16, tag="skill")
             nc.sync.dma_start(
-                out=half[:],
-                in_=lora_b[q, k].rearrange("(p t) d -> p t d", t=PACK)[
-                    :, :, c * GROUP : (c + 1) * GROUP
-                ],
+                out=skill[:],
+                in_=lora_b[q, k].rearrange("(p t) d -> p t d", t=PACK)[:, :, column : column + width],
             )
-            skills.setdefault((q, c), []).append(half[:])
-
-        def load_whole_skill(q, k):
-            whole = whole_pool.tile([P, PACK, DO], BF16, tag="whole")
-            nc.sync.dma_start(out=whole[:], in_=lora_b[q, k].rearrange("(p t) d -> p t d", t=PACK))
-            for c in range(GROUPS_PER_SPLIT):
-                skills.setdefault((q, c), []).append(whole[:, :, c * GROUP : (c + 1) * GROUP])
+            for first in range(0, width, GROUP):
+                parts.setdefault((q, (column + first) // GROUP), []).append(skill[:, :, first:width])
 
         stacked_of = {}
 
-        def load_stacked(g):
-            q, c = MATMUL_GROUPS[g]
-            stacked = stacked_pool.tile([P, PAIRS, GROUP], BF16)
+        def load_stacked(g, q, column, width):
+            stacked = stacked_pool.tile([P, PAIRS, width], BF16)
             for e in range(2):
                 nc.sync.dma_start(
                     out=stacked[e:P:2, :, :],
                     in_=lora_b[q].rearrange("k (g s e) d -> e (k g) s d", g=RUNS, e=2)[
-                        e, :, :, c * GROUP : (c + 1) * GROUP
+                        e, :, :, column : column + width
                     ],
                 )
             stacked_of[g] = stacked
@@ -190,6 +183,8 @@ def tile_skilledlora_pb_kernel(tc, h, weights, lora_b, out):
 
         def for_vector(step, job):
             vector_queue.append([step, job])
+
+        state = {"made": 0, "over": False, "turn": False}
 
         def turn_h(b, n):
             h_grouped = h_grouped_pool.tile([P, S * PACK], BF16, align_bytes=64)
@@ -221,21 +216,27 @@ def tile_skilledlora_pb_kernel(tc, h, weights, lora_b, out):
 
             for_vector(n + COPY_OUT + 1, quantise_h)
 
+        def mix(bank, stacked, j, u, moving):
+            for a in range(MATMULS_PER_BANK):
+                nc.tensor.matmul(
+                    out=bank[:, a, :],
+                    lhsT=stacked[:, HALVES * a + u, j * P : (j + 1) * P],
+                    rhs=moving,
+                    start=True,
+                    stop=True,
+                )
+
+        mixed_of = {}
+
         def mix_piece(g, j, u, n):
-            q, c = MATMUL_GROUPS[g]
+            q = MATMUL_GROUPS[g][0]
             if g not in mixed_of:
                 mixed = mixed_pool.tile([P, BLOCKS, B, R], BF16)
                 mixed_of[g] = mixed
             mixed = mixed_of[g]
             bank = psum.tile([P, MATMULS_PER_BANK, FULL], BF16, tag="bank")
-            for a in range(MATMULS_PER_BANK):
-                nc.tensor.matmul(
-                    out=bank[:, a, :],
-                    lhsT=stacked_of[g][:, HALVES * a + u, j * P : (j + 1) * P],
-                    rhs=mixers[:, q - FIRST_MATMUL_SPLIT, :, :].rearrange("p b g -> p (b g)"),
-                    start=True,
-                    stop=True,
-                )
+            mix(bank, stacked_of[g], j, u,
+                mixers[:, q - FIRST_MATMUL_SPLIT, :, :].rearrange("p b g -> p (b g)"))
 
             def copy_out():
                 nc.scalar.copy(
@@ -247,35 +248,50 @@ def tile_skilledlora_pb_kernel(tc, h, weights, lora_b, out):
 
             due("scalar", n + COPY_OUT, copy_out)
 
-        mixed_of = {}
+        def mix_last(unit, u, n):
+            q, b, column, width = unit
+            if u == 0:
+                last = turned_pool.tile([P, R], BF16)
+                state["last"] = last
+            last = state["last"]
+            bank = psum.tile([P, MATMULS_PER_BANK, 2 * RUNS], BF16, tag="bank")
+            mix(bank, stacked_of["last"], 0, u, mixers[:, q - FIRST_MATMUL_SPLIT, b, :])
+
+            def copy_out():
+                nc.scalar.copy(
+                    out=last[:].bitcast(F32).rearrange("p (u g a) -> p u g a", u=HALVES, g=RUNS)[:, u, :, :],
+                    in_=bank[:].bitcast(F32).rearrange("p a g -> p g a"),
+                )
+
+            due("scalar", n + COPY_OUT, copy_out)
 
         def product(engine, unit, k):
-            q, c, b = unit[:3]
+            q, b, column, width = unit
             term = term_pool.tile([P, PACK, GROUP], F32)
             if engine == "scalar":
                 nc.scalar.activation(
-                    out=term[:], in_=skills[(q, c)][k], func=COPY, scale=weight_of(b, q, k)
+                    out=term[:], in_=skill_of(unit, k), func=COPY, scale=weight_of(b, q, k)
                 )
             else:
                 nc.vector.tensor_scalar(
-                    out=term[:], in0=skills[(q, c)][k], scalar1=weight_of(b, q, k), scalar2=None,
+                    out=term[:], in0=skill_of(unit, k), scalar1=weight_of(b, q, k), scalar2=None,
                     op0=MULT,
                 )
             return term
 
         late_of = {}
 
-        def turn_late(q, c, n):
+        def turn_late(unit, n):
+            q, b, column, width = unit
             bank = psum.tile([P, BLOCKS, 2, HALVES, P], BF16, tag="bank")
+            skill = skill_of(unit, LATE)
             for j in range(BLOCKS):
                 for t in range(PACK):
                     nc.tensor.transpose(
-                        bank[:, j, t % 2, t // 2, :],
-                        skills[(q, c)][LATE][:, t, j * P : (j + 1) * P],
-                        identity_bf16[:],
+                        bank[:, j, t % 2, t // 2, :], skill[:, t, j * P : (j + 1) * P], identity_bf16[:]
                     )
             late = late_pool.tile([P, BLOCKS, HALVES * P, 2], BF16)
-            late_of[(q, c)] = late
+            late_of[(q, column)] = late
 
             def copy_out():
                 nc.scalar.copy(out=late[:], in_=bank[:].rearrange("d j e u p -> d j (u p) e"))
@@ -285,7 +301,7 @@ def tile_skilledlora_pb_kernel(tc, h, weights, lora_b, out):
         accs = {}
 
         def add_block(unit, terms, j, u, turned, n):
-            q, c, b = unit[:3]
+            q, b, column, width = unit
             if u == 0:
                 acc = psum.tile([P, 2, HALVES, P], F32, tag="bank")
                 accs[j] = acc
@@ -304,7 +320,7 @@ def tile_skilledlora_pb_kernel(tc, h, weights, lora_b, out):
             def merge(step):
                 nc.vector.scalar_tensor_tensor(
                     out=turned[:, j, :].rearrange("d (x e) -> d x e", e=2),
-                    in0=late_of[(q, c)][:, j, :, :],
+                    in0=late_of[(q, column)][:, j, :, :],
                     scalar=weight_of(b, q, LATE),
                     in1=acc[:].rearrange("d e u p -> d (u p) e"),
                     op0=MULT,
@@ -312,289 +328,209 @@ def tile_skilledlora_pb_kernel(tc, h, weights, lora_b, out):
                 )
                 if j == BLOCKS - 1:
                     due("tensor", step + TURN, lambda m: turn_back(
-                        unit, [turned[:, i, :] for i in range(BLOCKS)], m))
+                        [unit], [turned[:, i, :] for i in range(BLOCKS)], m))
 
             if u == HALVES - 1:
                 for_vector(n + MERGE, merge)
 
-        def turn_back(unit, blocks, n):
-            width = len(blocks) * P
-            back = psum.tile([P, HALVES, width], F32, tag="bank")
-            for j, block in enumerate(blocks):
-                words = block.bitcast(F32)
-                for u in range(HALVES):
-                    nc.tensor.transpose(
-                        back[:, u, j * P : (j + 1) * P], words[:, u * P : (u + 1) * P],
-                        identity_f32[:],
+        def turn_back(units, blocks, n):
+            grouped = mx_pool.tile([P, len(blocks) * P * PACK], BF16, align_bytes=64)
+            per_bank = min(len(blocks), BLOCKS)
+            for first in range(0, len(blocks), per_bank):
+                width = per_bank * P
+                back = psum.tile([P, HALVES, width], F32, tag="bank")
+                for j in range(per_bank):
+                    words = blocks[first + j].bitcast(F32)
+                    for u in range(HALVES):
+                        nc.tensor.transpose(
+                            back[:, u, j * P : (j + 1) * P], words[:, u * P : (u + 1) * P],
+                            identity_f32[:],
+                        )
+
+                def copy_out(back, first, width):
+                    nc.scalar.copy(
+                        out=grouped[:, first * P * PACK : (first * P + width) * PACK]
+                        .bitcast(F32).rearrange("p (d u) -> p d u", u=HALVES),
+                        in_=back[:].rearrange("p u d -> p d u"),
                     )
 
-            def copy_out():
-                grouped = mx_pool.tile([P, width * PACK], BF16, align_bytes=64)
-                nc.scalar.copy(
-                    out=grouped[:].bitcast(F32).rearrange("p (d u) -> p d u", u=HALVES),
-                    in_=back[:].rearrange("p u d -> p d u"),
-                )
-                for_vector(n + QUANT, lambda step: quantise_and_multiply(unit, unit[3], unit[4], grouped, step))
+                due("scalar", n + COPY_OUT, lambda back=back, first=first, width=width:
+                    copy_out(back, first, width))
+            for_vector(n + COPY_OUT + QUANT, lambda step: quantise_and_multiply(units, grouped, step))
 
-            due("scalar", n + COPY_OUT, copy_out)
-
-        def regroup(copy, unit, rounded, n):
-            grouped = mx_pool.tile([P, GROUP * PACK], BF16, align_bytes=64)
-            copy(
-                out=grouped[:].rearrange("p (d t) -> p d t", t=PACK),
-                in_=rounded[:].rearrange("p t d -> p d t"),
-            )
-            for_vector(n + QUANT_S, lambda step: quantise_and_multiply(unit, 0, BLOCKS, grouped, step))
-
-        def regroup_pairs(copy, unit, paired, n):
-            first, blocks = unit[3:]
-            grouped = mx_pool.tile([P, blocks * P * PACK], BF16, align_bytes=64)
-            copy(
-                out=grouped[:].bitcast(F32).rearrange("p (d u) -> p d u", u=HALVES),
-                in_=paired[:].rearrange("p u d e -> p u (d e)").bitcast(F32).rearrange("p u d -> p d u"),
-            )
-            for_vector(n + QUANT_S, lambda step: quantise_and_multiply(unit, first, blocks, grouped, step))
-
-        def quantise_and_multiply(unit, first_block, blocks, grouped, n):
-            q, c, b = unit[:3]
-            width = blocks * P
-            codes = mx_pool.tile([P, width], U32, align_bytes=64)
-            scales = mx_pool.tile([P, width], U8, align_bytes=64)
+        def quantise_and_multiply(units, grouped, n):
+            width = units[0][3]
+            codes = mx_pool.tile([P, len(units) * width], U32, align_bytes=64)
+            scales = mx_pool.tile([P, len(units) * width], U8, align_bytes=64)
             nc.vector.quantize_mx(out=codes[:].bitcast(FP8X4), scales=scales[:], in_=grouped[:])
-            first_column = q * DO + c * GROUP + first_block * P
-            tiles_per_bank = BANK // width
-            result = store_pool.tile([P, TOKEN_TILES, width], F32)
+            tiles_per_bank = min(BANK // width, TOKEN_TILES)
+            tiles_per_store = min(2 * BANK // width, TOKEN_TILES)
 
-            def leave(product_bank, first):
+            def leave(unit, result, bank, first):
+                q, b, column, width = unit
+                inside = first % tiles_per_store
+                target = result[:, inside : inside + tiles_per_bank, :]
                 if TAIL_V and state["over"] and state["turn"]:
                     nc.vector.tensor_scalar(
-                        out=result[:, first : first + tiles_per_bank, :], in0=product_bank[:],
-                        scalar1=SCALING, scalar2=None, op0=MULT,
+                        out=target, in0=bank[:], scalar1=SCALING, scalar2=None, op0=MULT
                     )
                 else:
-                    nc.scalar.activation(
-                        out=result[:, first : first + tiles_per_bank, :], in_=product_bank[:],
-                        func=COPY, scale=SCALING,
-                    )
+                    nc.scalar.activation(out=target, in_=bank[:], func=COPY, scale=SCALING)
                 state["turn"] = not state["turn"]
-                if first + tiles_per_bank == TOKEN_TILES:
+                done = first + tiles_per_bank
+                if done % tiles_per_store == 0:
                     nc.sync.dma_start(
-                        out=out[b, :, first_column : first_column + width].rearrange(
-                            "(n p) d -> p n d", p=P
-                        ),
+                        out=out[
+                            b, (done - tiles_per_store) * P : done * P,
+                            q * DO + column : q * DO + column + width,
+                        ].rearrange("(n p) d -> p n d", p=P),
                         in_=result[:],
                     )
 
-            for first in range(0, TOKEN_TILES, tiles_per_bank):
-                product_bank = psum.tile([P, tiles_per_bank, width], F32, tag="bank")
-                for m in range(tiles_per_bank):
-                    tokens = slice((first + m) * P, (first + m + 1) * P)
-                    nc.tensor.matmul_mx(
-                        out=product_bank[:, m, :],
-                        lhsT=h_codes[:, b, tokens].bitcast(FP8X4),
-                        lhsT_scale=h_scales[:, b, tokens],
-                        rhs=codes[:].bitcast(FP8X4),
-                        rhs_scale=scales[:],
-                        start=True,
-                        stop=True,
-                    )
-                due("scalar", n + EXIT, lambda bank=product_bank, first=first: leave(bank, first))
+            for i, unit in enumerate(units):
+                columns = slice(i * width, (i + 1) * width)
+                b = unit[1]
+                for first in range(0, TOKEN_TILES, tiles_per_bank):
+                    if first % tiles_per_store == 0:
+                        result = store_pool.tile([P, tiles_per_store, width], F32)
+                    bank = psum.tile([P, tiles_per_bank, width], F32, tag="bank")
+                    for m in range(tiles_per_bank):
+                        tokens = slice((first + m) * P, (first + m + 1) * P)
+                        nc.tensor.matmul_mx(
+                            out=bank[:, m, :],
+                            lhsT=h_codes[:, b, tokens].bitcast(FP8X4),
+                            lhsT_scale=h_scales[:, b, tokens],
+                            rhs=codes[:, columns].bitcast(FP8X4),
+                            rhs_scale=scales[:, columns],
+                            start=True,
+                            stop=True,
+                        )
+                    due("scalar", n + EXIT, lambda unit=unit, result=result, bank=bank, first=first:
+                        leave(unit, result, bank, first))
 
-        groups = [(q, c, b, 0, BLOCKS) for q, c in ((0, 0), (1, 0), (0, 1), (1, 1), (2, 0)) for b in range(B)]
-        turned_units = groups[:8] + groups[16 : 8 + NTURN]
-        straight_units = groups[8:16] + groups[8 + NTURN :]
-        if SPLIT_LAST:
-            straight_units[-1] = straight_units[-1][:3] + (1, 1)
-        matmul_units = [(q, c, b, 0, BLOCKS) for (q, c) in MATMUL_GROUPS for b in range(B)]
-        pieces = [
-            (g, j, u)
-            for g in range(len(MATMUL_GROUPS))
-            for j in range(BLOCKS)
-            for u in range(HALVES)
+        def straight_op(unit, k, n):
+            q, b, column, width = unit
+            skill = skill_of(unit, k)
+            if k == 0:
+                total = sum_pool.tile([P, PACK, width], F32)
+                sums[unit] = total
+                nc.vector.tensor_scalar(
+                    out=total[:], in0=skill, scalar1=weight_of(b, q, k), scalar2=None, op0=MULT
+                )
+                return
+            total = sums[unit]
+            if k < NS - 1:
+                nc.vector.scalar_tensor_tensor(
+                    out=total[:], in0=skill, scalar=weight_of(b, q, k), in1=total[:],
+                    op0=MULT, op1=ADD,
+                )
+                return
+            grouped = mx_pool.tile([P, width * PACK], BF16, align_bytes=64)
+            nc.vector.scalar_tensor_tensor(
+                out=grouped[:].rearrange("p (d t) -> p d t", t=PACK),
+                in0=skill.rearrange("p t d -> p d t"),
+                scalar=weight_of(b, q, k),
+                in1=total[:].rearrange("p t d -> p d t"),
+                op0=MULT, op1=ADD,
+            )
+            for_vector(n + QUANT_S, lambda step: quantise_and_multiply([unit], grouped, step))
+
+        sums = {}
+        turned_units = [(1, b, column, GROUP) for column in (0, GROUP) for b in range(B)]
+        last_unit = (2, B - 1, 0, P)
+        straight_pairs = [
+            ((0, 0, 0, DO), (0, 1, 0, DO)),
+            ((0, 2, 0, DO), (0, 3, 0, DO)),
+            ((2, 0, 0, GROUP), (2, 1, 0, GROUP)),
+            ((2, 2, 0, GROUP), (2, 3, P, P)),
         ]
-        steps = len(straight_units) * NS
+        ops = []
+        for pair in straight_pairs:
+            for k in range(NS):
+                for unit in pair:
+                    ops.append((unit, k))
+                    if unit[3] > GROUP:
+                        ops.append(None)
+        steps = len(ops)
 
-        for k in range(NS):
-            load_whole_skill(0, k)
-            for b in range(B):
-                if H_AFTER[b] == k:
-                    load_h(b)
-        load_stacked(0)
-        later_loads = (
-            [lambda k=k: load_whole_skill(1, k) for k in range(NS)]
-            + [lambda: load_stacked(1)]
-            + [lambda: load_stacked(2)]
-            + [lambda k=k: load_half_skill(2, 0, k) for k in range(NS)]
-        )
-        load_steps = (
-            [WHOLE_STEP + k for k in range(NS)] + list(STACK_STEPS) + [HALF_STEPS + k for k in range(NS)]
-        )
+        head = {
+            "W": [lambda k=k: load_skill(whole_pool, 0, 0, DO, k) for k in range(NS)],
+            "h": [lambda k=k: load_skill(half_pool, 1, 0, GROUP, k) for k in range(NS)],
+            "H": [lambda b=b: load_h(b) for b in range(B)],
+        }
+        position = {"W": 0, "h": 0, "H": 0}
+        for kind in HEAD:
+            head[kind][position[kind]]()
+            position[kind] += 1
+        load_stacked(0, *MATMUL_GROUPS[0], GROUP)
+        loads = {}
+        for i in range(NS):
+            loads.setdefault(SECOND_STEP + SECOND_EVERY * i, []).append(
+                lambda k=i: load_skill(half_pool, 1, GROUP, GROUP, k))
+            loads.setdefault(THIRD_STEP + THIRD_EVERY * i, []).append(
+                lambda k=i: load_skill(whole_pool, 2, 0, GROUP, k))
+        for i in range(2):
+            loads.setdefault(STACK_STEPS[i], []).append(
+                lambda g=i + 1: load_stacked(g, *MATMUL_GROUPS[g], GROUP))
+        loads.setdefault(LAST_STEPS[0], []).append(lambda: load_stacked("last", 2, 0, P))
 
         for b in range(B):
             due("tensor", H_STEPS[b], lambda n, b=b: turn_h(b, n))
-        for i, (g, j, u) in enumerate(pieces):
-            step = P_START + 2 * i if i < PACK else int(M_START + 1 + M_EVERY * (i - PACK))
-            due("tensor", step, lambda n, g=g, j=j, u=u: mix_piece(g, j, u, n))
-        for i, unit in enumerate(matmul_units):
-            g = i // B
-            due("tensor", int(M_START + M_EVERY * i), lambda n, g=g, unit=unit: turn_back(
-                unit, [mixed_of[g][:, j, unit[2], :] for j in range(BLOCKS)], n))
-        if SPLIT_LAST:
-            last_q, last_c, last_b = straight_units[-1][:3]
+        for g in range(len(MATMUL_GROUPS)):
+            for i in range(PACK):
+                step = P_START + P_EVERY * i if g == 0 else M_START + 2 * M_EVERY * (g - 1) + 1 + M_EVERY * i // 2
+                due("tensor", step, lambda n, g=g, i=i: mix_piece(g, i // 2, i % 2, n))
+            for i in range(B // 2):
+                due("tensor", M_START + M_EVERY * (2 * g + i), lambda n, g=g, i=i: turn_back(
+                    [MATMUL_GROUPS[g][:1] + (b,) + MATMUL_GROUPS[g][1:] + (GROUP,) for b in (2 * i, 2 * i + 1)],
+                    [mixed_of[g][:, j, b, :] for b in (2 * i, 2 * i + 1) for j in range(BLOCKS)], n))
+        for u in range(HALVES):
+            due("tensor", LAST_STEPS[1 + u], lambda n, u=u: mix_last(last_unit, u, n))
+        due("tensor", LAST_STEPS[3] + COPY_OUT, lambda n: turn_back([last_unit], [state["last"][:]], n))
 
-            def load_last():
-                stacked = stacked_pool.tile([P, PAIRS, P], BF16)
-                for e in range(2):
-                    nc.sync.dma_start(
-                        out=stacked[e:P:2, :, :],
-                        in_=lora_b[last_q].rearrange("k (g s e) d -> e (k g) s d", g=RUNS, e=2)[
-                            e, :, :, last_c * GROUP : last_c * GROUP + P
-                        ],
-                    )
-                state["stacked"] = stacked
+        stream = [(unit, k) for unit in turned_units for k in range(NS - 1)]
 
-            def mix_last(u, n):
-                if u == 0:
-                    last = turned_pool.tile([P, R], BF16)
-                    state["last"] = last
-                last = state["last"]
-                bank = psum.tile([P, MATMULS_PER_BANK, 2 * RUNS], BF16, tag="bank")
-                for a in range(MATMULS_PER_BANK):
-                    nc.tensor.matmul(
-                        out=bank[:, a, :], lhsT=state["stacked"][:, HALVES * a + u, :],
-                        rhs=mixers[:, last_q - FIRST_MATMUL_SPLIT, last_b, :], start=True, stop=True,
-                    )
+        def next_product(engine, n):
+            if state["made"] == len(stream):
+                return
+            unit, k = stream[state["made"]]
+            state["made"] += 1
+            if k == 0:
+                state["terms"] = []
+            state["terms"].append(product(engine, unit, k))
+            if k == NS - 2:
+                if (unit[0], unit[2]) not in late_of:
+                    due("tensor", n + 1, lambda m: turn_late(unit, m))
+                due_adds(unit, state["terms"], n + ADD_DELAY)
 
-                def copy_out():
-                    nc.scalar.copy(
-                        out=last[:].bitcast(F32).rearrange("p (u g a) -> p u g a", u=HALVES, g=RUNS)[:, u, :, :],
-                        in_=bank[:].bitcast(F32).rearrange("p a g -> p g a"),
-                    )
-
-                due("scalar", n + COPY_OUT, copy_out)
-
-            for u in range(HALVES):
-                due("tensor", LAST_STEPS[1 + u], lambda n, u=u: mix_last(u, n))
-            due("tensor", LAST_STEPS[3] + COPY_OUT, lambda n: turn_back((last_q, last_c, last_b, 0, 1), [state["last"][:]], n))
-
-        stream = [(i, k) for i in range(len(turned_units)) for k in range(NS - 1)]
-
-
-        def due_adds(i, terms, n):
-            unit = turned_units[i]
+        def due_adds(unit, terms, n):
             turned = turned_pool.tile([P, BLOCKS, R], BF16)
             for j in range(BLOCKS):
                 for u in range(HALVES):
                     due("tensor", n + ADD_GAP * (HALVES * j + u), lambda m, j=j, u=u:
                         add_block(unit, terms, j, u, turned, m))
 
-        state = {"made": 0, "over": False, "turn": False}
-        sums = {}
-
-        def next_product(engine, n):
-            if state["made"] == len(stream):
-                return
-            i, k = stream[state["made"]]
-            state["made"] += 1
-            unit = turned_units[i]
-            if k == 0:
-                state["terms"] = []
-            state["terms"].append(product(engine, unit, k))
-            if k == NS - 2:
-                if unit[:2] not in late_of:
-                    due("tensor", n + 1, lambda m: turn_late(unit[0], unit[1], m))
-                due_adds(i, state["terms"], n + ADD_DELAY)
-
         n = 0
         while n < steps or vector_queue or any(
             step >= n for jobs in agenda.values() for step in jobs
         ):
             state["over"] = n >= steps + 2
-            pair, k, member = n // (2 * NS), n // 2 % NS, n % 2
-            if n < steps:
-                unit = straight_units[2 * pair + member]
-                q, c, b, first, blocks = unit
-                skill = skills[(q, c)][k][:, :, first * P : (first + blocks) * P]
-                if k == 0:
-                    total = sum_pool.tile([P, PACK, blocks * P], F32)
-                    sums[member] = total
-                    nc.vector.tensor_scalar(
-                        out=total[:], in0=skill, scalar1=weight_of(b, q, k), scalar2=None, op0=MULT
-                    )
-                elif k < NS - 1:
-                    total = sums[member]
-                    nc.vector.scalar_tensor_tensor(
-                        out=total[:], in0=skill, scalar=weight_of(b, q, k), in1=total[:],
-                        op0=MULT, op1=ADD,
-                    )
-                elif FINAL == "pairs":
-                    total = sums[member]
-                    paired = rounded_pool.tile([P, HALVES, blocks * P, 2], BF16)
-                    for u in range(HALVES):
-                        planes = slice(2 * u, 2 * u + 2)
-                        nc.vector.scalar_tensor_tensor(
-                            out=paired[:, u, :, :],
-                            in0=skill[:, planes, :].rearrange("p e d -> p d e"),
-                            scalar=weight_of(b, q, k),
-                            in1=total[:, planes, :].rearrange("p e d -> p d e"),
-                            op0=MULT, op1=ADD,
-                        )
-                    if member < SCALAR_REGROUPS:
-                        due("scalar", n + REGROUP, lambda unit=unit, paired=paired, n=n:
-                            regroup_pairs(nc.scalar.copy, unit, paired, n + REGROUP))
-                    else:
-                        for_vector(n + REGROUP, lambda step, unit=unit, paired=paired:
-                                   regroup_pairs(nc.vector.tensor_copy, unit, paired, step))
-                elif FINAL == "strided":
-                    total = sums[member]
-                    grouped = mx_pool.tile([P, GROUP * PACK], BF16, align_bytes=64)
-                    nc.vector.scalar_tensor_tensor(
-                        out=grouped[:].rearrange("p (d t) -> p d t", t=PACK),
-                        in0=skill.rearrange("p t d -> p d t"),
-                        scalar=weight_of(b, q, k),
-                        in1=total[:].rearrange("p t d -> p d t"),
-                        op0=MULT, op1=ADD,
-                    )
-                    for_vector(n + QUANT_S, lambda step, unit=unit, grouped=grouped:
-                               quantise_and_multiply(unit, 0, BLOCKS, grouped, step))
-                else:
-                    total = sums[member]
-                    rounded = rounded_pool.tile([P, PACK, GROUP], BF16)
-                    nc.vector.scalar_tensor_tensor(
-                        out=rounded[:], in0=skill, scalar=weight_of(b, q, k), in1=total[:],
-                        op0=MULT, op1=ADD,
-                    )
-                    if member < SCALAR_REGROUPS:
-                        due("scalar", n + REGROUP, lambda unit=unit, rounded=rounded, n=n:
-                            regroup(nc.scalar.copy, unit, rounded, n + REGROUP))
-                    else:
-                        for_vector(n + REGROUP, lambda step, unit=unit, rounded=rounded:
-                                   regroup(nc.vector.tensor_copy, unit, rounded, step))
-            if EXITS_FIRST:
-                for job in agenda["scalar"].get(n, []):
-                    job()
+            if n < steps and ops[n]:
+                straight_op(ops[n][0], ops[n][1], n)
+            for job in agenda["scalar"].get(n, []):
+                job()
             if n < EARLY or n % 8 in S_STEPS:
                 next_product("scalar", n)
             if n >= EARLY and n % 8 in V_STEPS:
                 next_product("vector", n)
-            if n == 1:
+            if n == 2:
                 make_mixers()
-            if not EXITS_FIRST:
-                for job in agenda["scalar"].get(n, []):
-                    job()
-            if ADDS_FIRST:
-                for job in agenda["tensor"].get(n, []):
-                    job(n)
+            for job in agenda["tensor"].get(n, []):
+                job(n)
             ready = [entry for entry in vector_queue if entry[0] <= n]
             for entry in ready[: 1 if len(ready) < BACKLOG else 2]:
                 vector_queue.remove(entry)
                 entry[1](n)
-            if not ADDS_FIRST:
-                for job in agenda["tensor"].get(n, []):
-                    job(n)
-            if SPLIT_LAST and n == LAST_STEPS[0]:
-                load_last()
-            for load_step, load in zip(load_steps, later_loads):
-                if load_step == n:
-                    load()
+            for load in loads.get(n, []):
+                load()
             n += 1

@@ -35,7 +35,7 @@ MATMULS_PER_BANK = 2 * BANK // FULL
 MATMUL_GROUPS = ((2, GROUP), (3, 0), (3, GROUP))
 FIRST_MATMUL_SPLIT = 2
 MATMUL_SPLITS = Q - FIRST_MATMUL_SPLIT
-LAST_MATMULS = 2 * MATMULS_PER_BANK
+LAST_MATMULS = 3 * MATMULS_PER_BANK
 assert (
     len(MATMUL_GROUPS) * BLOCKS * PAIRS * FULL + LAST_MATMULS * 2 * RUNS
 ) * P * P * 10 < B * S * R * OUT
@@ -43,6 +43,7 @@ assert (
 LATE = NS - 1
 TERM_BUFS = 13
 STORE_BUFS = 4
+GROUPED_BUFS = 4
 MX_BUFS = 3
 TURNED_BUFS = 2
 EXIT = 3
@@ -52,20 +53,23 @@ MERGE = 6
 TURN = 1
 ADD_GAP = 1
 ADD_DELAY = 2
+BY_SCALAR = (3,)
+LEAD = 3
+SUM_BUFS = 2
 BACKLOG = 3
 EARLY = 16
 S_STEPS = (0, 1, 3, 4, 6)
 V_STEPS = (7,)
 QUANT_S = 2
 H_STEPS = (10, 14, 18, 22)
-P_START = 22
+P_START = 20
 P_EVERY = 2
 M_START = 32
 M_EVERY = 10
-LAST_STEPS = (60, 80, 82, 84)
-STACK_STEPS = (26, 42)
+LAST_STEPS = (56, 76, 78, 82)
+STACK_STEPS = (24, 40)
 SECOND_STEP = 22
-THIRD_STEP = 38
+THIRD_STEP = 36
 TAIL_V = True
 HALF_BUFS = 11
 SECOND_EVERY = 2
@@ -79,15 +83,15 @@ def tile_skilledlora_pb_kernel(tc, h, weights, lora_b, out):
     nc = tc.nc
     with ExitStack() as ctx:
         consts = ctx.enter_context(tc.tile_pool(name="consts", bufs=1))
-        h_grouped_pool = ctx.enter_context(tc.tile_pool(name="h_grouped", bufs=1))
         half_pool = ctx.enter_context(tc.tile_pool(name="half_skills", bufs=HALF_BUFS))
         whole_pool = ctx.enter_context(tc.tile_pool(name="whole_skills", bufs=NS))
         stacked_pool = ctx.enter_context(tc.tile_pool(name="stacked", bufs=2))
         term_pool = ctx.enter_context(tc.tile_pool(name="terms", bufs=TERM_BUFS))
-        sum_pool = ctx.enter_context(tc.tile_pool(name="sums", bufs=2))
+        sum_pool = ctx.enter_context(tc.tile_pool(name="sums", bufs=SUM_BUFS))
         late_pool = ctx.enter_context(tc.tile_pool(name="late", bufs=2))
         turned_pool = ctx.enter_context(tc.tile_pool(name="turned", bufs=TURNED_BUFS))
         mixed_pool = ctx.enter_context(tc.tile_pool(name="mixed", bufs=2))
+        grouped_pool = ctx.enter_context(tc.tile_pool(name="grouped", bufs=GROUPED_BUFS))
         mx_pool = ctx.enter_context(tc.tile_pool(name="mx", bufs=MX_BUFS))
         store_pool = ctx.enter_context(tc.tile_pool(name="store", bufs=STORE_BUFS))
         psum = ctx.enter_context(tc.psum_pool(name="psum", bufs=8))
@@ -187,7 +191,7 @@ def tile_skilledlora_pb_kernel(tc, h, weights, lora_b, out):
         state = {"made": 0, "over": False, "turn": False}
 
         def turn_h(b, n):
-            h_grouped = h_grouped_pool.tile([P, S * PACK], BF16, align_bytes=64)
+            h_grouped = grouped_pool.tile([P, S * PACK], BF16, align_bytes=64, tag="grouped")
             grouped_words = h_grouped[:].bitcast(F32).rearrange("p (s u) -> p s u", u=HALVES)
             tiles_per_bank = BANK // (HALVES * P)
 
@@ -248,19 +252,35 @@ def tile_skilledlora_pb_kernel(tc, h, weights, lora_b, out):
 
             due("scalar", n + COPY_OUT, copy_out)
 
-        def mix_last(unit, u, n):
+        def mix_last(unit, j, u, n):
             q, b, column, width = unit
-            if u == 0:
-                last = turned_pool.tile([P, R], BF16)
+            if j == 0 and u == 0:
+                last = turned_pool.tile([P, BLOCKS, R], BF16)
                 state["last"] = last
             last = state["last"]
             bank = psum.tile([P, MATMULS_PER_BANK, 2 * RUNS], BF16, tag="bank")
-            mix(bank, stacked_of["last"], 0, u, mixers[:, q - FIRST_MATMUL_SPLIT, b, :])
+            mix(bank, stacked_of["last"], j, u, mixers[:, q - FIRST_MATMUL_SPLIT, b, :])
 
             def copy_out():
                 nc.scalar.copy(
-                    out=last[:].bitcast(F32).rearrange("p (u g a) -> p u g a", u=HALVES, g=RUNS)[:, u, :, :],
+                    out=last[:, j, :].bitcast(F32).rearrange("p (u g a) -> p u g a", u=HALVES, g=RUNS)[:, u, :, :],
                     in_=bank[:].bitcast(F32).rearrange("p a g -> p g a"),
+                )
+
+            due("scalar", n + COPY_OUT, copy_out)
+
+        def turn_quarter(n):
+            back = psum.tile([P, P], F32, tag="bank")
+            nc.tensor.transpose(
+                back[:], state["last"][:, 1, :].bitcast(F32)[:, :P], identity_f32[:]
+            )
+
+            def copy_out():
+                grouped = grouped_pool.tile([P, P * PACK], BF16, align_bytes=64, tag="grouped")
+                state["quarter"] = grouped
+                nc.scalar.copy(
+                    out=grouped[:].bitcast(F32).rearrange("p (d u) -> p d u", u=HALVES)[:, :, 0],
+                    in_=back[:],
                 )
 
             due("scalar", n + COPY_OUT, copy_out)
@@ -334,7 +354,7 @@ def tile_skilledlora_pb_kernel(tc, h, weights, lora_b, out):
                 for_vector(n + MERGE, merge)
 
         def turn_back(units, blocks, n):
-            grouped = mx_pool.tile([P, len(blocks) * P * PACK], BF16, align_bytes=64)
+            grouped = grouped_pool.tile([P, len(blocks) * P * PACK], BF16, align_bytes=64, tag="grouped")
             per_bank = min(len(blocks), BLOCKS)
             for first in range(0, len(blocks), per_bank):
                 width = per_bank * P
@@ -408,15 +428,22 @@ def tile_skilledlora_pb_kernel(tc, h, weights, lora_b, out):
                     due("scalar", n + EXIT, lambda unit=unit, result=result, bank=bank, first=first:
                         leave(unit, result, bank, first))
 
-        def straight_op(unit, k, n):
+        def straight_op(unit, k, n, by_scalar):
             q, b, column, width = unit
             skill = skill_of(unit, k)
+            planes = PACK
+            if unit == quarter_unit:
+                skill = skill[:, HALVES:PACK, :]
+                planes = PACK - HALVES
             if k == 0:
-                total = sum_pool.tile([P, PACK, width], F32)
+                total = sum_pool.tile([P, planes, width], F32)
                 sums[unit] = total
-                nc.vector.tensor_scalar(
-                    out=total[:], in0=skill, scalar1=weight_of(b, q, k), scalar2=None, op0=MULT
-                )
+                if by_scalar:
+                    nc.scalar.activation(out=total[:], in_=skill, func=COPY, scale=weight_of(b, q, k))
+                else:
+                    nc.vector.tensor_scalar(
+                        out=total[:], in0=skill, scalar1=weight_of(b, q, k), scalar2=None, op0=MULT
+                    )
                 return
             total = sums[unit]
             if k < NS - 1:
@@ -425,9 +452,12 @@ def tile_skilledlora_pb_kernel(tc, h, weights, lora_b, out):
                     op0=MULT, op1=ADD,
                 )
                 return
-            grouped = mx_pool.tile([P, width * PACK], BF16, align_bytes=64)
+            if unit == quarter_unit:
+                grouped = state["quarter"]
+            else:
+                grouped = grouped_pool.tile([P, width * PACK], BF16, align_bytes=64, tag="grouped")
             nc.vector.scalar_tensor_tensor(
-                out=grouped[:].rearrange("p (d t) -> p d t", t=PACK),
+                out=grouped[:].rearrange("p (d t) -> p d t", t=PACK)[:, :, PACK - planes : PACK],
                 in0=skill.rearrange("p t d -> p d t"),
                 scalar=weight_of(b, q, k),
                 in1=total[:].rearrange("p t d -> p d t"),
@@ -438,17 +468,18 @@ def tile_skilledlora_pb_kernel(tc, h, weights, lora_b, out):
         sums = {}
         turned_units = [(1, b, column, GROUP) for column in (0, GROUP) for b in range(B)]
         last_unit = (2, B - 1, 0, P)
+        quarter_unit = (2, B - 1, P, P)
         straight_pairs = [
             ((0, 0, 0, DO), (0, 1, 0, DO)),
             ((0, 2, 0, DO), (0, 3, 0, DO)),
             ((2, 0, 0, GROUP), (2, 1, 0, GROUP)),
-            ((2, 2, 0, GROUP), (2, 3, P, P)),
+            ((2, 2, 0, GROUP), quarter_unit),
         ]
         ops = []
-        for pair in straight_pairs:
+        for i, pair in enumerate(straight_pairs):
             for k in range(NS):
                 for unit in pair:
-                    ops.append((unit, k))
+                    ops.append((unit, k, i in BY_SCALAR))
                     if unit[3] > GROUP:
                         ops.append(None)
         steps = len(ops)
@@ -472,7 +503,7 @@ def tile_skilledlora_pb_kernel(tc, h, weights, lora_b, out):
         for i in range(2):
             loads.setdefault(STACK_STEPS[i], []).append(
                 lambda g=i + 1: load_stacked(g, *MATMUL_GROUPS[g], GROUP))
-        loads.setdefault(LAST_STEPS[0], []).append(lambda: load_stacked("last", 2, 0, P))
+        loads.setdefault(LAST_STEPS[0], []).append(lambda: load_stacked("last", 2, 0, GROUP))
 
         for b in range(B):
             due("tensor", H_STEPS[b], lambda n, b=b: turn_h(b, n))
@@ -484,9 +515,10 @@ def tile_skilledlora_pb_kernel(tc, h, weights, lora_b, out):
                 due("tensor", M_START + M_EVERY * (2 * g + i), lambda n, g=g, i=i: turn_back(
                     [MATMUL_GROUPS[g][:1] + (b,) + MATMUL_GROUPS[g][1:] + (GROUP,) for b in (2 * i, 2 * i + 1)],
                     [mixed_of[g][:, j, b, :] for b in (2 * i, 2 * i + 1) for j in range(BLOCKS)], n))
-        for u in range(HALVES):
-            due("tensor", LAST_STEPS[1 + u], lambda n, u=u: mix_last(last_unit, u, n))
-        due("tensor", LAST_STEPS[3] + COPY_OUT, lambda n: turn_back([last_unit], [state["last"][:]], n))
+        for i, (j, u) in enumerate(((0, 0), (0, 1), (1, 0))):
+            due("tensor", LAST_STEPS[1] + i, lambda n, j=j, u=u: mix_last(last_unit, j, u, n))
+        due("tensor", LAST_STEPS[3] + COPY_OUT, lambda n: turn_back([last_unit], [state["last"][:, 0, :]], n))
+        due("tensor", LAST_STEPS[3] + COPY_OUT + 1, turn_quarter)
 
         stream = [(unit, k) for unit in turned_units for k in range(NS - 1)]
 
@@ -515,8 +547,11 @@ def tile_skilledlora_pb_kernel(tc, h, weights, lora_b, out):
             step >= n for jobs in agenda.values() for step in jobs
         ):
             state["over"] = n >= steps + 2
-            if n < steps and ops[n]:
-                straight_op(ops[n][0], ops[n][1], n)
+            ahead = n + LEAD
+            if ahead < steps and ops[ahead] and ops[ahead][1] == 0 and ops[ahead][2]:
+                straight_op(ops[ahead][0], 0, ahead, True)
+            if n < steps and ops[n] and not (ops[n][1] == 0 and ops[n][2]):
+                straight_op(ops[n][0], ops[n][1], n, ops[n][2])
             for job in agenda["scalar"].get(n, []):
                 job()
             if n < EARLY or n % 8 in S_STEPS:

@@ -101,6 +101,9 @@ def tile_skilledlora_pb_kernel(tc, h, weights, lora_b, out):
         nc.scalar.dma_start(
             out=w_bf16[:], in_=weights.rearrange("b q k -> (b q k)").partition_broadcast(P)
         )
+        warm_up = consts.tile([P, 1], F32)
+        nc.vector.memset(warm_up[:], 0.0)
+        nc.scalar.activation(out=warm_up[:], in_=warm_up[:], func=COPY)
         w_f32 = consts.tile([P, B * Q * NS], F32)
         nc.vector.tensor_copy(out=w_f32[:], in_=w_bf16[:])
 

from contextlib import ExitStack

import concourse.mybir as mybir
from concourse.masks import make_identity

BF16 = mybir.dt.bfloat16
F32 = mybir.dt.float32
U32 = mybir.dt.uint32
U8 = mybir.dt.uint8
FP8X4 = mybir.dt.float8_e4m3fn_x4
MULT = mybir.AluOpType.mult
ADD = mybir.AluOpType.add
COPY = mybir.ActivationFunctionType.Copy
X = mybir.AxisListType.X

B, S, R, OUT, Q, NS = 4, 512, 512, 2048, 4, 8
DO = OUT // Q
SCALING = 2.0

P = 128
PACK = 4
HALVES = PACK // 2
assert R == P * PACK
TOKEN_TILES = S // P
BANK = 512

GROUP = 256
BLOCKS = GROUP // P

RUNS = 8
PAIRS = R // RUNS // 2
FULL = B * RUNS * 2
MATMULS_PER_BANK = 2 * BANK // FULL

MATMUL_GROUPS = ((2, GROUP), (3, 0), (3, GROUP))
FIRST_MATMUL_SPLIT = 2
MATMUL_SPLITS = Q - FIRST_MATMUL_SPLIT
LAST_MATMULS = 3 * MATMULS_PER_BANK
assert (
    len(MATMUL_GROUPS) * BLOCKS * PAIRS * FULL + LAST_MATMULS * 2 * RUNS
) * P * P * 10 < B * S * R * OUT

LATE = NS - 1
TERM_BUFS = 13
STORE_BUFS = 4
GROUPED_BUFS = 4
MX_BUFS = 3
TURNED_BUFS = 2
EXIT = 3
COPY_OUT = 1
QUANT = 5
MERGE = 6
TURN = 1
ADD_GAP = 1
ADD_DELAY = 2
BY_SCALAR = (3,)
LEAD = 3
SUM_BUFS = 2
BACKLOG = 3
EARLY = 16
S_STEPS = (0, 1, 3, 4, 6)
V_STEPS = (7,)
QUANT_S = 2
H_STEPS = (10, 14, 18, 22)
P_START = 20
P_EVERY = 2
M_START = 32
M_EVERY = 10
LAST_STEPS = (56, 76, 78, 82)
STACK_STEPS = (24, 40)
SECOND_STEP = 22
THIRD_STEP = 36
TAIL_V = True
HALF_BUFS = 11
SECOND_EVERY = 2
THIRD_EVERY = 4
HEAD = "WhhhhWhhhhWHWHWHWHWW"

FLOPS = 2 * B * S * R * OUT + 2 * B * Q * NS * R * DO


def tile_skilledlora_pb_kernel(tc, h, weights, lora_b, out):
    nc = tc.nc
    with ExitStack() as ctx:
        consts = ctx.enter_context(tc.tile_pool(name="consts", bufs=1))
        half_pool = ctx.enter_context(tc.tile_pool(name="half_skills", bufs=HALF_BUFS))
        whole_pool = ctx.enter_context(tc.tile_pool(name="whole_skills", bufs=NS))
        stacked_pool = ctx.enter_context(tc.tile_pool(name="stacked", bufs=2))
        term_pool = ctx.enter_context(tc.tile_pool(name="terms", bufs=TERM_BUFS))
        sum_pool = ctx.enter_context(tc.tile_pool(name="sums", bufs=SUM_BUFS))
        late_pool = ctx.enter_context(tc.tile_pool(name="late", bufs=2))
        turned_pool = ctx.enter_context(tc.tile_pool(name="turned", bufs=TURNED_BUFS))
        mixed_pool = ctx.enter_context(tc.tile_pool(name="mixed", bufs=2))
        grouped_pool = ctx.enter_context(tc.tile_pool(name="grouped", bufs=GROUPED_BUFS))
        mx_pool = ctx.enter_context(tc.tile_pool(name="mx", bufs=MX_BUFS))
        store_pool = ctx.enter_context(tc.tile_pool(name="store", bufs=STORE_BUFS))
        psum = ctx.enter_context(tc.psum_pool(name="psum", bufs=8))
        ctx.enter_context(tc.manual_schedule())

        w_bf16 = consts.tile([P, B * Q * NS], BF16)
        nc.scalar.dma_start(
            out=w_bf16[:], in_=weights.rearrange("b q k -> (b q k)").partition_broadcast(P)
        )
        warm_up = consts.tile([P, 1], F32)
        nc.vector.memset(warm_up[:], 0.0)
        nc.scalar.activation(out=warm_up[:], in_=warm_up[:], func=COPY)
        w_f32 = consts.tile([P, B * Q * NS], F32)
        nc.vector.tensor_copy(out=w_f32[:], in_=w_bf16[:])

        identity_f32 = consts.tile([P, P], F32)
        make_identity(nc, identity_f32[:])
        identity_bf16 = consts.tile([P, P], BF16)
        make_identity(nc, identity_bf16[:])

        mixers = consts.tile([P, MATMUL_SPLITS, B, RUNS * 2], BF16)

        def make_mixers():
            is_skill = consts.tile([P, NS], F32)
            nc.vector.tensor_reduce(
                out=is_skill[:], in_=identity_f32[:].rearrange("p (k g) -> p k g", k=NS), axis=X, op=ADD
            )
            is_rank = consts.tile([P, RUNS * 2], F32)
            nc.vector.tensor_reduce(
                out=is_rank[:], in_=identity_f32[:].rearrange("p (k g) -> p g k", k=NS), axis=X, op=ADD
            )
            masked = consts.tile([P, B, MATMUL_SPLITS, NS], F32)
            nc.vector.tensor_tensor(
                out=masked[:],
                in0=w_f32[:].rearrange("p (b q k) -> p b q k", b=B, q=Q)[:, :, FIRST_MATMUL_SPLIT:Q, :],
                in1=is_skill[:].unsqueeze(1).unsqueeze(1).to_broadcast([P, B, MATMUL_SPLITS, NS]),
                op=MULT,
            )
            own_weight = consts.tile([P, B, MATMUL_SPLITS], F32)
            nc.vector.tensor_reduce(out=own_weight[:], in_=masked[:], axis=X, op=ADD)
            shape = [P, MATMUL_SPLITS, B, RUNS * 2]
            nc.vector.tensor_tensor(
                out=mixers[:],
                in0=is_rank[:].unsqueeze(1).unsqueeze(1).to_broadcast(shape),
                in1=own_weight[:].rearrange("p b q -> p q b").unsqueeze(3).to_broadcast(shape),
                op=MULT,
            )

        h_codes = consts.tile([P, B, S], U32, align_bytes=64)
        h_scales = consts.tile([P, B, S], U8, align_bytes=64)

        def weight_of(b, q, k):
            column = (b * Q + q) * NS + k
            return w_f32[:, column : column + 1]

        parts = {}

        def skill_of(unit, k):
            q, b, column, width = unit
            view = parts[(q, column // GROUP)][k]
            inside = column % GROUP
            return view[:, :, inside : inside + width]

        def load_skill(pool, q, column, width, k):
            skill = pool.tile([P, PACK, width], BF16, tag="skill")
            nc.sync.dma_start(
                out=skill[:],
                in_=lora_b[q, k].rearrange("(p t) d -> p t d", t=PACK)[:, :, column : column + width],
            )
            for first in range(0, width, GROUP):
                parts.setdefault((q, (column + first) // GROUP), []).append(skill[:, :, first:width])

        stacked_of = {}

        def load_stacked(g, q, column, width):
            stacked = stacked_pool.tile([P, PAIRS, width], BF16)
            for e in range(2):
                nc.sync.dma_start(
                    out=stacked[e:P:2, :, :],
                    in_=lora_b[q].rearrange("k (g s e) d -> e (k g) s d", g=RUNS, e=2)[
                        e, :, :, column : column + width
                    ],
                )
            stacked_of[g] = stacked

        h_rows = stacked_pool.tile([P, B, TOKEN_TILES, R], BF16, tag="stacked")

        def load_h(b):
            nc.sync.dma_start(out=h_rows[:, b, :, :], in_=h[b].rearrange("(n p) r -> p n r", p=P))

        agenda = {"tensor": {}, "scalar": {}}
        vector_queue = []

        def due(engine, step, job):
            agenda[engine].setdefault(step, []).append(job)

        def for_vector(step, job):
            vector_queue.append([step, job])

        state = {"made": 0, "over": False, "turn": False}

        def turn_h(b, n):
            h_grouped = grouped_pool.tile([P, S * PACK], BF16, align_bytes=64, tag="grouped")
            grouped_words = h_grouped[:].bitcast(F32).rearrange("p (s u) -> p s u", u=HALVES)
            tiles_per_bank = BANK // (HALVES * P)

            def copy_out(turned_h, first):
                nc.scalar.copy(
                    out=grouped_words[:, first * P : (first + tiles_per_bank) * P, :].rearrange(
                        "p (n s) u -> p n s u", n=tiles_per_bank
                    ),
                    in_=turned_h[:].rearrange("p n u s -> p n s u"),
                )

            for first in range(0, TOKEN_TILES, tiles_per_bank):
                turned_h = psum.tile([P, tiles_per_bank, HALVES, P], F32, tag="bank")
                for m in range(tiles_per_bank):
                    words = h_rows[:, b, first + m, :].bitcast(F32).rearrange(
                        "p (w u) -> p u w", u=HALVES
                    )
                    for u in range(HALVES):
                        nc.tensor.transpose(turned_h[:, m, u, :], words[:, u, :], identity_f32[:])
                due("scalar", n + COPY_OUT, lambda turned_h=turned_h, first=first: copy_out(turned_h, first))

            def quantise_h(step):
                nc.vector.quantize_mx(
                    out=h_codes[:, b, :].bitcast(FP8X4), scales=h_scales[:, b, :], in_=h_grouped[:]
                )

            for_vector(n + COPY_OUT + 1, quantise_h)

        def mix(bank, stacked, j, u, moving):
            for a in range(MATMULS_PER_BANK):
                nc.tensor.matmul(
                    out=bank[:, a, :],
                    lhsT=stacked[:, HALVES * a + u, j * P : (j + 1) * P],
                    rhs=moving,
                    start=True,
                    stop=True,
                )

        mixed_of = {}

        def mix_piece(g, j, u, n):
            q = MATMUL_GROUPS[g][0]
            if g not in mixed_of:
                mixed = mixed_pool.tile([P, BLOCKS, B, R], BF16)
                mixed_of[g] = mixed
            mixed = mixed_of[g]
            bank = psum.tile([P, MATMULS_PER_BANK, FULL], BF16, tag="bank")
            mix(bank, stacked_of[g], j, u,
                mixers[:, q - FIRST_MATMUL_SPLIT, :, :].rearrange("p b g -> p (b g)"))

            def copy_out():
                nc.scalar.copy(
                    out=mixed[:, j, :, :].bitcast(F32).rearrange(
                        "p b (u g a) -> p b u g a", u=HALVES, g=RUNS
                    )[:, :, u, :, :],
                    in_=bank[:].bitcast(F32).rearrange("p a (b g) -> p b g a", b=B),
                )

            due("scalar", n + COPY_OUT, copy_out)

        def mix_last(unit, j, u, n):
            q, b, column, width = unit
            if j == 0 and u == 0:
                last = turned_pool.tile([P, BLOCKS, R], BF16)
                state["last"] = last
            last = state["last"]
            bank = psum.tile([P, MATMULS_PER_BANK, 2 * RUNS], BF16, tag="bank")
            mix(bank, stacked_of["last"], j, u, mixers[:, q - FIRST_MATMUL_SPLIT, b, :])

            def copy_out():
                nc.scalar.copy(
                    out=last[:, j, :].bitcast(F32).rearrange("p (u g a) -> p u g a", u=HALVES, g=RUNS)[:, u, :, :],
                    in_=bank[:].bitcast(F32).rearrange("p a g -> p g a"),
                )

            due("scalar", n + COPY_OUT, copy_out)

        def turn_quarter(n):
            back = psum.tile([P, P], F32, tag="bank")
            nc.tensor.transpose(
                back[:], state["last"][:, 1, :].bitcast(F32)[:, :P], identity_f32[:]
            )

            def copy_out():
                grouped = grouped_pool.tile([P, P * PACK], BF16, align_bytes=64, tag="grouped")
                state["quarter"] = grouped
                nc.scalar.copy(
                    out=grouped[:].bitcast(F32).rearrange("p (d u) -> p d u", u=HALVES)[:, :, 0],
                    in_=back[:],
                )

            due("scalar", n + COPY_OUT, copy_out)

        def product(engine, unit, k):
            q, b, column, width = unit
            term = term_pool.tile([P, PACK, GROUP], F32)
            if engine == "scalar":
                nc.scalar.activation(
                    out=term[:], in_=skill_of(unit, k), func=COPY, scale=weight_of(b, q, k)
                )
            else:
                nc.vector.tensor_scalar(
                    out=term[:], in0=skill_of(unit, k), scalar1=weight_of(b, q, k), scalar2=None,
                    op0=MULT,
                )
            return term

        late_of = {}

        def turn_late(unit, n):
            q, b, column, width = unit
            bank = psum.tile([P, BLOCKS, 2, HALVES, P], BF16, tag="bank")
            skill = skill_of(unit, LATE)
            for j in range(BLOCKS):
                for t in range(PACK):
                    nc.tensor.transpose(
                        bank[:, j, t % 2, t // 2, :], skill[:, t, j * P : (j + 1) * P], identity_bf16[:]
                    )
            late = late_pool.tile([P, BLOCKS, HALVES * P, 2], BF16)
            late_of[(q, column)] = late

            def copy_out():
                nc.scalar.copy(out=late[:], in_=bank[:].rearrange("d j e u p -> d j (u p) e"))

            due("scalar", n + COPY_OUT, copy_out)

        accs = {}

        def add_block(unit, terms, j, u, turned, n):
            q, b, column, width = unit
            if u == 0:
                acc = psum.tile([P, 2, HALVES, P], F32, tag="bank")
                accs[j] = acc
            acc = accs[j]
            for t in range(2 * u, 2 * u + 2):
                for i, term in enumerate(terms):
                    nc.tensor.matmul(
                        out=acc[:, t % 2, t // 2, :],
                        lhsT=term[:, t, j * P : (j + 1) * P],
                        rhs=identity_f32[:],
                        is_transpose=True,
                        start=(i == 0),
                        stop=(i == len(terms) - 1),
                    )

            def merge(step):
                nc.vector.scalar_tensor_tensor(
                    out=turned[:, j, :].rearrange("d (x e) -> d x e", e=2),
                    in0=late_of[(q, column)][:, j, :, :],
                    scalar=weight_of(b, q, LATE),
                    in1=acc[:].rearrange("d e u p -> d (u p) e"),
                    op0=MULT,
                    op1=ADD,
                )
                if j == BLOCKS - 1:
                    due("tensor", step + TURN, lambda m: turn_back(
                        [unit], [turned[:, i, :] for i in range(BLOCKS)], m))

            if u == HALVES - 1:
                for_vector(n + MERGE, merge)

        def turn_back(units, blocks, n):
            grouped = grouped_pool.tile([P, len(blocks) * P * PACK], BF16, align_bytes=64, tag="grouped")
            per_bank = min(len(blocks), BLOCKS)
            for first in range(0, len(blocks), per_bank):
                width = per_bank * P
                back = psum.tile([P, HALVES, width], F32, tag="bank")
                for j in range(per_bank):
                    words = blocks[first + j].bitcast(F32)
                    for u in range(HALVES):
                        nc.tensor.transpose(
                            back[:, u, j * P : (j + 1) * P], words[:, u * P : (u + 1) * P],
                            identity_f32[:],
                        )

                def copy_out(back, first, width):
                    nc.scalar.copy(
                        out=grouped[:, first * P * PACK : (first * P + width) * PACK]
                        .bitcast(F32).rearrange("p (d u) -> p d u", u=HALVES),
                        in_=back[:].rearrange("p u d -> p d u"),
                    )

                due("scalar", n + COPY_OUT, lambda back=back, first=first, width=width:
                    copy_out(back, first, width))
            for_vector(n + COPY_OUT + QUANT, lambda step: quantise_and_multiply(units, grouped, step))

        def quantise_and_multiply(units, grouped, n):
            width = units[0][3]
            codes = mx_pool.tile([P, len(units) * width], U32, align_bytes=64)
            scales = mx_pool.tile([P, len(units) * width], U8, align_bytes=64)
            nc.vector.quantize_mx(out=codes[:].bitcast(FP8X4), scales=scales[:], in_=grouped[:])
            tiles_per_bank = min(BANK // width, TOKEN_TILES)
            tiles_per_store = min(2 * BANK // width, TOKEN_TILES)

            def leave(unit, result, bank, first):
                q, b, column, width = unit
                inside = first % tiles_per_store
                target = result[:, inside : inside + tiles_per_bank, :]
                if TAIL_V and state["over"] and state["turn"]:
                    nc.vector.tensor_scalar(
                        out=target, in0=bank[:], scalar1=SCALING, scalar2=None, op0=MULT
                    )
                else:
                    nc.scalar.activation(out=target, in_=bank[:], func=COPY, scale=SCALING)
                state["turn"] = not state["turn"]
                done = first + tiles_per_bank
                if done % tiles_per_store == 0:
                    nc.sync.dma_start(
                        out=out[
                            b, (done - tiles_per_store) * P : done * P,
                            q * DO + column : q * DO + column + width,
                        ].rearrange("(n p) d -> p n d", p=P),
                        in_=result[:],
                    )

            for i, unit in enumerate(units):
                columns = slice(i * width, (i + 1) * width)
                b = unit[1]
                for first in range(0, TOKEN_TILES, tiles_per_bank):
                    if first % tiles_per_store == 0:
                        result = store_pool.tile([P, tiles_per_store, width], F32)
                    bank = psum.tile([P, tiles_per_bank, width], F32, tag="bank")
                    for m in range(tiles_per_bank):
                        tokens = slice((first + m) * P, (first + m + 1) * P)
                        nc.tensor.matmul_mx(
                            out=bank[:, m, :],
                            lhsT=h_codes[:, b, tokens].bitcast(FP8X4),
                            lhsT_scale=h_scales[:, b, tokens],
                            rhs=codes[:, columns].bitcast(FP8X4),
                            rhs_scale=scales[:, columns],
                            start=True,
                            stop=True,
                        )
                    due("scalar", n + EXIT, lambda unit=unit, result=result, bank=bank, first=first:
                        leave(unit, result, bank, first))

        def straight_op(unit, k, n, by_scalar):
            q, b, column, width = unit
            skill = skill_of(unit, k)
            planes = PACK
            if unit == quarter_unit:
                skill = skill[:, HALVES:PACK, :]
                planes = PACK - HALVES
            if k == 0:
                total = sum_pool.tile([P, planes, width], F32)
                sums[unit] = total
                if by_scalar:
                    nc.scalar.activation(out=total[:], in_=skill, func=COPY, scale=weight_of(b, q, k))
                else:
                    nc.vector.tensor_scalar(
                        out=total[:], in0=skill, scalar1=weight_of(b, q, k), scalar2=None, op0=MULT
                    )
                return
            total = sums[unit]
            if k < NS - 1:
                nc.vector.scalar_tensor_tensor(
                    out=total[:], in0=skill, scalar=weight_of(b, q, k), in1=total[:],
                    op0=MULT, op1=ADD,
                )
                return
            if unit == quarter_unit:
                grouped = state["quarter"]
            else:
                grouped = grouped_pool.tile([P, width * PACK], BF16, align_bytes=64, tag="grouped")
            nc.vector.scalar_tensor_tensor(
                out=grouped[:].rearrange("p (d t) -> p d t", t=PACK)[:, :, PACK - planes : PACK],
                in0=skill.rearrange("p t d -> p d t"),
                scalar=weight_of(b, q, k),
                in1=total[:].rearrange("p t d -> p d t"),
                op0=MULT, op1=ADD,
            )
            for_vector(n + QUANT_S, lambda step: quantise_and_multiply([unit], grouped, step))

        sums = {}
        turned_units = [(1, b, column, GROUP) for column in (0, GROUP) for b in range(B)]
        last_unit = (2, B - 1, 0, P)
        quarter_unit = (2, B - 1, P, P)
        straight_pairs = [
            ((0, 0, 0, DO), (0, 1, 0, DO)),
            ((0, 2, 0, DO), (0, 3, 0, DO)),
            ((2, 0, 0, GROUP), (2, 1, 0, GROUP)),
            ((2, 2, 0, GROUP), quarter_unit),
        ]
        ops = []
        for i, pair in enumerate(straight_pairs):
            for k in range(NS):
                for unit in pair:
                    ops.append((unit, k, i in BY_SCALAR))
                    if unit[3] > GROUP:
                        ops.append(None)
        steps = len(ops)

        head = {
            "W": [lambda k=k: load_skill(whole_pool, 0, 0, DO, k) for k in range(NS)],
            "h": [lambda k=k: load_skill(half_pool, 1, 0, GROUP, k) for k in range(NS)],
            "H": [lambda b=b: load_h(b) for b in range(B)],
        }
        position = {"W": 0, "h": 0, "H": 0}
        for kind in HEAD:
            head[kind][position[kind]]()
            position[kind] += 1
        load_stacked(0, *MATMUL_GROUPS[0], GROUP)
        loads = {}
        for i in range(NS):
            loads.setdefault(SECOND_STEP + SECOND_EVERY * i, []).append(
                lambda k=i: load_skill(half_pool, 1, GROUP, GROUP, k))
            loads.setdefault(THIRD_STEP + THIRD_EVERY * i, []).append(
                lambda k=i: load_skill(whole_pool, 2, 0, GROUP, k))
        for i in range(2):
            loads.setdefault(STACK_STEPS[i], []).append(
                lambda g=i + 1: load_stacked(g, *MATMUL_GROUPS[g], GROUP))
        loads.setdefault(LAST_STEPS[0], []).append(lambda: load_stacked("last", 2, 0, GROUP))

        for b in range(B):
            due("tensor", H_STEPS[b], lambda n, b=b: turn_h(b, n))
        for g in range(len(MATMUL_GROUPS)):
            for i in range(PACK):
                step = P_START + P_EVERY * i if g == 0 else M_START + 2 * M_EVERY * (g - 1) + 1 + M_EVERY * i // 2
                due("tensor", step, lambda n, g=g, i=i: mix_piece(g, i // 2, i % 2, n))
            for i in range(B // 2):
                due("tensor", M_START + M_EVERY * (2 * g + i), lambda n, g=g, i=i: turn_back(
                    [MATMUL_GROUPS[g][:1] + (b,) + MATMUL_GROUPS[g][1:] + (GROUP,) for b in (2 * i, 2 * i + 1)],
                    [mixed_of[g][:, j, b, :] for b in (2 * i, 2 * i + 1) for j in range(BLOCKS)], n))
        for i, (j, u) in enumerate(((0, 0), (0, 1), (1, 0))):
            due("tensor", LAST_STEPS[1] + i, lambda n, j=j, u=u: mix_last(last_unit, j, u, n))
        due("tensor", LAST_STEPS[3] + COPY_OUT, lambda n: turn_back([last_unit], [state["last"][:, 0, :]], n))
        due("tensor", LAST_STEPS[3] + COPY_OUT + 1, turn_quarter)

        stream = [(unit, k) for unit in turned_units for k in range(NS - 1)]

        def next_product(engine, n):
            if state["made"] == len(stream):
                return
            unit, k = stream[state["made"]]
            state["made"] += 1
            if k == 0:
                state["terms"] = []
            state["terms"].append(product(engine, unit, k))
            if k == NS - 2:
                if (unit[0], unit[2]) not in late_of:
                    due("tensor", n + 1, lambda m: turn_late(unit, m))
                due_adds(unit, state["terms"], n + ADD_DELAY)

        def due_adds(unit, terms, n):
            turned = turned_pool.tile([P, BLOCKS, R], BF16)
            for j in range(BLOCKS):
                for u in range(HALVES):
                    due("tensor", n + ADD_GAP * (HALVES * j + u), lambda m, j=j, u=u:
                        add_block(unit, terms, j, u, turned, m))

        n = 0
        while n < steps or vector_queue or any(
            step >= n for jobs in agenda.values() for step in jobs
        ):
            state["over"] = n >= steps + 2
            ahead = n + LEAD
            if ahead < steps and ops[ahead] and ops[ahead][1] == 0 and ops[ahead][2]:
                straight_op(ops[ahead][0], 0, ahead, True)
            if n < steps and ops[n] and not (ops[n][1] == 0 and ops[n][2]):
                straight_op(ops[n][0], ops[n][1], n, ops[n][2])
            for job in agenda["scalar"].get(n, []):
                job()
            if n < EARLY or n % 8 in S_STEPS:
                next_product("scalar", n)
            if n >= EARLY and n % 8 in V_STEPS:
                next_product("vector", n)
            if n == 2:
                make_mixers()
            for job in agenda["tensor"].get(n, []):
                job(n)
            ready = [entry for entry in vector_queue if entry[0] <= n]
            for entry in ready[: 1 if len(ready) < BACKLOG else 2]:
                vector_queue.remove(entry)
                entry[1](n)
            for load in loads.get(n, []):
                load()
            n += 1
